import numpy as np
import ml_dtypes


def mxq(x, axis, fmt="e4m3"):
    dtype, down = {"e4m3": (ml_dtypes.float8_e4m3fn, 7), "e5m2": (ml_dtypes.float8_e5m2, 14)}[fmt]
    v = np.moveaxis(np.asarray(x, np.float32).astype(ml_dtypes.bfloat16).astype(np.float64), axis, -1)
    blocks = v.reshape(v.shape[:-1] + (-1, 32))
    amax = np.abs(blocks).max(-1, keepdims=True)
    byte = np.maximum(np.where(amax > 0, np.frexp(amax)[1] - 1 + 127, 0) - down, 1)
    scale = np.exp2(byte - 127.0)
    codes = (blocks / scale).astype(np.float32).astype(dtype).astype(np.float64)
    return np.moveaxis((codes * scale).reshape(v.shape), -1, axis)


WIDE = False


def mx_kscale(k):
    if not WIDE:
        return np.ones(k)
    levels = np.array([10, -10, 5, -5, 0])
    a = np.random.permutation(np.resize(levels, k // 512 * 4)).reshape(k // 512, 4)
    idx = np.arange(k)
    return np.exp2(a[idx // 512, idx % 128 // 32])


BF16 = ml_dtypes.bfloat16


def bf(x):
    return np.asarray(x, np.float32).astype(BF16)


def f64(x):
    return np.asarray(x).astype(np.float64)


A, B, D, E, H, C = 4, 128, 512, 512, 32, 16
NUM_ITERS = 3


def squash(t):
    sq = np.sum(t * t, axis=-1, keepdims=True)
    return (sq / (1.0 + sq)) * t / np.sqrt(sq)


def softmax(v, axis):
    e = np.exp(v - v.max(axis=axis, keepdims=True))
    return e / e.sum(axis=axis, keepdims=True)


def route(priors, n_iters):
    logits = np.zeros(priors.shape[:-1] + (1,))
    outputs = None
    for i in range(n_iters):
        probs = softmax(logits, 2)
        outputs = squash(np.sum(probs * priors, axis=2, keepdims=True))
        if i != n_iters - 1:
            logits = logits + np.sum(priors * outputs, axis=-1, keepdims=True)
    return outputs


def setup_inputs():
    s = mx_kscale(D)
    return {"x": bf(np.random.standard_normal((A, B, D)) * s),
            "route_weights1": bf(np.random.standard_normal((H, D, E)) * (B / E) ** 0.25 / np.sqrt(D) / s[:, None]),
            "route_weights": bf(np.random.standard_normal((C, E, E)) * (H / E) ** 0.25)}


def reference(x, route_weights1, route_weights):
    priors1 = (mxq(f64(x), 2, "e4m3").reshape(A * B, D) @ mxq(f64(route_weights1), 1, "e4m3")).reshape(H, A, B, E)
    out1 = route(priors1, NUM_ITERS)
    out1 = np.transpose(out1[:, :, 0, :], (1, 0, 2))
    priors = (mxq(out1, 2, "e4m3").reshape(A * H, E) @ mxq(f64(route_weights), 1, "e4m3")).reshape(C, A, H, E)
    out = route(priors, NUM_ITERS)
    return out[:, :, 0, :]

@@ -1,0 +1,241 @@
+from contextlib import ExitStack
+
+import concourse.mybir as mybir
+from concourse.masks import make_identity
+
+FP8X4 = mybir.dt.float8_e4m3fn_x4
+BF16 = mybir.dt.bfloat16
+F32 = mybir.dt.float32
+U32 = mybir.dt.uint32
+U8 = mybir.dt.uint8
+ALU = mybir.AluOpType
+ACT = mybir.ActivationFunctionType
+AX = mybir.AxisListType
+
+P = 128
+NA, NB, ND, NE, NH, NC2 = 4, 128, 512, 512, 32, 16
+HG = 4
+FLOPS = 2 * (NA * NB * ND * NE * NH + NA * NH * NE * NE * NC2)
+
+
+def tile_capsulelayer_kernel(tc, x, route_weights1, route_weights, out):
+    nc = tc.nc
+    with ExitStack() as ctx:
+        const = ctx.enter_context(tc.tile_pool(name="const", bufs=1))
+        stage = ctx.enter_context(tc.tile_pool(name="stage", bufs=2))
+        split = ctx.enter_context(tc.tile_pool(name="split", bufs=2 * HG))
+        small = ctx.enter_context(tc.tile_pool(name="small", bufs=2))
+        psum = ctx.enter_context(tc.psum_pool(name="psum", bufs=1))
+
+        ident_f = const.tile([P, P], F32, name="ident_f")
+        make_identity(nc, ident_f[:])
+        ident_b = const.tile([P, P], BF16, name="ident_b")
+        make_identity(nc, ident_b[:])
+        ones_f = const.tile([P, 2], F32, name="ones_f")
+        nc.vector.memset(ones_f[:], 1.0)
+        half = const.tile([P, 1], F32, name="half")
+        nc.vector.memset(half[:], 0.5)
+        ev_one = const.tile([P, P], F32, name="ev_one")
+        nc.vector.memset(ev_one[:], 1.0)
+        z_one = const.tile([P, 1], F32, name="z_one")
+        nc.vector.memset(z_one[:], float(NB))
+        lt_zero = const.tile([P, P], F32, name="lt_zero")
+        nc.vector.memset(lt_zero[:], 0.0)
+        ev_blk = const.tile([P, P], F32, name="ev_blk")
+        nc.vector.memset(ev_blk[:], 0.0)
+        lt_blk = const.tile([P, P], F32, name="lt_blk")
+        nc.vector.memset(lt_blk[:], -1.0e30)
+        for a in range(NA):
+            blk = slice(32 * a, 32 * a + 32)
+            nc.vector.memset(ev_blk[blk, blk], 1.0)
+            nc.vector.memset(lt_blk[blk, blk], 0.0)
+        z_blk = const.tile([P, 1], F32, name="z_blk")
+        nc.vector.memset(z_blk[:], float(NH))
+        ucols = []
+        sqcs = []
+        for i in range(2):
+            ucol = const.tile([P, P], F32, name="ucol%d" % i)
+            nc.vector.memset(ucol[:], 0.0)
+            ucols.append(ucol)
+            sqc = const.tile([P, P], F32, name="sqc%d" % i)
+            nc.vector.memset(sqc[:], 0.0)
+            sqcs.append(sqc)
+
+        xc = const.tile([P, NA * NB], U32, name="xc", align_bytes=64)
+        xs = const.tile([P, NA * NB], U8, name="xs", align_bytes=64)
+        w2c = const.tile([P, NC2, NE], U32, name="w2c", align_bytes=64)
+        w2s = const.tile([P, NC2, NE], U8, name="w2s", align_bytes=64)
+        og = const.tile([P, NA * NH, 4], BF16, name="og", align_bytes=64)
+        oc = const.tile([P, NA * NH], U32, name="oc", align_bytes=64)
+        os_ = const.tile([P, NA * NH], U8, name="os_", align_bytes=64)
+
+        def quantise_weights(rows, codes, scales):
+            raw = stage.tile([P, 4, NE], BF16, name="raw", tag="raw", bufs=3)
+            nc.sync.dma_start(out=raw[:], in_=rows)
+            grouped = stage.tile([P, NE, 4], BF16, name="grouped", tag="grouped", align_bytes=64)
+            nc.vector.tensor_copy(
+                out=grouped[:].rearrange("p (c i) t -> p c t i", i=4),
+                in_=raw[:].rearrange("p t (c i) -> p c t i", i=4),
+            )
+            nc.vector.quantize_mx(out=codes.bitcast(FP8X4), scales=scales, in_=grouped[:].rearrange("p w t -> p (w t)"))
+
+        def evacuate(bank, dst, on_scalar):
+            if on_scalar:
+                nc.scalar.copy(out=dst, in_=bank)
+            else:
+                nc.vector.tensor_copy(out=dst, in_=bank)
+
+        def mx(out_ps, l_codes, l_scales, r_codes, r_scales):
+            nc.tensor.matmul_mx(out=out_ps, lhsT=l_codes.bitcast(FP8X4), lhsT_scale=l_scales,
+                                rhs=r_codes.bitcast(FP8X4), rhs_scale=r_scales, start=True, stop=True)
+
+        def routing(n_tiles, n_prob, stat, stat_t, ev, z, lt, which, finish):
+            ucol, sqc = ucols[which], sqcs[which]
+            cols = P if n_prob > 1 else n_tiles
+            for rnd in range(3):
+                s_ps = psum.tile([P, n_tiles * 4, n_prob], F32, name="s_ps", tag="s")
+                evv = ev[:].rearrange("p (n c) -> p n c", c=32)
+                for t in range(n_tiles):
+                    for fc in range(4):
+                        nc.tensor.matmul(s_ps[:, t * 4 + fc, :], lhsT=stat(t, fc), rhs=evv[:, 0:n_prob, t], start=True, stop=True)
+                scol = small.tile([P, n_tiles * 4, n_prob], F32, name="scol", tag="scol")
+                nc.vector.tensor_copy(out=scol[:], in_=s_ps[:])
+                sq = small.tile([P, n_tiles * 4, n_prob], F32, name="sq", tag="sq")
+                nc.scalar.activation(out=sq[:], in_=scol[:], func=ACT.Square)
+                nc.vector.tensor_reduce(
+                    out=sqc[:].rearrange("p (n c) -> p c n", c=32)[:, 0:n_tiles, 0:n_prob],
+                    in_=sq[:].rearrange("p (t f) n -> p t n f", f=4), axis=AX.X, op=ALU.add)
+                n_ps = psum.tile([P, 2], F32, name="n_ps", tag="s")
+                nc.tensor.matmul(n_ps[:], lhsT=sqc[:], rhs=ones_f[:], start=True, stop=True)
+                n_sb = small.tile([P, 1], F32, name="n_sb", tag="n_sb")
+                nc.vector.tensor_copy(out=n_sb[:], in_=n_ps[:, 0:1])
+                den = small.tile([P, 1], F32, name="den", tag="den")
+                nc.vector.tensor_scalar(out=den[:], in0=z[:], scalar1=z[:, 0:1], scalar2=n_sb[:, 0:1], op0=ALU.mult, op1=ALU.add)
+                rden = small.tile([P, 1], F32, name="rden", tag="rden")
+                nc.vector.reciprocal(out=rden[:], in_=den[:])
+                rt = small.tile([P, 1], F32, name="rt", tag="rt")
+                nc.gpsimd.tensor_tensor(out=rt[:], in0=n_sb[:], in1=half[:], op=ALU.pow)
+                f = small.tile([P, 1], F32, name="f", tag="f")
+                nc.vector.tensor_tensor(out=f[:], in0=rt[:], in1=rden[:], op=ALU.mult)
+                if rnd == 2:
+                    fb_ps = psum.tile([P, P], F32, name="fb_ps", tag="t", bufs=2)
+                    nc.tensor.transpose(fb_ps[:], f[:, 0:1].to_broadcast([P, P]), ident_f[:])
+                    finish(scol, fb_ps)
+                    break
+                u_ps = psum.tile([P, n_tiles, n_prob], F32, name="u_ps", tag="u")
+                for t in range(n_tiles):
+                    for fc in range(4):
+                        nc.tensor.matmul(u_ps[:, t, :], lhsT=stat_t(t, fc), rhs=scol[:, t * 4 + fc, :], start=(fc == 0), stop=(fc == 3))
+                nc.vector.tensor_copy(out=ucol[:].rearrange("p (n c) -> p c n", c=32)[:, 0:n_tiles, 0:n_prob], in_=u_ps[:])
+                ut_ps = psum.tile([P, P], F32, name="ut_ps", tag="t", bufs=2)
+                nc.tensor.transpose(ut_ps[:], ucol[:], ident_f[:])
+                lt_new = small.tile([P, P], F32, name="lt_new", tag="lt")
+                nc.vector.scalar_tensor_tensor(out=lt_new[:], in0=ut_ps[:], scalar=f[:, 0:1], in1=lt[:], op0=ALU.mult, op1=ALU.add)
+                lt = lt_new
+                negmax = small.tile([P, 1], F32, name="negmax", tag="negmax")
+                nc.vector.tensor_reduce(out=negmax[:], in_=lt[:], axis=AX.X, op=ALU.max, negate=True)
+                e_sb = small.tile([P, P], F32, name="e_sb", tag="e_sb")
+                z = small.tile([P, 1], F32, name="z", tag="z")
+                nc.scalar.activation(out=e_sb[:], in_=lt[:], func=ACT.Exp, bias=negmax[:, 0:1], scale=1.0, accum_out=z[:])
+                et_ps = psum.tile([P, P], F32, name="et_ps", tag="t", bufs=2)
+                nc.tensor.transpose(et_ps[:], e_sb[:], ident_f[:])
+                ev = small.tile([P, P], F32, name="ev", tag="ev")
+                nc.scalar.copy(out=ev[:, 0:cols], in_=et_ps[:, 0:cols])
+
+        x_sb = stage.tile([P, NA, ND], BF16, name="x_sb", tag="raw", bufs=3)
+        nc.sync.dma_start(out=x_sb[:], in_=x.rearrange("a b d -> b a d"))
+        xg = stage.tile([P, NA * NB, 4], BF16, name="xg", tag="grouped", align_bytes=64)
+        for a in range(NA):
+            xt_ps = psum.tile([P, 4, NB], BF16, name="xt_ps", tag="t", bufs=2)
+            for t in range(4):
+                nc.tensor.transpose(xt_ps[:, t, :], x_sb[:, a, :].rearrange("b (p t) -> b t p", t=4)[:, t, :], ident_b[:])
+            nc.vector.tensor_copy(out=xg[:, a * NB:(a + 1) * NB, :], in_=xt_ps[:].rearrange("p t b -> p b t"))
+        nc.vector.quantize_mx(out=xc[:].bitcast(FP8X4), scales=xs[:], in_=xg[:].rearrange("p w t -> p (w t)"))
+
+        tiles1 = {}
+
+        def produce1(h):
+            wc = stage.tile([P, NE], U32, name="wc", tag="wc", align_bytes=64)
+            ws = stage.tile([P, NE], U8, name="ws", tag="ws", align_bytes=64)
+            quantise_weights(route_weights1[h].rearrange("(p t) e -> p t e", t=4), wc[:], ws[:])
+            pf = split.tile([P, NA, NE], F32, name="pf", tag="pf")
+            ptf = split.tile([P, 4, NA * NB], F32, name="ptf", tag="ptf")
+            for a in range(NA):
+                cs = slice(a * NB, (a + 1) * NB)
+                p_ps = psum.tile([P, NE], F32, name="p_ps", tag="big", bufs=4)
+                mx(p_ps[:], xc[:, cs], xs[:, cs], wc[:], ws[:])
+                evacuate(p_ps[:], pf[:, a, :], True)
+            for c in range(4):
+                cs = slice(c * P, (c + 1) * P)
+                pt_ps = psum.tile([P, NA * NB], F32, name="pt_ps", tag="big", bufs=4)
+                mx(pt_ps[:], wc[:, cs], ws[:, cs], xc[:], xs[:])
+                evacuate(pt_ps[:], ptf[:, c, :], False)
+            tiles1[h] = (pf, ptf)
+
+        def chain1(g):
+            def stat(t, fc):
+                return tiles1[g * HG + t // NA][0][:, t % NA, fc * P:(fc + 1) * P]
+
+            def stat_t(t, fc):
+                return tiles1[g * HG + t // NA][1][:, fc, (t % NA) * NB:(t % NA + 1) * NB]
+
+            def finish(scol, fb_ps):
+                nc.vector.tensor_tensor(
+                    out=og[:].rearrange("p (a h) c -> p h a c", a=NA)[:, g * HG:(g + 1) * HG],
+                    in0=scol[:].rearrange("p (l a f) n -> p l a (f n)", l=HG, a=NA),
+                    in1=fb_ps[:, 0:HG * NA].rearrange("p (l a) -> p l a", a=NA).unsqueeze(3).to_broadcast([P, HG, NA, 4]),
+                    op=ALU.mult)
+
+            routing(HG * NA, 1, stat, stat_t, ev_one, z_one, lt_zero, g % 2, finish)
+
+        n_groups = NH // HG
+        for h in range(HG):
+            produce1(h)
+        for g in range(n_groups):
+            chain1(g)
+            if g + 1 < n_groups:
+                for h in range((g + 1) * HG, (g + 2) * HG):
+                    produce1(h)
+            for c in range(2 * g, 2 * g + 2):
+                quantise_weights(route_weights[c].rearrange("(t p) f -> p t f", p=P), w2c[:, c, :], w2s[:, c, :])
+
+        nc.vector.quantize_mx(out=oc[:].bitcast(FP8X4), scales=os_[:], in_=og[:].rearrange("p w t -> p (w t)"))
+        tiles2 = {}
+        for q in range(NC2 // 4):
+            qf = split.tile([P, 4, NE], F32, name="qf", tag="pf")
+            qtf = split.tile([P, 4, NE], F32, name="qtf", tag="ptf")
+            tiles2[q] = (qf, qtf)
+            for i in range(4):
+                c = 4 * q + i
+                q_ps = psum.tile([P, NE], F32, name="q_ps", tag="big", bufs=4)
+                mx(q_ps[:], oc[:], os_[:], w2c[:, c, :], w2s[:, c, :])
+                evacuate(q_ps[:], qf[:, i, :], True)
+                qt_ps = psum.tile([P, 4, P], F32, name="qt_ps", tag="big", bufs=4)
+                for fc in range(4):
+                    cs = slice(fc * P, (fc + 1) * P)
+                    mx(qt_ps[:, fc, :], w2c[:, c, cs], w2s[:, c, cs], oc[:], os_[:])
+                evacuate(qt_ps[:].rearrange("p k j -> p (k j)"), qtf[:, i, :], False)
+
+        def stat2(t, fc):
+            return tiles2[t // 4][0][:, t % 4, fc * P:(fc + 1) * P]
+
+        def stat2_t(t, fc):
+            return tiles2[t // 4][1][:, t % 4, fc * P:(fc + 1) * P]
+
+        def finish2(scol, fb_ps):
+            o_sb = small.tile([P, NC2, NA, 4], F32, name="o_sb", tag="o_sb", bufs=1)
+            nc.vector.tensor_tensor(
+                out=o_sb[:],
+                in0=scol[:].rearrange("p (t f) n -> p t n f", f=4),
+                in1=fb_ps[:].rearrange("p (n c) -> p c n", c=32)[:, 0:NC2, :].unsqueeze(3).to_broadcast([P, NC2, NA, 4]),
+                op=ALU.mult)
+            o_flat = o_sb[:].rearrange("p t n f -> p (t n f)")
+            out_rows = out.rearrange("c a (k f) -> (c a k) f", f=P)
+            for i in range(2):
+                ot_ps = psum.tile([P, P], F32, name="ot_ps", tag="t", bufs=2)
+                nc.tensor.transpose(ot_ps[:], o_flat[:, i * P:(i + 1) * P], ident_f[:])
+                res = small.tile([P, P], F32, name="res", tag="res")
+                nc.scalar.copy(out=res[:], in_=ot_ps[:])
+                nc.sync.dma_start(out=out_rows[i * P:(i + 1) * P, :], in_=res[:])
+
+        routing(NC2, NA, stat2, stat2_t, ev_blk, z_blk, lt_blk, 0, finish2)

@@ -15,6 +15,8 @@ AX = mybir.AxisListType
 P = 128
 NA, NB, ND, NE, NH, NC2 = 4, 128, 512, 512, 32, 16
 HG = 4
+SPLIT_BUFS = 6
+LO_ON_POOL = ()
 FLOPS = 2 * (NA * NB * ND * NE * NH + NA * NH * NE * NE * NC2)
 
 
@@ -23,7 +25,7 @@ def tile_capsulelayer_kernel(tc, x, route_weights1, route_weights, out):
     with ExitStack() as ctx:
         const = ctx.enter_context(tc.tile_pool(name="const", bufs=1))
         stage = ctx.enter_context(tc.tile_pool(name="stage", bufs=2))
-        split = ctx.enter_context(tc.tile_pool(name="split", bufs=2 * HG))
+        split = ctx.enter_context(tc.tile_pool(name="split", bufs=SPLIT_BUFS))
         small = ctx.enter_context(tc.tile_pool(name="small", bufs=2))
         psum = ctx.enter_context(tc.psum_pool(name="psum", bufs=1))
 
@@ -35,19 +37,20 @@ def tile_capsulelayer_kernel(tc, x, route_weights1, route_weights, out):
         nc.vector.memset(ones_f[:], 1.0)
         half = const.tile([P, 1], F32, name="half")
         nc.vector.memset(half[:], 0.5)
-        ev_one = const.tile([P, P], F32, name="ev_one")
-        nc.vector.memset(ev_one[:], 1.0)
+        ev_one = const.tile([P, 3, P], BF16, name="ev_one")
+        nc.vector.memset(ev_one[:], 0.0)
+        nc.vector.memset(ev_one[:, 0, :], 1.0)
         z_one = const.tile([P, 1], F32, name="z_one")
         nc.vector.memset(z_one[:], float(NB))
         lt_zero = const.tile([P, P], F32, name="lt_zero")
         nc.vector.memset(lt_zero[:], 0.0)
-        ev_blk = const.tile([P, P], F32, name="ev_blk")
+        ev_blk = const.tile([P, 3, P], BF16, name="ev_blk")
         nc.vector.memset(ev_blk[:], 0.0)
         lt_blk = const.tile([P, P], F32, name="lt_blk")
         nc.vector.memset(lt_blk[:], -1.0e30)
         for a in range(NA):
             blk = slice(32 * a, 32 * a + 32)
-            nc.vector.memset(ev_blk[blk, blk], 1.0)
+            nc.vector.memset(ev_blk[blk, 0, blk], 1.0)
             nc.vector.memset(lt_blk[blk, blk], 0.0)
         z_blk = const.tile([P, 1], F32, name="z_blk")
         nc.vector.memset(z_blk[:], float(NH))
@@ -70,20 +73,34 @@ def tile_capsulelayer_kernel(tc, x, route_weights1, route_weights, out):
         os_ = const.tile([P, NA * NH], U8, name="os_", align_bytes=64)
 
         def quantise_weights(rows, codes, scales):
-            raw = stage.tile([P, 4, NE], BF16, name="raw", tag="raw", bufs=3)
+            raw = stage.tile([P, 4, NE], BF16, name="raw", tag="raw", bufs=2)
             nc.sync.dma_start(out=raw[:], in_=rows)
             grouped = stage.tile([P, NE, 4], BF16, name="grouped", tag="grouped", align_bytes=64)
-            nc.vector.tensor_copy(
+            nc.gpsimd.tensor_scalar(
                 out=grouped[:].rearrange("p (c i) t -> p c t i", i=4),
-                in_=raw[:].rearrange("p t (c i) -> p c t i", i=4),
+                in0=raw[:].rearrange("p t (c i) -> p c t i", i=4),
+                scalar1=1.0, scalar2=0.0, op0=ALU.mult, op1=ALU.add,
             )
             nc.vector.quantize_mx(out=codes.bitcast(FP8X4), scales=scales, in_=grouped[:].rearrange("p w t -> p (w t)"))
 
-        def evacuate(bank, dst, on_scalar):
-            if on_scalar:
-                nc.scalar.copy(out=dst, in_=bank)
-            else:
-                nc.vector.tensor_copy(out=dst, in_=bank)
+        banks = [0]
+
+        def split_bank(bank, terms):
+            hi, mid, lo = terms
+            nc.scalar.copy(out=hi, in_=bank)
+            rest = small.tile([P, NE], F32, name="rest", tag="rest", bufs=2)
+            nc.vector.tensor_tensor(out=rest[:], in0=bank, in1=hi, op=ALU.subtract)
+            nc.scalar.copy(out=mid, in_=rest[:])
+            eng = nc.gpsimd if banks[0] % 8 in LO_ON_POOL else nc.vector
+            eng.tensor_tensor(out=lo, in0=rest[:], in1=mid, op=ALU.subtract)
+            banks[0] += 1
+
+        def split_small(src, dst, width):
+            nc.vector.tensor_copy(out=dst[:, 0, 0:width], in_=src)
+            rest = small.tile([P, 256], F32, name="rest_s", tag="rest_s")
+            nc.vector.tensor_tensor(out=rest[:, 0:width], in0=src, in1=dst[:, 0, 0:width], op=ALU.subtract)
+            nc.vector.tensor_copy(out=dst[:, 1, 0:width], in_=rest[:, 0:width])
+            nc.vector.tensor_tensor(out=dst[:, 2, 0:width], in0=rest[:, 0:width], in1=dst[:, 1, 0:width], op=ALU.subtract)
 
         def mx(out_ps, l_codes, l_scales, r_codes, r_scales):
             nc.tensor.matmul_mx(out=out_ps, lhsT=l_codes.bitcast(FP8X4), lhsT_scale=l_scales,
@@ -93,19 +110,27 @@ def tile_capsulelayer_kernel(tc, x, route_weights1, route_weights, out):
             ucol, sqc = ucols[which], sqcs[which]
             cols = P if n_prob > 1 else n_tiles
             for rnd in range(3):
-                s_ps = psum.tile([P, n_tiles * 4, n_prob], F32, name="s_ps", tag="s")
-                evv = ev[:].rearrange("p (n c) -> p n c", c=32)
-                for t in range(n_tiles):
-                    for fc in range(4):
-                        nc.tensor.matmul(s_ps[:, t * 4 + fc, :], lhsT=stat(t, fc), rhs=evv[:, 0:n_prob, t], start=True, stop=True)
                 scol = small.tile([P, n_tiles * 4, n_prob], F32, name="scol", tag="scol")
-                nc.vector.tensor_copy(out=scol[:], in_=s_ps[:])
+                evv = ev[:].rearrange("p s (n c) -> p s n c", c=32)
+                per = n_tiles if n_prob == 1 else n_tiles // 2
+                for t0 in range(0, n_tiles, per):
+                    s_ps = psum.tile([P, per, 4, 3, n_prob], F32, name="s_ps", tag="s", bufs=2)
+                    for t in range(t0, t0 + per):
+                        rhs = evv[:, :, 0:n_prob, t]
+                        for fc in range(4):
+                            for part in range(3):
+                                nc.tensor.matmul(s_ps[:, t - t0, fc, 0:3 - part], lhsT=stat(t, fc, part), rhs=rhs[:, 0:3 - part], start=(part == 0), stop=(part == 2))
+                    nc.vector.tensor_reduce(out=scol[:, t0 * 4:(t0 + per) * 4, :], in_=s_ps[:].rearrange("p t f s n -> p (t f) n s"), axis=AX.X, op=ALU.add)
+                scol_flat = scol[:].rearrange("p a n -> p (a n)")
+                if rnd < 2:
+                    sv = small.tile([P, 3, n_tiles * 4 * n_prob], BF16, name="sv", tag="sv")
+                    split_small(scol_flat, sv, n_tiles * 4 * n_prob)
                 sq = small.tile([P, n_tiles * 4, n_prob], F32, name="sq", tag="sq")
                 nc.scalar.activation(out=sq[:], in_=scol[:], func=ACT.Square)
                 nc.vector.tensor_reduce(
                     out=sqc[:].rearrange("p (n c) -> p c n", c=32)[:, 0:n_tiles, 0:n_prob],
                     in_=sq[:].rearrange("p (t f) n -> p t n f", f=4), axis=AX.X, op=ALU.add)
-                n_ps = psum.tile([P, 2], F32, name="n_ps", tag="s")
+                n_ps = psum.tile([P, 2], F32, name="n_ps", tag="s", bufs=2)
                 nc.tensor.matmul(n_ps[:], lhsT=sqc[:], rhs=ones_f[:], start=True, stop=True)
                 n_sb = small.tile([P, 1], F32, name="n_sb", tag="n_sb")
                 nc.vector.tensor_copy(out=n_sb[:], in_=n_ps[:, 0:1])
@@ -122,11 +147,16 @@ def tile_capsulelayer_kernel(tc, x, route_weights1, route_weights, out):
                     nc.tensor.transpose(fb_ps[:], f[:, 0:1].to_broadcast([P, P]), ident_f[:])
                     finish(scol, fb_ps)
                     break
-                u_ps = psum.tile([P, n_tiles, n_prob], F32, name="u_ps", tag="u")
+                u_ps = psum.tile([P, n_tiles, 3, n_prob], F32, name="u_ps", tag="u")
+                svv = sv[:].rearrange("p s (t f n) -> p s t f n", t=n_tiles, f=4)
                 for t in range(n_tiles):
                     for fc in range(4):
-                        nc.tensor.matmul(u_ps[:, t, :], lhsT=stat_t(t, fc), rhs=scol[:, t * 4 + fc, :], start=(fc == 0), stop=(fc == 3))
-                nc.vector.tensor_copy(out=ucol[:].rearrange("p (n c) -> p c n", c=32)[:, 0:n_tiles, 0:n_prob], in_=u_ps[:])
+                        rhs = svv[:, :, t, fc, :]
+                        for part in range(3):
+                            nc.tensor.matmul(u_ps[:, t, 0:3 - part], lhsT=stat_t(t, fc, part), rhs=rhs[:, 0:3 - part], start=(fc == 0 and part == 0), stop=(fc == 3 and part == 2))
+                nc.vector.tensor_reduce(
+                    out=ucol[:].rearrange("p (n c) -> p c n", c=32)[:, 0:n_tiles, 0:n_prob],
+                    in_=u_ps[:].rearrange("p t s n -> p t n s"), axis=AX.X, op=ALU.add)
                 ut_ps = psum.tile([P, P], F32, name="ut_ps", tag="t", bufs=2)
                 nc.tensor.transpose(ut_ps[:], ucol[:], ident_f[:])
                 lt_new = small.tile([P, P], F32, name="lt_new", tag="lt")
@@ -139,10 +169,10 @@ def tile_capsulelayer_kernel(tc, x, route_weights1, route_weights, out):
                 nc.scalar.activation(out=e_sb[:], in_=lt[:], func=ACT.Exp, bias=negmax[:, 0:1], scale=1.0, accum_out=z[:])
                 et_ps = psum.tile([P, P], F32, name="et_ps", tag="t", bufs=2)
                 nc.tensor.transpose(et_ps[:], e_sb[:], ident_f[:])
-                ev = small.tile([P, P], F32, name="ev", tag="ev")
-                nc.scalar.copy(out=ev[:, 0:cols], in_=et_ps[:, 0:cols])
+                ev = small.tile([P, 3, P], BF16, name="ev", tag="ev")
+                split_small(et_ps[:, 0:cols], ev, cols)
 
-        x_sb = stage.tile([P, NA, ND], BF16, name="x_sb", tag="raw", bufs=3)
+        x_sb = stage.tile([P, NA, ND], BF16, name="x_sb", tag="raw", bufs=2)
         nc.sync.dma_start(out=x_sb[:], in_=x.rearrange("a b d -> b a d"))
         xg = stage.tile([P, NA * NB, 4], BF16, name="xg", tag="grouped", align_bytes=64)
         for a in range(NA):
@@ -158,26 +188,26 @@ def tile_capsulelayer_kernel(tc, x, route_weights1, route_weights, out):
             wc = stage.tile([P, NE], U32, name="wc", tag="wc", align_bytes=64)
             ws = stage.tile([P, NE], U8, name="ws", tag="ws", align_bytes=64)
             quantise_weights(route_weights1[h].rearrange("(p t) e -> p t e", t=4), wc[:], ws[:])
-            pf = split.tile([P, NA, NE], F32, name="pf", tag="pf")
-            ptf = split.tile([P, 4, NA * NB], F32, name="ptf", tag="ptf")
+            pn = [split.tile([P, NA, NE], BF16, name="pn%d" % i, tag="pn%d" % i) for i in range(3)]
+            pt = [split.tile([P, 4, NA * NB], BF16, name="pt%d" % i, tag="pt%d" % i) for i in range(3)]
             for a in range(NA):
                 cs = slice(a * NB, (a + 1) * NB)
-                p_ps = psum.tile([P, NE], F32, name="p_ps", tag="big", bufs=4)
+                p_ps = psum.tile([P, NE], F32, name="p_ps", tag="big", bufs=3)
                 mx(p_ps[:], xc[:, cs], xs[:, cs], wc[:], ws[:])
-                evacuate(p_ps[:], pf[:, a, :], True)
+                split_bank(p_ps[:], [w[:, a, :] for w in pn])
             for c in range(4):
                 cs = slice(c * P, (c + 1) * P)
-                pt_ps = psum.tile([P, NA * NB], F32, name="pt_ps", tag="big", bufs=4)
+                pt_ps = psum.tile([P, NA * NB], F32, name="pt_ps", tag="big", bufs=3)
                 mx(pt_ps[:], wc[:, cs], ws[:, cs], xc[:], xs[:])
-                evacuate(pt_ps[:], ptf[:, c, :], False)
-            tiles1[h] = (pf, ptf)
+                split_bank(pt_ps[:], [w[:, c, :] for w in pt])
+            tiles1[h] = (pn, pt)
 
         def chain1(g):
-            def stat(t, fc):
-                return tiles1[g * HG + t // NA][0][:, t % NA, fc * P:(fc + 1) * P]
+            def stat(t, fc, part):
+                return tiles1[g * HG + t // NA][0][part][:, t % NA, fc * P:(fc + 1) * P]
 
-            def stat_t(t, fc):
-                return tiles1[g * HG + t // NA][1][:, fc, (t % NA) * NB:(t % NA + 1) * NB]
+            def stat_t(t, fc, part):
+                return tiles1[g * HG + t // NA][1][part][:, fc, (t % NA) * NB:(t % NA + 1) * NB]
 
             def finish(scol, fb_ps):
                 nc.vector.tensor_tensor(
@@ -202,25 +232,25 @@ def tile_capsulelayer_kernel(tc, x, route_weights1, route_weights, out):
         nc.vector.quantize_mx(out=oc[:].bitcast(FP8X4), scales=os_[:], in_=og[:].rearrange("p w t -> p (w t)"))
         tiles2 = {}
         for q in range(NC2 // 4):
-            qf = split.tile([P, 4, NE], F32, name="qf", tag="pf")
-            qtf = split.tile([P, 4, NE], F32, name="qtf", tag="ptf")
-            tiles2[q] = (qf, qtf)
+            qn = [split.tile([P, 4, NE], BF16, name="qn%d" % i, tag="pn%d" % i) for i in range(3)]
+            qt = [split.tile([P, 4, NE], BF16, name="qt%d" % i, tag="pt%d" % i) for i in range(3)]
+            tiles2[q] = (qn, qt)
             for i in range(4):
                 c = 4 * q + i
-                q_ps = psum.tile([P, NE], F32, name="q_ps", tag="big", bufs=4)
+                q_ps = psum.tile([P, NE], F32, name="q_ps", tag="big", bufs=3)
                 mx(q_ps[:], oc[:], os_[:], w2c[:, c, :], w2s[:, c, :])
-                evacuate(q_ps[:], qf[:, i, :], True)
-                qt_ps = psum.tile([P, 4, P], F32, name="qt_ps", tag="big", bufs=4)
+                split_bank(q_ps[:], [w[:, i, :] for w in qn])
+                qt_ps = psum.tile([P, 4, P], F32, name="qt_ps", tag="big", bufs=3)
                 for fc in range(4):
                     cs = slice(fc * P, (fc + 1) * P)
                     mx(qt_ps[:, fc, :], w2c[:, c, cs], w2s[:, c, cs], oc[:], os_[:])
-                evacuate(qt_ps[:].rearrange("p k j -> p (k j)"), qtf[:, i, :], False)
+                split_bank(qt_ps[:].rearrange("p k j -> p (k j)"), [w[:, i, :] for w in qt])
 
-        def stat2(t, fc):
-            return tiles2[t // 4][0][:, t % 4, fc * P:(fc + 1) * P]
+        def stat2(t, fc, part):
+            return tiles2[t // 4][0][part][:, t % 4, fc * P:(fc + 1) * P]
 
-        def stat2_t(t, fc):
-            return tiles2[t // 4][1][:, t % 4, fc * P:(fc + 1) * P]
+        def stat2_t(t, fc, part):
+            return tiles2[t // 4][1][part][:, t % 4, fc * P:(fc + 1) * P]
 
         def finish2(scol, fb_ps):
             o_sb = small.tile([P, NC2, NA, 4], F32, name="o_sb", tag="o_sb", bufs=1)

@@ -15,8 +15,11 @@ AX = mybir.AxisListType
 P = 128
 NA, NB, ND, NE, NH, NC2 = 4, 128, 512, 512, 32, 16
 HG = 4
-SPLIT_BUFS = 6
+NT = HG * NA
+HELD = 14
 LO_ON_POOL = ()
+ON_VECTOR = ()
+SCALERS = "GVGVGVGVGVGVGVGV"
 FLOPS = 2 * (NA * NB * ND * NE * NH + NA * NH * NE * NE * NC2)
 
 
@@ -25,7 +28,8 @@ def tile_capsulelayer_kernel(tc, x, route_weights1, route_weights, out):
     with ExitStack() as ctx:
         const = ctx.enter_context(tc.tile_pool(name="const", bufs=1))
         stage = ctx.enter_context(tc.tile_pool(name="stage", bufs=2))
-        split = ctx.enter_context(tc.tile_pool(name="split", bufs=SPLIT_BUFS))
+        split = ctx.enter_context(tc.tile_pool(name="split", bufs=HELD))
+        carry = ctx.enter_context(tc.tile_pool(name="carry", bufs=4))
         small = ctx.enter_context(tc.tile_pool(name="small", bufs=2))
         psum = ctx.enter_context(tc.psum_pool(name="psum", bufs=1))
 
@@ -56,7 +60,7 @@ def tile_capsulelayer_kernel(tc, x, route_weights1, route_weights, out):
         nc.vector.memset(z_blk[:], float(NH))
         ucols = []
         sqcs = []
-        for i in range(2):
+        for i in range(3):
             ucol = const.tile([P, P], F32, name="ucol%d" % i)
             nc.vector.memset(ucol[:], 0.0)
             ucols.append(ucol)
@@ -114,7 +118,7 @@ def tile_capsulelayer_kernel(tc, x, route_weights1, route_weights, out):
                 evv = ev[:].rearrange("p s (n c) -> p s n c", c=32)
                 per = n_tiles if n_prob == 1 else n_tiles // 2
                 for t0 in range(0, n_tiles, per):
-                    s_ps = psum.tile([P, per, 4, 3, n_prob], F32, name="s_ps", tag="s", bufs=2)
+                    s_ps = psum.tile([P, per, 4, 3, n_prob], F32, name="s_ps", tag="pb", bufs=3)
                     for t in range(t0, t0 + per):
                         rhs = evv[:, :, 0:n_prob, t]
                         for fc in range(4):
@@ -130,17 +134,17 @@ def tile_capsulelayer_kernel(tc, x, route_weights1, route_weights, out):
                 nc.vector.tensor_reduce(
                     out=sqc[:].rearrange("p (n c) -> p c n", c=32)[:, 0:n_tiles, 0:n_prob],
                     in_=sq[:].rearrange("p (t f) n -> p t n f", f=4), axis=AX.X, op=ALU.add)
-                n_ps = psum.tile([P, 2], F32, name="n_ps", tag="s", bufs=2)
+                n_ps = psum.tile([P, 2], F32, name="n_ps", tag="u")
                 nc.tensor.matmul(n_ps[:], lhsT=sqc[:], rhs=ones_f[:], start=True, stop=True)
-                n_sb = small.tile([P, 1], F32, name="n_sb", tag="n_sb")
+                n_sb = small.tile([P, 1], F32, name="n_sb", tag="n_sb", bufs=6)
                 nc.vector.tensor_copy(out=n_sb[:], in_=n_ps[:, 0:1])
-                den = small.tile([P, 1], F32, name="den", tag="den")
+                den = small.tile([P, 1], F32, name="den", tag="den", bufs=6)
                 nc.vector.tensor_scalar(out=den[:], in0=z[:], scalar1=z[:, 0:1], scalar2=n_sb[:, 0:1], op0=ALU.mult, op1=ALU.add)
-                rden = small.tile([P, 1], F32, name="rden", tag="rden")
+                rden = small.tile([P, 1], F32, name="rden", tag="rden", bufs=6)
                 nc.vector.reciprocal(out=rden[:], in_=den[:])
-                rt = small.tile([P, 1], F32, name="rt", tag="rt")
+                rt = small.tile([P, 1], F32, name="rt", tag="rt", bufs=6)
                 nc.gpsimd.tensor_tensor(out=rt[:], in0=n_sb[:], in1=half[:], op=ALU.pow)
-                f = small.tile([P, 1], F32, name="f", tag="f")
+                f = small.tile([P, 1], F32, name="f", tag="f", bufs=6)
                 nc.vector.tensor_tensor(out=f[:], in0=rt[:], in1=rden[:], op=ALU.mult)
                 if rnd == 2:
                     fb_ps = psum.tile([P, P], F32, name="fb_ps", tag="t", bufs=2)
@@ -162,9 +166,9 @@ def tile_capsulelayer_kernel(tc, x, route_weights1, route_weights, out):
                 lt_new = small.tile([P, P], F32, name="lt_new", tag="lt")
                 nc.vector.scalar_tensor_tensor(out=lt_new[:], in0=ut_ps[:], scalar=f[:, 0:1], in1=lt[:], op0=ALU.mult, op1=ALU.add)
                 lt = lt_new
-                negmax = small.tile([P, 1], F32, name="negmax", tag="negmax")
+                negmax = small.tile([P, 1], F32, name="negmax", tag="negmax", bufs=6)
                 nc.vector.tensor_reduce(out=negmax[:], in_=lt[:], axis=AX.X, op=ALU.max, negate=True)
-                e_sb = small.tile([P, P], F32, name="e_sb", tag="e_sb")
+                e_sb = small.tile([P, P], F32, name="e_sb", tag="e_sb", bufs=3)
                 z = small.tile([P, 1], F32, name="z", tag="z")
                 nc.scalar.activation(out=e_sb[:], in_=lt[:], func=ACT.Exp, bias=negmax[:, 0:1], scale=1.0, accum_out=z[:])
                 et_ps = psum.tile([P, P], F32, name="et_ps", tag="t", bufs=2)
@@ -183,74 +187,174 @@ def tile_capsulelayer_kernel(tc, x, route_weights1, route_weights, out):
         nc.vector.quantize_mx(out=xc[:].bitcast(FP8X4), scales=xs[:], in_=xg[:].rearrange("p w t -> p (w t)"))
 
         tiles1 = {}
+        sums1 = {}
+        state1 = {}
+        turn = [0]
 
-        def produce1(h):
-            wc = stage.tile([P, NE], U32, name="wc", tag="wc", align_bytes=64)
-            ws = stage.tile([P, NE], U8, name="ws", tag="ws", align_bytes=64)
-            quantise_weights(route_weights1[h].rearrange("(p t) e -> p t e", t=4), wc[:], ws[:])
-            pn = [split.tile([P, NA, NE], BF16, name="pn%d" % i, tag="pn%d" % i) for i in range(3)]
-            pt = [split.tile([P, 4, NA * NB], BF16, name="pt%d" % i, tag="pt%d" % i) for i in range(3)]
-            for a in range(NA):
-                cs = slice(a * NB, (a + 1) * NB)
-                p_ps = psum.tile([P, NE], F32, name="p_ps", tag="big", bufs=3)
-                mx(p_ps[:], xc[:, cs], xs[:, cs], wc[:], ws[:])
-                split_bank(p_ps[:], [w[:, a, :] for w in pn])
-            for c in range(4):
-                cs = slice(c * P, (c + 1) * P)
-                pt_ps = psum.tile([P, NA * NB], F32, name="pt_ps", tag="big", bufs=3)
-                mx(pt_ps[:], wc[:, cs], ws[:, cs], xc[:], xs[:])
-                split_bank(pt_ps[:], [w[:, c, :] for w in pt])
-            tiles1[h] = (pn, pt)
+        def new_sums():
+            scol = carry.tile([P, NT * 4], F32, name="scol1", tag="scol1", bufs=6)
+            return scol
 
-        def chain1(g):
-            def stat(t, fc, part):
-                return tiles1[g * HG + t // NA][0][part][:, t % NA, fc * P:(fc + 1) * P]
+        def produce1(g):
+            scol = new_sums()
+            sums1[g] = scol
+            for l in range(HG):
+                h = g * HG + l
+                wc = stage.tile([P, NE], U32, name="wc", tag="wc", align_bytes=64)
+                ws = stage.tile([P, NE], U8, name="ws", tag="ws", align_bytes=64)
+                quantise_weights(route_weights1[h].rearrange("(p t) e -> p t e", t=4), wc[:], ws[:])
+                ptf = split.tile([P, 4, NA * NB], F32, name="ptf", tag="ptf")
+                tiles1[h] = ptf
+                for c in range(4):
+                    cs = slice(c * P, (c + 1) * P)
+                    pt_ps = psum.tile([P, NA * NB], F32, name="pt_ps", tag="big", bufs=2)
+                    mx(pt_ps[:], wc[:, cs], ws[:, cs], xc[:], xs[:])
+                    for a in range(NA):
+                        bs = slice(a * NB, (a + 1) * NB)
+                        col = (l * NA + a) * 4 + c
+                        nc.scalar.activation(out=ptf[:, c, bs], in_=pt_ps[:, bs], func=ACT.Copy, accum_out=scol[:, col:col + 1])
 
-            def stat_t(t, fc, part):
-                return tiles1[g * HG + t // NA][1][part][:, fc, (t % NA) * NB:(t % NA + 1) * NB]
+        def squash_factor(scol, z):
+            sqc = sqcs[turn[0] % 3]
+            sq = small.tile([P, NT, 4], F32, name="sq1", tag="sq1", bufs=3)
+            nc.scalar.activation(out=sq[:].rearrange("p t f -> p (t f)"), in_=scol[:, 0:NT * 4], func=ACT.Square)
+            nc.vector.tensor_reduce(out=sqc[:, 0:NT], in_=sq[:], axis=AX.X, op=ALU.add)
+            n_ps = psum.tile([P, 2], F32, name="n_ps1", tag="u")
+            nc.tensor.matmul(n_ps[:], lhsT=sqc[:], rhs=ones_f[:], start=True, stop=True)
+            n_sb = small.tile([P, 1], F32, name="n_sb", tag="n_sb", bufs=6)
+            nc.vector.tensor_copy(out=n_sb[:], in_=n_ps[:, 0:1])
+            den = small.tile([P, 1], F32, name="den", tag="den", bufs=6)
+            nc.vector.tensor_scalar(out=den[:], in0=z[:], scalar1=z[:, 0:1], scalar2=n_sb[:, 0:1], op0=ALU.mult, op1=ALU.add)
+            rden = small.tile([P, 1], F32, name="rden", tag="rden", bufs=6)
+            nc.vector.reciprocal(out=rden[:], in_=den[:])
+            rt = small.tile([P, 1], F32, name="rt", tag="rt", bufs=6)
+            nc.gpsimd.tensor_tensor(out=rt[:], in0=n_sb[:], in1=half[:], op=ALU.pow)
+            f = small.tile([P, 1], F32, name="f", tag="f", bufs=6)
+            nc.vector.tensor_tensor(out=f[:], in0=rt[:], in1=rden[:], op=ALU.mult)
+            return f
 
-            def finish(scol, fb_ps):
-                nc.vector.tensor_tensor(
-                    out=og[:].rearrange("p (a h) c -> p h a c", a=NA)[:, g * HG:(g + 1) * HG],
-                    in0=scol[:].rearrange("p (l a f) n -> p l a (f n)", l=HG, a=NA),
-                    in1=fb_ps[:, 0:HG * NA].rearrange("p (l a) -> p l a", a=NA).unsqueeze(3).to_broadcast([P, HG, NA, 4]),
-                    op=ALU.mult)
+        def agree_and_softmax(g, scol, f, lt):
+            ucol = ucols[turn[0] % 3]
+            for l in range(HG):
+                ptf = tiles1[g * HG + l]
+                fold_ps = psum.tile([P, NA, P], F32, name="fold_ps", tag="pb", bufs=3)
+                for a in range(NA):
+                    t = l * NA + a
+                    bs = slice(a * NB, (a + 1) * NB)
+                    scaled = small.tile([P, 4, NB], F32, name="scaled", tag="scaled", bufs=4)
+                    for c in range(4):
+                        sc = scol[:, t * 4 + c:t * 4 + c + 1]
+                        if SCALERS[t] == "G":
+                            nc.gpsimd.tensor_scalar(out=scaled[:, c, :], in0=ptf[:, c, bs], scalar1=sc, scalar2=0.0, op0=ALU.mult, op1=ALU.add)
+                        elif SCALERS[t] == "V":
+                            nc.vector.tensor_scalar(out=scaled[:, c, :], in0=ptf[:, c, bs], scalar1=sc, scalar2=None, op0=ALU.mult)
+                        else:
+                            nc.scalar.activation(out=scaled[:, c, :], in_=ptf[:, c, bs], func=ACT.Copy, scale=sc)
+                    for c in range(4):
+                        nc.tensor.matmul(fold_ps[:, a, :], lhsT=scaled[:, c, :], rhs=ident_f[:], is_transpose=True, start=(c == 0), stop=(c == 3))
+                nc.vector.tensor_reduce(out=ucol[:, l * NA:(l + 1) * NA], in_=fold_ps[:], axis=AX.X, op=ALU.add)
+            ut_ps = psum.tile([P, P], F32, name="ut_ps", tag="t", bufs=2)
+            nc.tensor.transpose(ut_ps[:], ucol[:], ident_f[:])
+            lt_new = carry.tile([P, P], F32, name="lt1", tag="lt1")
+            nc.vector.scalar_tensor_tensor(out=lt_new[:], in0=ut_ps[:], scalar=f[:, 0:1], in1=lt[:], op0=ALU.mult, op1=ALU.add)
+            negmax = small.tile([P, 1], F32, name="negmax", tag="negmax", bufs=6)
+            nc.vector.tensor_reduce(out=negmax[:], in_=lt_new[:], axis=AX.X, op=ALU.max, negate=True)
+            e_sb = small.tile([P, P], F32, name="e_sb", tag="e_sb", bufs=3)
+            z = carry.tile([P, 1], F32, name="z1", tag="z1")
+            nc.scalar.activation(out=e_sb[:], in_=lt_new[:], func=ACT.Exp, bias=negmax[:, 0:1], scale=1.0, accum_out=z[:])
+            et_ps = psum.tile([P, P], F32, name="et_ps", tag="t", bufs=2)
+            nc.tensor.transpose(et_ps[:], e_sb[:], ident_f[:])
+            et = carry.tile([P, NT], F32, name="et1", tag="et1")
+            nc.vector.tensor_copy(out=et[:], in_=et_ps[:, 0:NT])
+            return lt_new, z, et
 
-            routing(HG * NA, 1, stat, stat_t, ev_one, z_one, lt_zero, g % 2, finish)
+        def weighted_sums(g, et):
+            scol = new_sums()
+            for l in range(HG):
+                ptf = tiles1[g * HG + l]
+                pb_ps = psum.tile([P, NA, NB], F32, name="pb_ps", tag="pb", bufs=3)
+                for a in range(NA):
+                    t = l * NA + a
+                    nc.tensor.transpose(pb_ps[:, a, :], et[:, t:t + 1].to_broadcast([P, P]), ident_f[:])
+                for c in range(4):
+                    if l in ON_VECTOR:
+                        for a in range(NA):
+                            col = (l * NA + a) * 4 + c
+                            waste_v = small.tile([P, NB], F32, name="waste_v", tag="waste_v")
+                            nc.vector.scalar_tensor_tensor(
+                                out=waste_v[:], in0=pb_ps[:, a, :], scalar=1.0, in1=ptf[:, c, a * NB:(a + 1) * NB],
+                                op0=ALU.mult, op1=ALU.mult, accum_out=scol[:, col:col + 1])
+                    else:
+                        prod = small.tile([P, NA * NB], F32, name="prod", tag="prod", bufs=3)
+                        nc.vector.tensor_tensor(out=prod[:], in0=pb_ps[:].rearrange("p a b -> p (a b)"), in1=ptf[:, c, :], op=ALU.mult)
+                        for a in range(NA):
+                            col = (l * NA + a) * 4 + c
+                            waste_s = small.tile([P, NB], BF16, name="waste_s", tag="waste_s")
+                            nc.scalar.activation(out=waste_s[:], in_=prod[:, a * NB:(a + 1) * NB], func=ACT.Copy, accum_out=scol[:, col:col + 1])
+            return scol
+
+        def round1(g):
+            turn[0] += 1
+            f = squash_factor(sums1[g], z_one)
+            state1[g] = agree_and_softmax(g, sums1[g], f, lt_zero)
+
+        def round2(g):
+            turn[0] += 1
+            lt, z, et = state1[g]
+            scol = weighted_sums(g, et)
+            f = squash_factor(scol, z)
+            state1[g] = agree_and_softmax(g, scol, f, lt)
+
+        def round3(g):
+            turn[0] += 1
+            lt, z, et = state1[g]
+            scol = weighted_sums(g, et)
+            f = squash_factor(scol, z)
+            fb_ps = psum.tile([P, P], F32, name="fb_ps1", tag="t", bufs=2)
+            nc.tensor.transpose(fb_ps[:], f[:, 0:1].to_broadcast([P, P]), ident_f[:])
+            nc.vector.tensor_tensor(
+                out=og[:].rearrange("p (a h) c -> p h a c", a=NA)[:, g * HG:(g + 1) * HG],
+                in0=scol[:, 0:NT * 4].rearrange("p (l a f) -> p l a f", l=HG, a=NA),
+                in1=fb_ps[:, 0:NT].rearrange("p (l a) -> p l a", a=NA).unsqueeze(3).to_broadcast([P, HG, NA, 4]),
+                op=ALU.mult)
 
         n_groups = NH // HG
-        for h in range(HG):
-            produce1(h)
-        for g in range(n_groups):
-            chain1(g)
-            if g + 1 < n_groups:
-                for h in range((g + 1) * HG, (g + 2) * HG):
-                    produce1(h)
-            for c in range(2 * g, 2 * g + 2):
-                quantise_weights(route_weights[c].rearrange("(t p) f -> p t f", p=P), w2c[:, c, :], w2s[:, c, :])
+        produce1(0)
+        for k in range(n_groups + 2):
+            if 0 <= k - 2 < n_groups:
+                round3(k - 2)
+            if 0 <= k - 1 < n_groups:
+                round2(k - 1)
+            if k < n_groups:
+                round1(k)
+            if k + 1 < n_groups:
+                produce1(k + 1)
+            if k < n_groups:
+                for c in range(2 * k, 2 * k + 2):
+                    quantise_weights(route_weights[c].rearrange("(t p) f -> p t f", p=P), w2c[:, c, :], w2s[:, c, :])
 
         nc.vector.quantize_mx(out=oc[:].bitcast(FP8X4), scales=os_[:], in_=og[:].rearrange("p w t -> p (w t)"))
         tiles2 = {}
-        for q in range(NC2 // 4):
-            qn = [split.tile([P, 4, NE], BF16, name="qn%d" % i, tag="pn%d" % i) for i in range(3)]
-            qt = [split.tile([P, 4, NE], BF16, name="qt%d" % i, tag="pt%d" % i) for i in range(3)]
+        for q in range(NC2 // 8):
+            qn = [split.tile([P, 8, NE], BF16, name="qn%d" % i, tag="ptf") for i in range(3)]
+            qt = [split.tile([P, 8, NE], BF16, name="qt%d" % i, tag="ptf") for i in range(3)]
             tiles2[q] = (qn, qt)
-            for i in range(4):
-                c = 4 * q + i
-                q_ps = psum.tile([P, NE], F32, name="q_ps", tag="big", bufs=3)
+            for i in range(8):
+                c = 8 * q + i
+                q_ps = psum.tile([P, NE], F32, name="q_ps", tag="big", bufs=2)
                 mx(q_ps[:], oc[:], os_[:], w2c[:, c, :], w2s[:, c, :])
                 split_bank(q_ps[:], [w[:, i, :] for w in qn])
-                qt_ps = psum.tile([P, 4, P], F32, name="qt_ps", tag="big", bufs=3)
+                qt_ps = psum.tile([P, 4, P], F32, name="qt_ps", tag="big", bufs=2)
                 for fc in range(4):
                     cs = slice(fc * P, (fc + 1) * P)
                     mx(qt_ps[:, fc, :], w2c[:, c, cs], w2s[:, c, cs], oc[:], os_[:])
                 split_bank(qt_ps[:].rearrange("p k j -> p (k j)"), [w[:, i, :] for w in qt])
 
         def stat2(t, fc, part):
-            return tiles2[t // 4][0][part][:, t % 4, fc * P:(fc + 1) * P]
+            return tiles2[t // 8][0][part][:, t % 8, fc * P:(fc + 1) * P]
 
         def stat2_t(t, fc, part):
-            return tiles2[t // 4][1][part][:, t % 4, fc * P:(fc + 1) * P]
+            return tiles2[t // 8][1][part][:, t % 8, fc * P:(fc + 1) * P]
 
         def finish2(scol, fb_ps):
             o_sb = small.tile([P, NC2, NA, 4], F32, name="o_sb", tag="o_sb", bufs=1)

@@ -16,10 +16,12 @@ P = 128
 NA, NB, ND, NE, NH, NC2 = 4, 128, 512, 512, 32, 16
 HG = 4
 NT = HG * NA
-HELD = 14
+HELD = 13
 LO_ON_POOL = ()
-ON_VECTOR = ()
-SCALERS = "GVGVGVGVGVGVGVGV"
+SCALERS = "VVVS"
+W2_PER = 2
+FIRST_ON_VECTOR = 8
+PREP_EVERY = 2
 FLOPS = 2 * (NA * NB * ND * NE * NH + NA * NH * NE * NE * NC2)
 
 
@@ -29,8 +31,7 @@ def tile_capsulelayer_kernel(tc, x, route_weights1, route_weights, out):
         const = ctx.enter_context(tc.tile_pool(name="const", bufs=1))
         stage = ctx.enter_context(tc.tile_pool(name="stage", bufs=2))
         split = ctx.enter_context(tc.tile_pool(name="split", bufs=HELD))
-        carry = ctx.enter_context(tc.tile_pool(name="carry", bufs=4))
-        small = ctx.enter_context(tc.tile_pool(name="small", bufs=2))
+        carry = ctx.enter_context(tc.tile_pool(name="carry", bufs=6))
         psum = ctx.enter_context(tc.psum_pool(name="psum", bufs=1))
 
         ident_f = const.tile([P, P], F32, name="ident_f")
@@ -60,7 +61,7 @@ def tile_capsulelayer_kernel(tc, x, route_weights1, route_weights, out):
         nc.vector.memset(z_blk[:], float(NH))
         ucols = []
         sqcs = []
-        for i in range(3):
+        for i in range(4):
             ucol = const.tile([P, P], F32, name="ucol%d" % i)
             nc.vector.memset(ucol[:], 0.0)
             ucols.append(ucol)
@@ -118,7 +119,7 @@ def tile_capsulelayer_kernel(tc, x, route_weights1, route_weights, out):
                 evv = ev[:].rearrange("p s (n c) -> p s n c", c=32)
                 per = n_tiles if n_prob == 1 else n_tiles // 2
                 for t0 in range(0, n_tiles, per):
-                    s_ps = psum.tile([P, per, 4, 3, n_prob], F32, name="s_ps", tag="pb", bufs=3)
+                    s_ps = psum.tile([P, per, 4, 3, n_prob], F32, name="s_ps", tag="pb", bufs=2)
                     for t in range(t0, t0 + per):
                         rhs = evv[:, :, 0:n_prob, t]
                         for fc in range(4):
@@ -134,7 +135,7 @@ def tile_capsulelayer_kernel(tc, x, route_weights1, route_weights, out):
                 nc.vector.tensor_reduce(
                     out=sqc[:].rearrange("p (n c) -> p c n", c=32)[:, 0:n_tiles, 0:n_prob],
                     in_=sq[:].rearrange("p (t f) n -> p t n f", f=4), axis=AX.X, op=ALU.add)
-                n_ps = psum.tile([P, 2], F32, name="n_ps", tag="u")
+                n_ps = psum.tile([P, 2], F32, name="n_ps", tag="t", bufs=2)
                 nc.tensor.matmul(n_ps[:], lhsT=sqc[:], rhs=ones_f[:], start=True, stop=True)
                 n_sb = small.tile([P, 1], F32, name="n_sb", tag="n_sb", bufs=6)
                 nc.vector.tensor_copy(out=n_sb[:], in_=n_ps[:, 0:1])
@@ -151,7 +152,7 @@ def tile_capsulelayer_kernel(tc, x, route_weights1, route_weights, out):
                     nc.tensor.transpose(fb_ps[:], f[:, 0:1].to_broadcast([P, P]), ident_f[:])
                     finish(scol, fb_ps)
                     break
-                u_ps = psum.tile([P, n_tiles, 3, n_prob], F32, name="u_ps", tag="u")
+                u_ps = psum.tile([P, n_tiles, 3, n_prob], F32, name="u_ps", tag="fold", bufs=2)
                 svv = sv[:].rearrange("p s (t f n) -> p s t f n", t=n_tiles, f=4)
                 for t in range(n_tiles):
                     for fc in range(4):
@@ -187,152 +188,266 @@ def tile_capsulelayer_kernel(tc, x, route_weights1, route_weights, out):
         nc.vector.quantize_mx(out=xc[:].bitcast(FP8X4), scales=xs[:], in_=xg[:].rearrange("p w t -> p (w t)"))
 
         tiles1 = {}
-        sums1 = {}
-        state1 = {}
-        turn = [0]
+        sums = {}
+        codes = {}
+        held = {}
+        state = {}
+        factor = {}
+        done = {}
+        later = {}
 
-        def new_sums():
-            scol = carry.tile([P, NT * 4], F32, name="scol1", tag="scol1", bufs=6)
-            return scol
+        def at(tick, step):
+            later[tick] = later.get(tick, []) + [step]
 
-        def produce1(g):
-            scol = new_sums()
-            sums1[g] = scol
-            for l in range(HG):
-                h = g * HG + l
-                wc = stage.tile([P, NE], U32, name="wc", tag="wc", align_bytes=64)
-                ws = stage.tile([P, NE], U8, name="ws", tag="ws", align_bytes=64)
-                quantise_weights(route_weights1[h].rearrange("(p t) e -> p t e", t=4), wc[:], ws[:])
-                ptf = split.tile([P, 4, NA * NB], F32, name="ptf", tag="ptf")
-                tiles1[h] = ptf
-                for c in range(4):
-                    cs = slice(c * P, (c + 1) * P)
-                    pt_ps = psum.tile([P, NA * NB], F32, name="pt_ps", tag="big", bufs=2)
-                    mx(pt_ps[:], wc[:, cs], ws[:, cs], xc[:], xs[:])
-                    for a in range(NA):
-                        bs = slice(a * NB, (a + 1) * NB)
-                        col = (l * NA + a) * 4 + c
-                        nc.scalar.activation(out=ptf[:, c, bs], in_=pt_ps[:, bs], func=ACT.Copy, accum_out=scol[:, col:col + 1])
+        jobs = []
+        for k in range(NH // HG):
+            jobs.extend([("w1", k * HG + l) for l in range(HG)])
+            if k >= 1:
+                jobs.extend([("w2", c) for c in range((k - 1) * W2_PER, min(k * W2_PER, NC2))])
+        jobs.extend([("w2", c) for c in range((NH // HG - 1) * W2_PER, NC2)])
+        prepared = [0, 0, 0]
 
-        def squash_factor(scol, z):
-            sqc = sqcs[turn[0] % 3]
-            sq = small.tile([P, NT, 4], F32, name="sq1", tag="sq1", bufs=3)
-            nc.scalar.activation(out=sq[:].rearrange("p t f -> p (t f)"), in_=scol[:, 0:NT * 4], func=ACT.Square)
-            nc.vector.tensor_reduce(out=sqc[:, 0:NT], in_=sq[:], axis=AX.X, op=ALU.add)
-            n_ps = psum.tile([P, 2], F32, name="n_ps1", tag="u")
-            nc.tensor.matmul(n_ps[:], lhsT=sqc[:], rhs=ones_f[:], start=True, stop=True)
-            n_sb = small.tile([P, 1], F32, name="n_sb", tag="n_sb", bufs=6)
-            nc.vector.tensor_copy(out=n_sb[:], in_=n_ps[:, 0:1])
-            den = small.tile([P, 1], F32, name="den", tag="den", bufs=6)
-            nc.vector.tensor_scalar(out=den[:], in0=z[:], scalar1=z[:, 0:1], scalar2=n_sb[:, 0:1], op0=ALU.mult, op1=ALU.add)
-            rden = small.tile([P, 1], F32, name="rden", tag="rden", bufs=6)
-            nc.vector.reciprocal(out=rden[:], in_=den[:])
-            rt = small.tile([P, 1], F32, name="rt", tag="rt", bufs=6)
-            nc.gpsimd.tensor_tensor(out=rt[:], in0=n_sb[:], in1=half[:], op=ALU.pow)
-            f = small.tile([P, 1], F32, name="f", tag="f", bufs=6)
-            nc.vector.tensor_tensor(out=f[:], in0=rt[:], in1=rden[:], op=ALU.mult)
-            return f
+        def prep(stage_no):
+            i = prepared[stage_no]
+            if i >= len(jobs) or (stage_no > 0 and prepared[stage_no - 1] <= i):
+                return
+            kind, n = jobs[i]
+            if stage_no == 2 and kind == "w1" and n >= len(tiles1) + 5:
+                return
+            prepared[stage_no] += 1
+            if stage_no == 0:
+                raw = stage.tile([P, 4, NE], BF16, name="raw", tag="raw", bufs=2)
+                held[("raw", i)] = raw
+                rows = route_weights1[n].rearrange("(p t) e -> p t e", t=4) if kind == "w1" else route_weights[n].rearrange("(t p) f -> p t f", p=P)
+                nc.sync.dma_start(out=raw[:], in_=rows)
+            elif stage_no == 1:
+                raw = held[("raw", i)]
+                grouped = stage.tile([P, NE, 4], BF16, name="grouped", tag="grouped", bufs=2, align_bytes=64)
+                held[("grouped", i)] = grouped
+                dst = grouped[:].rearrange("p (c i) t -> p c t i", i=4)
+                src = raw[:].rearrange("p t (c i) -> p c t i", i=4)
+                if i < FIRST_ON_VECTOR:
+                    nc.vector.tensor_copy(out=dst, in_=src)
+                else:
+                    nc.gpsimd.tensor_scalar(out=dst, in0=src, scalar1=1.0, scalar2=0.0, op0=ALU.mult, op1=ALU.add)
+            else:
+                grouped = held[("grouped", i)]
+                if kind == "w1":
+                    wc = stage.tile([P, NE], U32, name="wc", tag="wc", bufs=5, align_bytes=64)
+                    ws = stage.tile([P, NE], U8, name="ws", tag="ws", bufs=5, align_bytes=64)
+                    codes[n] = (wc, ws)
+                    cw, sw = wc[:], ws[:]
+                else:
+                    cw, sw = w2c[:, n, :], w2s[:, n, :]
+                nc.vector.quantize_mx(out=cw.bitcast(FP8X4), scales=sw, in_=grouped[:].rearrange("p w t -> p (w t)"))
 
-        def agree_and_softmax(g, scol, f, lt):
-            ucol = ucols[turn[0] % 3]
-            for l in range(HG):
-                ptf = tiles1[g * HG + l]
-                fold_ps = psum.tile([P, NA, P], F32, name="fold_ps", tag="pb", bufs=3)
+        def prep_until(h):
+            while h not in codes:
+                for stage_no in range(3):
+                    prep(stage_no)
+
+        def new_sums(g, rnd):
+            if (g, rnd) not in sums:
+                scol = carry.tile([P, NT * 4], F32, name="scol1", tag="scol1", bufs=8)
+                sums[(g, rnd)] = scol
+            return sums[(g, rnd)]
+
+        def first_sums(g, l):
+            h = g * HG + l
+            prep_until(h)
+            scol = new_sums(g, 0)
+            wc, ws = codes[h]
+            ptf = split.tile([P, 4, NA * NB], F32, name="ptf", tag="ptf")
+            tiles1[h] = ptf
+            for c in range(4):
+                cs = slice(c * P, (c + 1) * P)
+                pt_ps = psum.tile([P, NA * NB], F32, name="pt_ps", tag="big", bufs=2)
+                mx(pt_ps[:], wc[:, cs], ws[:, cs], xc[:], xs[:])
                 for a in range(NA):
-                    t = l * NA + a
                     bs = slice(a * NB, (a + 1) * NB)
-                    scaled = small.tile([P, 4, NB], F32, name="scaled", tag="scaled", bufs=4)
-                    for c in range(4):
-                        sc = scol[:, t * 4 + c:t * 4 + c + 1]
-                        if SCALERS[t] == "G":
-                            nc.gpsimd.tensor_scalar(out=scaled[:, c, :], in0=ptf[:, c, bs], scalar1=sc, scalar2=0.0, op0=ALU.mult, op1=ALU.add)
-                        elif SCALERS[t] == "V":
-                            nc.vector.tensor_scalar(out=scaled[:, c, :], in0=ptf[:, c, bs], scalar1=sc, scalar2=None, op0=ALU.mult)
-                        else:
-                            nc.scalar.activation(out=scaled[:, c, :], in_=ptf[:, c, bs], func=ACT.Copy, scale=sc)
-                    for c in range(4):
-                        nc.tensor.matmul(fold_ps[:, a, :], lhsT=scaled[:, c, :], rhs=ident_f[:], is_transpose=True, start=(c == 0), stop=(c == 3))
-                nc.vector.tensor_reduce(out=ucol[:, l * NA:(l + 1) * NA], in_=fold_ps[:], axis=AX.X, op=ALU.add)
-            ut_ps = psum.tile([P, P], F32, name="ut_ps", tag="t", bufs=2)
-            nc.tensor.transpose(ut_ps[:], ucol[:], ident_f[:])
-            lt_new = carry.tile([P, P], F32, name="lt1", tag="lt1")
-            nc.vector.scalar_tensor_tensor(out=lt_new[:], in0=ut_ps[:], scalar=f[:, 0:1], in1=lt[:], op0=ALU.mult, op1=ALU.add)
-            negmax = small.tile([P, 1], F32, name="negmax", tag="negmax", bufs=6)
-            nc.vector.tensor_reduce(out=negmax[:], in_=lt_new[:], axis=AX.X, op=ALU.max, negate=True)
-            e_sb = small.tile([P, P], F32, name="e_sb", tag="e_sb", bufs=3)
-            z = carry.tile([P, 1], F32, name="z1", tag="z1")
-            nc.scalar.activation(out=e_sb[:], in_=lt_new[:], func=ACT.Exp, bias=negmax[:, 0:1], scale=1.0, accum_out=z[:])
-            et_ps = psum.tile([P, P], F32, name="et_ps", tag="t", bufs=2)
-            nc.tensor.transpose(et_ps[:], e_sb[:], ident_f[:])
-            et = carry.tile([P, NT], F32, name="et1", tag="et1")
-            nc.vector.tensor_copy(out=et[:], in_=et_ps[:, 0:NT])
-            return lt_new, z, et
+                    col = (l * NA + a) * 4 + c
+                    nc.scalar.activation(out=ptf[:, c, bs], in_=pt_ps[:, bs], func=ACT.Copy, accum_out=scol[:, col:col + 1])
 
-        def weighted_sums(g, et):
-            scol = new_sums()
-            for l in range(HG):
-                ptf = tiles1[g * HG + l]
-                pb_ps = psum.tile([P, NA, NB], F32, name="pb_ps", tag="pb", bufs=3)
+        def weighted_sums(g, l, rnd):
+            scol = new_sums(g, rnd)
+            et = state[g][2]
+            ptf = tiles1[g * HG + l]
+            pb_ps = psum.tile([P, NA, NB], F32, name="pb_ps", tag="pb", bufs=2)
+            for a in range(NA):
+                t = l * NA + a
+                nc.tensor.transpose(pb_ps[:, a, :], et[:, t:t + 1].to_broadcast([P, P]), ident_f[:])
+            for c in range(4):
+                prod = work1.tile([P, NA * NB], F32, name="prod", tag="prod", bufs=6)
+                nc.vector.tensor_tensor(out=prod[:], in0=pb_ps[:].rearrange("p a b -> p (a b)"), in1=ptf[:, c, :], op=ALU.mult)
                 for a in range(NA):
-                    t = l * NA + a
-                    nc.tensor.transpose(pb_ps[:, a, :], et[:, t:t + 1].to_broadcast([P, P]), ident_f[:])
+                    col = (l * NA + a) * 4 + c
+                    waste_s = work1.tile([P, NB], BF16, name="waste_s", tag="waste_s")
+                    nc.scalar.activation(out=waste_s[:], in_=prod[:, a * NB:(a + 1) * NB], func=ACT.Copy, accum_out=scol[:, col:col + 1])
+
+        def scale(g, l, rnd):
+            scol = sums[(g, rnd)]
+            ptf = tiles1[g * HG + l]
+            for a in range(NA):
+                t = l * NA + a
+                bs = slice(a * NB, (a + 1) * NB)
+                scaled = work1.tile([P, 4, NB], F32, name="scaled", tag="scaled", bufs=12)
+                held[("scaled", g, l, a)] = scaled
                 for c in range(4):
-                    if l in ON_VECTOR:
-                        for a in range(NA):
-                            col = (l * NA + a) * 4 + c
-                            waste_v = small.tile([P, NB], F32, name="waste_v", tag="waste_v")
-                            nc.vector.scalar_tensor_tensor(
-                                out=waste_v[:], in0=pb_ps[:, a, :], scalar=1.0, in1=ptf[:, c, a * NB:(a + 1) * NB],
-                                op0=ALU.mult, op1=ALU.mult, accum_out=scol[:, col:col + 1])
+                    sc = scol[:, t * 4 + c:t * 4 + c + 1]
+                    if SCALERS[(rnd * NT + t) % len(SCALERS)] == "V":
+                        nc.vector.tensor_scalar(out=scaled[:, c, :], in0=ptf[:, c, bs], scalar1=sc, scalar2=None, op0=ALU.mult)
                     else:
-                        prod = small.tile([P, NA * NB], F32, name="prod", tag="prod", bufs=3)
-                        nc.vector.tensor_tensor(out=prod[:], in0=pb_ps[:].rearrange("p a b -> p (a b)"), in1=ptf[:, c, :], op=ALU.mult)
-                        for a in range(NA):
-                            col = (l * NA + a) * 4 + c
-                            waste_s = small.tile([P, NB], BF16, name="waste_s", tag="waste_s")
-                            nc.scalar.activation(out=waste_s[:], in_=prod[:, a * NB:(a + 1) * NB], func=ACT.Copy, accum_out=scol[:, col:col + 1])
-            return scol
+                        nc.scalar.activation(out=scaled[:, c, :], in_=ptf[:, c, bs], func=ACT.Copy, scale=sc)
 
-        def round1(g):
-            turn[0] += 1
-            f = squash_factor(sums1[g], z_one)
-            state1[g] = agree_and_softmax(g, sums1[g], f, lt_zero)
+        def fold(g, l):
+            fold_ps = psum.tile([P, NA, P], F32, name="fold_ps", tag="fold", bufs=2)
+            held[("fold", g, l)] = fold_ps
+            for a in range(NA):
+                scaled = held[("scaled", g, l, a)]
+                for c in range(4):
+                    nc.tensor.matmul(fold_ps[:, a, :], lhsT=scaled[:, c, :], rhs=ident_f[:], is_transpose=True, start=(c == 0), stop=(c == 3))
 
-        def round2(g):
-            turn[0] += 1
-            lt, z, et = state1[g]
-            scol = weighted_sums(g, et)
-            f = squash_factor(scol, z)
-            state1[g] = agree_and_softmax(g, scol, f, lt)
+        def agreement(g, l, rnd):
+            ucol = ucols[(2 * g + rnd) % len(ucols)]
+            nc.vector.tensor_reduce(out=ucol[:, l * NA:(l + 1) * NA], in_=held[("fold", g, l)][:], axis=AX.X, op=ALU.add)
 
-        def round3(g):
-            turn[0] += 1
-            lt, z, et = state1[g]
-            scol = weighted_sums(g, et)
-            f = squash_factor(scol, z)
-            fb_ps = psum.tile([P, P], F32, name="fb_ps1", tag="t", bufs=2)
-            nc.tensor.transpose(fb_ps[:], f[:, 0:1].to_broadcast([P, P]), ident_f[:])
-            nc.vector.tensor_tensor(
-                out=og[:].rearrange("p (a h) c -> p h a c", a=NA)[:, g * HG:(g + 1) * HG],
-                in0=scol[:, 0:NT * 4].rearrange("p (l a f) -> p l a f", l=HG, a=NA),
-                in1=fb_ps[:, 0:NT].rearrange("p (l a) -> p l a", a=NA).unsqueeze(3).to_broadcast([P, HG, NA, 4]),
-                op=ALU.mult)
+        def squash_steps(g, rnd):
+            key = (g, rnd)
+            sqc = sqcs[(3 * g + rnd) % len(sqcs)]
+
+            def step1():
+                sq = work1.tile([P, NT, 4], F32, name="sq1", tag="sq1", bufs=3)
+                held[("sq", key)] = sq
+                nc.scalar.activation(out=sq[:].rearrange("p t f -> p (t f)"), in_=sums[key][:], func=ACT.Square)
+
+            def step2():
+                nc.vector.tensor_reduce(out=sqc[:, 0:NT], in_=held[("sq", key)][:], axis=AX.X, op=ALU.add)
+                n_ps = psum.tile([P, 2], F32, name="n_ps1", tag="t", bufs=2)
+                held[("n", key)] = n_ps
+                nc.tensor.matmul(n_ps[:], lhsT=sqc[:], rhs=ones_f[:], start=True, stop=True)
+
+            def step3():
+                z = z_one if rnd == 0 else state[g][1]
+                n_sb = work1.tile([P, 1], F32, name="n_sb", tag="n_sb", bufs=6)
+                nc.vector.tensor_copy(out=n_sb[:], in_=held[("n", key)][:, 0:1])
+                rt = work1.tile([P, 1], F32, name="rt", tag="rt", bufs=6)
+                held[("rt", key)] = rt
+                nc.gpsimd.tensor_tensor(out=rt[:], in0=n_sb[:], in1=half[:], op=ALU.pow)
+                den = work1.tile([P, 1], F32, name="den", tag="den", bufs=6)
+                nc.vector.tensor_scalar(out=den[:], in0=z[:], scalar1=z[:, 0:1], scalar2=n_sb[:, 0:1], op0=ALU.mult, op1=ALU.add)
+                rden = work1.tile([P, 1], F32, name="rden", tag="rden", bufs=6)
+                held[("rden", key)] = rden
+                nc.vector.reciprocal(out=rden[:], in_=den[:])
+
+            def step4():
+                f = work1.tile([P, 1], F32, name="f", tag="f", bufs=6)
+                factor[key] = f
+                nc.vector.tensor_tensor(out=f[:], in0=held[("rt", key)][:], in1=held[("rden", key)][:], op=ALU.mult)
+
+            return [step1, step2, step3, step4]
+
+        def softmax_steps(g, rnd):
+            key = (g, rnd)
+            ucol = ucols[(2 * g + rnd) % len(ucols)]
+
+            def step1():
+                ut_ps = psum.tile([P, P], F32, name="ut_ps", tag="t", bufs=2)
+                held[("ut", key)] = ut_ps
+                nc.tensor.transpose(ut_ps[:], ucol[:], ident_f[:])
+
+            def step2():
+                lt = lt_zero if rnd == 0 else state[g][0]
+                lt_new = carry.tile([P, P], F32, name="lt1", tag="lt1")
+                held[("lt", key)] = lt_new
+                nc.vector.scalar_tensor_tensor(out=lt_new[:], in0=held[("ut", key)][:], scalar=factor[key][:, 0:1], in1=lt[:], op0=ALU.mult, op1=ALU.add)
+                negmax = work1.tile([P, 1], F32, name="negmax", tag="negmax", bufs=6)
+                held[("negmax", key)] = negmax
+                nc.vector.tensor_reduce(out=negmax[:], in_=lt_new[:], axis=AX.X, op=ALU.max, negate=True)
+
+            def step3():
+                e_sb = work1.tile([P, P], F32, name="e_sb", tag="e_sb", bufs=3)
+                z = carry.tile([P, 1], F32, name="z1", tag="z1")
+                held[("z", key)] = z
+                nc.scalar.activation(out=e_sb[:], in_=held[("lt", key)][:], func=ACT.Exp, bias=held[("negmax", key)][:, 0:1], scale=1.0, accum_out=z[:])
+                et_ps = psum.tile([P, P], F32, name="et_ps", tag="t", bufs=2)
+                held[("et", key)] = et_ps
+                nc.tensor.transpose(et_ps[:], e_sb[:], ident_f[:])
+
+            def step4():
+                et = carry.tile([P, NT], F32, name="et1", tag="et1")
+                nc.vector.tensor_copy(out=et[:], in_=held[("et", key)][:, 0:NT])
+                state[g] = (held[("lt", key)], held[("z", key)], et)
+                done[key] = True
+
+            return [step1, step2, step3, step4]
+
+        def finish_steps(g):
+            def step1():
+                fb_ps = psum.tile([P, P], F32, name="fb_ps1", tag="t", bufs=2)
+                held[("fb", g)] = fb_ps
+                nc.tensor.transpose(fb_ps[:], factor[(g, 2)][:, 0:1].to_broadcast([P, P]), ident_f[:])
+
+            def step2():
+                nc.vector.tensor_tensor(
+                    out=og[:].rearrange("p (a h) c -> p h a c", a=NA)[:, g * HG:(g + 1) * HG],
+                    in0=sums[(g, 2)][:].rearrange("p (l a f) -> p l a f", l=HG, a=NA),
+                    in1=held[("fb", g)][:, 0:NT].rearrange("p (l a) -> p l a", a=NA).unsqueeze(3).to_broadcast([P, HG, NA, 4]),
+                    op=ALU.mult)
+                done[(g, 2)] = True
+
+            return [step1, step2]
 
         n_groups = NH // HG
-        produce1(0)
+        items = []
         for k in range(n_groups + 2):
-            if 0 <= k - 2 < n_groups:
-                round3(k - 2)
-            if 0 <= k - 1 < n_groups:
-                round2(k - 1)
-            if k < n_groups:
-                round1(k)
-            if k + 1 < n_groups:
-                produce1(k + 1)
-            if k < n_groups:
-                for c in range(2 * k, 2 * k + 2):
-                    quantise_weights(route_weights[c].rearrange("(t p) f -> p t f", p=P), w2c[:, c, :], w2s[:, c, :])
+            for rnd in range(3):
+                if 0 <= k - rnd < n_groups:
+                    items.extend([(k - rnd, l, rnd) for l in range(HG)])
 
+        with tc.tile_pool(name="work1", bufs=2) as work1, tc.manual_schedule():
+            placed = {}
+            nxt = 0
+            tick = 0
+            while len(done) < 3 * n_groups:
+                if tick % PREP_EVERY == 0:
+                    for stage_no in (2, 1, 0):
+                        prep(stage_no)
+                if nxt < len(items):
+                    g, l, rnd = items[nxt]
+                    if rnd == 0 or (g, rnd - 1) in done:
+                        if rnd == 0:
+                            first_sums(g, l)
+                        else:
+                            weighted_sums(g, l, rnd)
+                        placed[tick] = items[nxt]
+                        nxt += 1
+                        if l == HG - 1:
+                            steps = squash_steps(g, rnd)
+                            for i in range(len(steps)):
+                                at(tick + 2 + i, steps[i])
+                            if rnd == 2:
+                                steps = finish_steps(g)
+                                for i in range(len(steps)):
+                                    at(tick + 6 + i, steps[i])
+                            else:
+                                steps = softmax_steps(g, rnd)
+                                for i in range(len(steps)):
+                                    at(tick + 6 + i, steps[i])
+                for lag, stage_fn in ((2, scale), (3, fold), (4, agreement)):
+                    if tick - lag in placed and placed[tick - lag][2] < 2:
+                        g, l, rnd = placed[tick - lag]
+                        if lag == 3:
+                            fold(g, l)
+                        else:
+                            stage_fn(g, l, rnd)
+                for step in later.get(tick, []):
+                    step()
+                tick += 1
+            while prepared[2] < len(jobs):
+                for stage_no in range(3):
+                    prep(stage_no)
+
+        small = ctx.enter_context(tc.tile_pool(name="small", bufs=2))
         nc.vector.quantize_mx(out=oc[:].bitcast(FP8X4), scales=os_[:], in_=og[:].rearrange("p w t -> p (w t)"))
         tiles2 = {}
         for q in range(NC2 // 8):

@@ -14,15 +14,15 @@ AX = mybir.AxisListType
 
 P = 128
 NA, NB, ND, NE, NH, NC2 = 4, 128, 512, 512, 32, 16
+FLOPS = 2 * (NA * NB * ND * NE * NH + NA * NH * NE * NE * NC2)
+
 HG = 4
 NT = HG * NA
+NG = NH // HG
+TURNS = 3 * HG
 HELD = 13
-LO_ON_POOL = ()
-SCALERS = "VVVS"
-W2_PER = 2
-FIRST_ON_VECTOR = 8
-PREP_EVERY = 2
-FLOPS = 2 * (NA * NB * ND * NE * NH + NA * NH * NE * NE * NC2)
+SCALAR_SCALES = 4
+ON_VECTOR = 8
 
 
 def tile_capsulelayer_kernel(tc, x, route_weights1, route_weights, out):
@@ -30,9 +30,9 @@ def tile_capsulelayer_kernel(tc, x, route_weights1, route_weights, out):
     with ExitStack() as ctx:
         const = ctx.enter_context(tc.tile_pool(name="const", bufs=1))
         stage = ctx.enter_context(tc.tile_pool(name="stage", bufs=2))
-        split = ctx.enter_context(tc.tile_pool(name="split", bufs=HELD))
-        carry = ctx.enter_context(tc.tile_pool(name="carry", bufs=6))
-        psum = ctx.enter_context(tc.psum_pool(name="psum", bufs=1))
+        priors1 = ctx.enter_context(tc.tile_pool(name="priors1", bufs=HELD))
+        carry = ctx.enter_context(tc.tile_pool(name="carry", bufs=8))
+        psum = ctx.enter_context(tc.psum_pool(name="psum", bufs=2))
 
         ident_f = const.tile([P, P], F32, name="ident_f")
         make_identity(nc, ident_f[:])
@@ -42,20 +42,14 @@ def tile_capsulelayer_kernel(tc, x, route_weights1, route_weights, out):
         nc.vector.memset(ones_f[:], 1.0)
         half = const.tile([P, 1], F32, name="half")
         nc.vector.memset(half[:], 0.5)
-        ev_one = const.tile([P, 3, P], BF16, name="ev_one")
-        nc.vector.memset(ev_one[:], 0.0)
-        nc.vector.memset(ev_one[:, 0, :], 1.0)
         z_one = const.tile([P, 1], F32, name="z_one")
         nc.vector.memset(z_one[:], float(NB))
         lt_zero = const.tile([P, P], F32, name="lt_zero")
         nc.vector.memset(lt_zero[:], 0.0)
-        ev_blk = const.tile([P, 3, P], BF16, name="ev_blk")
-        nc.vector.memset(ev_blk[:], 0.0)
         lt_blk = const.tile([P, P], F32, name="lt_blk")
         nc.vector.memset(lt_blk[:], -1.0e30)
         for a in range(NA):
             blk = slice(32 * a, 32 * a + 32)
-            nc.vector.memset(ev_blk[blk, 0, blk], 1.0)
             nc.vector.memset(lt_blk[blk, blk], 0.0)
         z_blk = const.tile([P, 1], F32, name="z_blk")
         nc.vector.memset(z_blk[:], float(NH))
@@ -77,212 +71,161 @@ def tile_capsulelayer_kernel(tc, x, route_weights1, route_weights, out):
         oc = const.tile([P, NA * NH], U32, name="oc", align_bytes=64)
         os_ = const.tile([P, NA * NH], U8, name="os_", align_bytes=64)
 
-        def quantise_weights(rows, codes, scales):
-            raw = stage.tile([P, 4, NE], BF16, name="raw", tag="raw", bufs=2)
-            nc.sync.dma_start(out=raw[:], in_=rows)
-            grouped = stage.tile([P, NE, 4], BF16, name="grouped", tag="grouped", align_bytes=64)
-            nc.gpsimd.tensor_scalar(
-                out=grouped[:].rearrange("p (c i) t -> p c t i", i=4),
-                in0=raw[:].rearrange("p t (c i) -> p c t i", i=4),
-                scalar1=1.0, scalar2=0.0, op0=ALU.mult, op1=ALU.add,
-            )
-            nc.vector.quantize_mx(out=codes.bitcast(FP8X4), scales=scales, in_=grouped[:].rearrange("p w t -> p (w t)"))
-
-        banks = [0]
-
-        def split_bank(bank, terms):
-            hi, mid, lo = terms
-            nc.scalar.copy(out=hi, in_=bank)
-            rest = small.tile([P, NE], F32, name="rest", tag="rest", bufs=2)
-            nc.vector.tensor_tensor(out=rest[:], in0=bank, in1=hi, op=ALU.subtract)
-            nc.scalar.copy(out=mid, in_=rest[:])
-            eng = nc.gpsimd if banks[0] % 8 in LO_ON_POOL else nc.vector
-            eng.tensor_tensor(out=lo, in0=rest[:], in1=mid, op=ALU.subtract)
-            banks[0] += 1
-
-        def split_small(src, dst, width):
-            nc.vector.tensor_copy(out=dst[:, 0, 0:width], in_=src)
-            rest = small.tile([P, 256], F32, name="rest_s", tag="rest_s")
-            nc.vector.tensor_tensor(out=rest[:, 0:width], in0=src, in1=dst[:, 0, 0:width], op=ALU.subtract)
-            nc.vector.tensor_copy(out=dst[:, 1, 0:width], in_=rest[:, 0:width])
-            nc.vector.tensor_tensor(out=dst[:, 2, 0:width], in0=rest[:, 0:width], in1=dst[:, 1, 0:width], op=ALU.subtract)
-
         def mx(out_ps, l_codes, l_scales, r_codes, r_scales):
             nc.tensor.matmul_mx(out=out_ps, lhsT=l_codes.bitcast(FP8X4), lhsT_scale=l_scales,
                                 rhs=r_codes.bitcast(FP8X4), rhs_scale=r_scales, start=True, stop=True)
 
-        def routing(n_tiles, n_prob, stat, stat_t, ev, z, lt, which, finish):
-            ucol, sqc = ucols[which], sqcs[which]
-            cols = P if n_prob > 1 else n_tiles
-            for rnd in range(3):
-                scol = small.tile([P, n_tiles * 4, n_prob], F32, name="scol", tag="scol")
-                evv = ev[:].rearrange("p s (n c) -> p s n c", c=32)
-                per = n_tiles if n_prob == 1 else n_tiles // 2
-                for t0 in range(0, n_tiles, per):
-                    s_ps = psum.tile([P, per, 4, 3, n_prob], F32, name="s_ps", tag="pb", bufs=2)
-                    for t in range(t0, t0 + per):
-                        rhs = evv[:, :, 0:n_prob, t]
-                        for fc in range(4):
-                            for part in range(3):
-                                nc.tensor.matmul(s_ps[:, t - t0, fc, 0:3 - part], lhsT=stat(t, fc, part), rhs=rhs[:, 0:3 - part], start=(part == 0), stop=(part == 2))
-                    nc.vector.tensor_reduce(out=scol[:, t0 * 4:(t0 + per) * 4, :], in_=s_ps[:].rearrange("p t f s n -> p (t f) n s"), axis=AX.X, op=ALU.add)
-                scol_flat = scol[:].rearrange("p a n -> p (a n)")
-                if rnd < 2:
-                    sv = small.tile([P, 3, n_tiles * 4 * n_prob], BF16, name="sv", tag="sv")
-                    split_small(scol_flat, sv, n_tiles * 4 * n_prob)
-                sq = small.tile([P, n_tiles * 4, n_prob], F32, name="sq", tag="sq")
-                nc.scalar.activation(out=sq[:], in_=scol[:], func=ACT.Square)
-                nc.vector.tensor_reduce(
-                    out=sqc[:].rearrange("p (n c) -> p c n", c=32)[:, 0:n_tiles, 0:n_prob],
-                    in_=sq[:].rearrange("p (t f) n -> p t n f", f=4), axis=AX.X, op=ALU.add)
-                n_ps = psum.tile([P, 2], F32, name="n_ps", tag="t", bufs=2)
-                nc.tensor.matmul(n_ps[:], lhsT=sqc[:], rhs=ones_f[:], start=True, stop=True)
-                n_sb = small.tile([P, 1], F32, name="n_sb", tag="n_sb", bufs=6)
-                nc.vector.tensor_copy(out=n_sb[:], in_=n_ps[:, 0:1])
-                den = small.tile([P, 1], F32, name="den", tag="den", bufs=6)
-                nc.vector.tensor_scalar(out=den[:], in0=z[:], scalar1=z[:, 0:1], scalar2=n_sb[:, 0:1], op0=ALU.mult, op1=ALU.add)
-                rden = small.tile([P, 1], F32, name="rden", tag="rden", bufs=6)
-                nc.vector.reciprocal(out=rden[:], in_=den[:])
-                rt = small.tile([P, 1], F32, name="rt", tag="rt", bufs=6)
-                nc.gpsimd.tensor_tensor(out=rt[:], in0=n_sb[:], in1=half[:], op=ALU.pow)
-                f = small.tile([P, 1], F32, name="f", tag="f", bufs=6)
-                nc.vector.tensor_tensor(out=f[:], in0=rt[:], in1=rden[:], op=ALU.mult)
-                if rnd == 2:
-                    fb_ps = psum.tile([P, P], F32, name="fb_ps", tag="t", bufs=2)
-                    nc.tensor.transpose(fb_ps[:], f[:, 0:1].to_broadcast([P, P]), ident_f[:])
-                    finish(scol, fb_ps)
-                    break
-                u_ps = psum.tile([P, n_tiles, 3, n_prob], F32, name="u_ps", tag="fold", bufs=2)
-                svv = sv[:].rearrange("p s (t f n) -> p s t f n", t=n_tiles, f=4)
-                for t in range(n_tiles):
-                    for fc in range(4):
-                        rhs = svv[:, :, t, fc, :]
-                        for part in range(3):
-                            nc.tensor.matmul(u_ps[:, t, 0:3 - part], lhsT=stat_t(t, fc, part), rhs=rhs[:, 0:3 - part], start=(fc == 0 and part == 0), stop=(fc == 3 and part == 2))
-                nc.vector.tensor_reduce(
-                    out=ucol[:].rearrange("p (n c) -> p c n", c=32)[:, 0:n_tiles, 0:n_prob],
-                    in_=u_ps[:].rearrange("p t s n -> p t n s"), axis=AX.X, op=ALU.add)
-                ut_ps = psum.tile([P, P], F32, name="ut_ps", tag="t", bufs=2)
-                nc.tensor.transpose(ut_ps[:], ucol[:], ident_f[:])
-                lt_new = small.tile([P, P], F32, name="lt_new", tag="lt")
-                nc.vector.scalar_tensor_tensor(out=lt_new[:], in0=ut_ps[:], scalar=f[:, 0:1], in1=lt[:], op0=ALU.mult, op1=ALU.add)
-                lt = lt_new
-                negmax = small.tile([P, 1], F32, name="negmax", tag="negmax", bufs=6)
-                nc.vector.tensor_reduce(out=negmax[:], in_=lt[:], axis=AX.X, op=ALU.max, negate=True)
-                e_sb = small.tile([P, P], F32, name="e_sb", tag="e_sb", bufs=3)
-                z = small.tile([P, 1], F32, name="z", tag="z")
-                nc.scalar.activation(out=e_sb[:], in_=lt[:], func=ACT.Exp, bias=negmax[:, 0:1], scale=1.0, accum_out=z[:])
-                et_ps = psum.tile([P, P], F32, name="et_ps", tag="t", bufs=2)
-                nc.tensor.transpose(et_ps[:], e_sb[:], ident_f[:])
-                ev = small.tile([P, 3, P], BF16, name="ev", tag="ev")
-                split_small(et_ps[:, 0:cols], ev, cols)
+        def squash_steps(pool, s_flat, by_problem, sqc, sqc_own, z, f):
+            sq = pool.tile(list(s_flat.shape), F32, name="sq", tag="sq", bufs=4)
+            n_sb = pool.tile([P, 1], F32, name="n_sb", tag="n_sb", bufs=6)
+            rt = pool.tile([P, 1], F32, name="rt", tag="rt", bufs=6)
+            den = pool.tile([P, 1], F32, name="den", tag="den", bufs=6)
+            rden = pool.tile([P, 1], F32, name="rden", tag="rden", bufs=6)
+            got = {}
 
-        x_sb = stage.tile([P, NA, ND], BF16, name="x_sb", tag="raw", bufs=2)
+            def step1():
+                nc.scalar.activation(out=sq[:], in_=s_flat, func=ACT.Square)
+
+            def step2():
+                nc.vector.tensor_reduce(out=sqc_own, in_=by_problem(sq[:]), axis=AX.X, op=ALU.add)
+                n_ps = psum.tile([P, 2], F32, name="n_ps", tag="t")
+                got["n"] = n_ps
+                nc.tensor.matmul(n_ps[:], lhsT=sqc[:], rhs=ones_f[:], start=True, stop=True)
+
+            def step3():
+                nc.vector.tensor_copy(out=n_sb[:], in_=got["n"][:, 0:1])
+                nc.gpsimd.tensor_tensor(out=rt[:], in0=n_sb[:], in1=half[:], op=ALU.pow)
+                nc.vector.tensor_scalar(out=den[:], in0=z[:], scalar1=z[:, 0:1], scalar2=n_sb[:, 0:1], op0=ALU.mult, op1=ALU.add)
+                nc.vector.reciprocal(out=rden[:], in_=den[:])
+
+            def step4():
+                nc.vector.tensor_tensor(out=f[:], in0=rt[:], in1=rden[:], op=ALU.mult)
+
+            return [step1, step2, step3, step4]
+
+        def softmax_steps(pool, ucol, f, lt, lt_new, z, take_weights):
+            negmax = pool.tile([P, 1], F32, name="negmax", tag="negmax", bufs=6)
+            e_sb = pool.tile([P, P], F32, name="e_sb", tag="e_sb", bufs=4)
+            got = {}
+
+            def step1():
+                ut_ps = psum.tile([P, P], F32, name="ut_ps", tag="t")
+                got["ut"] = ut_ps
+                nc.tensor.transpose(ut_ps[:], ucol[:], ident_f[:])
+
+            def step2():
+                nc.vector.scalar_tensor_tensor(out=lt_new[:], in0=got["ut"][:], scalar=f[:, 0:1], in1=lt[:], op0=ALU.mult, op1=ALU.add)
+                nc.vector.tensor_reduce(out=negmax[:], in_=lt_new[:], axis=AX.X, op=ALU.max, negate=True)
+
+            def step3():
+                nc.scalar.activation(out=e_sb[:], in_=lt_new[:], func=ACT.Exp, bias=negmax[:, 0:1], scale=1.0, accum_out=z[:])
+                et_ps = psum.tile([P, P], F32, name="et_ps", tag="t")
+                got["et"] = et_ps
+                nc.tensor.transpose(et_ps[:], e_sb[:], ident_f[:])
+
+            def step4():
+                take_weights(got["et"])
+
+            return [step1, step2, step3, step4]
+
+        x_sb = stage.tile([P, NA, ND], BF16, name="x_sb", tag="raw")
         nc.sync.dma_start(out=x_sb[:], in_=x.rearrange("a b d -> b a d"))
         xg = stage.tile([P, NA * NB, 4], BF16, name="xg", tag="grouped", align_bytes=64)
         for a in range(NA):
-            xt_ps = psum.tile([P, 4, NB], BF16, name="xt_ps", tag="t", bufs=2)
+            xt_ps = psum.tile([P, 4, NB], BF16, name="xt_ps", tag="t")
             for t in range(4):
                 nc.tensor.transpose(xt_ps[:, t, :], x_sb[:, a, :].rearrange("b (p t) -> b t p", t=4)[:, t, :], ident_b[:])
             nc.vector.tensor_copy(out=xg[:, a * NB:(a + 1) * NB, :], in_=xt_ps[:].rearrange("p t b -> p b t"))
         nc.vector.quantize_mx(out=xc[:].bitcast(FP8X4), scales=xs[:], in_=xg[:].rearrange("p w t -> p (w t)"))
 
-        tiles1 = {}
-        sums = {}
+        per_group = NC2 // NG
+        jobs = [("w1", h) for h in range(HG)]
+        for g in range(1, NG + 1):
+            jobs.extend([("w2", (g - 1) * per_group + i) for i in range(per_group)])
+            if g < NG:
+                jobs.extend([("w1", g * HG + l) for l in range(HG)])
+        raws = {}
+        groupeds = {}
         codes = {}
-        held = {}
-        state = {}
-        factor = {}
-        done = {}
-        later = {}
 
-        def at(tick, step):
-            later[tick] = later.get(tick, []) + [step]
-
-        jobs = []
-        for k in range(NH // HG):
-            jobs.extend([("w1", k * HG + l) for l in range(HG)])
-            if k >= 1:
-                jobs.extend([("w2", c) for c in range((k - 1) * W2_PER, min(k * W2_PER, NC2))])
-        jobs.extend([("w2", c) for c in range((NH // HG - 1) * W2_PER, NC2)])
-        prepared = [0, 0, 0]
-
-        def prep(stage_no):
-            i = prepared[stage_no]
-            if i >= len(jobs) or (stage_no > 0 and prepared[stage_no - 1] <= i):
-                return
-            kind, n = jobs[i]
-            if stage_no == 2 and kind == "w1" and n >= len(tiles1) + 5:
-                return
-            prepared[stage_no] += 1
-            if stage_no == 0:
-                raw = stage.tile([P, 4, NE], BF16, name="raw", tag="raw", bufs=2)
-                held[("raw", i)] = raw
-                rows = route_weights1[n].rearrange("(p t) e -> p t e", t=4) if kind == "w1" else route_weights[n].rearrange("(t p) f -> p t f", p=P)
+        def weights_step(n):
+            if 0 <= n < len(jobs):
+                kind, m = jobs[n]
+                raw = stage.tile([P, 4, NE], BF16, name="raw", tag="raw")
+                raws[n] = raw
+                rows = route_weights1[m].rearrange("(p t) e -> p t e", t=4) if kind == "w1" else route_weights[m].rearrange("(t p) f -> p t f", p=P)
                 nc.sync.dma_start(out=raw[:], in_=rows)
-            elif stage_no == 1:
-                raw = held[("raw", i)]
-                grouped = stage.tile([P, NE, 4], BF16, name="grouped", tag="grouped", bufs=2, align_bytes=64)
-                held[("grouped", i)] = grouped
+            if 0 <= n - 1 < len(jobs):
+                grouped = stage.tile([P, NE, 4], BF16, name="grouped", tag="grouped", align_bytes=64)
+                groupeds[n - 1] = grouped
                 dst = grouped[:].rearrange("p (c i) t -> p c t i", i=4)
-                src = raw[:].rearrange("p t (c i) -> p c t i", i=4)
-                if i < FIRST_ON_VECTOR:
+                src = raws[n - 1][:].rearrange("p t (c i) -> p c t i", i=4)
+                if n - 1 < ON_VECTOR:
                     nc.vector.tensor_copy(out=dst, in_=src)
                 else:
                     nc.gpsimd.tensor_scalar(out=dst, in0=src, scalar1=1.0, scalar2=0.0, op0=ALU.mult, op1=ALU.add)
-            else:
-                grouped = held[("grouped", i)]
+            if 0 <= n - 2 < len(jobs):
+                kind, m = jobs[n - 2]
                 if kind == "w1":
-                    wc = stage.tile([P, NE], U32, name="wc", tag="wc", bufs=5, align_bytes=64)
-                    ws = stage.tile([P, NE], U8, name="ws", tag="ws", bufs=5, align_bytes=64)
-                    codes[n] = (wc, ws)
+                    wc = stage.tile([P, NE], U32, name="wc", tag="wc", bufs=HG + 1, align_bytes=64)
+                    ws = stage.tile([P, NE], U8, name="ws", tag="ws", bufs=HG + 1, align_bytes=64)
+                    codes[m] = (wc, ws)
                     cw, sw = wc[:], ws[:]
                 else:
-                    cw, sw = w2c[:, n, :], w2s[:, n, :]
-                nc.vector.quantize_mx(out=cw.bitcast(FP8X4), scales=sw, in_=grouped[:].rearrange("p w t -> p (w t)"))
+                    cw, sw = w2c[:, m, :], w2s[:, m, :]
+                nc.vector.quantize_mx(out=cw.bitcast(FP8X4), scales=sw, in_=groupeds[n - 2][:].rearrange("p w t -> p (w t)"))
 
-        def prep_until(h):
-            while h not in codes:
-                for stage_no in range(3):
-                    prep(stage_no)
+        tiles1 = {}
+        sums = {}
+        scaleds = {}
+        folds = {}
+        state = {}
+        factor = {}
+        chains = {}
 
-        def new_sums(g, rnd):
-            if (g, rnd) not in sums:
-                scol = carry.tile([P, NT * 4], F32, name="scol1", tag="scol1", bufs=8)
-                sums[(g, rnd)] = scol
-            return sums[(g, rnd)]
+        def turn(i):
+            step_no, r = divmod(i, TURNS)
+            rnd, l = divmod(r, HG)
+            g = step_no - rnd
+            return (g, l, rnd) if i >= 0 and 0 <= g < NG else None
 
-        def first_sums(g, l):
+        def by_scalar(t):
+            return t % SCALAR_SCALES == SCALAR_SCALES - 1
+
+        def sums_of(g, l, rnd):
+            if l == 0:
+                scol_new = carry.tile([P, NT * 4], F32, name="scol1", tag="scol1", bufs=10)
+                sums[(g, rnd)] = scol_new
+            scol = sums[(g, rnd)]
             h = g * HG + l
-            prep_until(h)
-            scol = new_sums(g, 0)
-            wc, ws = codes[h]
-            ptf = split.tile([P, 4, NA * NB], F32, name="ptf", tag="ptf")
-            tiles1[h] = ptf
+            if rnd == 0:
+                wc, ws = codes[h]
+                ptf = priors1.tile([P, 4, NA * NB], F32, name="ptf", tag="ptf")
+                tiles1[h] = ptf
+            else:
+                ptf = tiles1[h]
+                et = state[g][2]
+                pb_ps = psum.tile([P, NA, NB], F32, name="pb_ps", tag="pb")
+                for a in range(NA):
+                    t = l * NA + a
+                    nc.tensor.transpose(pb_ps[:, a, :], et[:, t:t + 1].to_broadcast([P, P]), ident_f[:])
             for c in range(4):
-                cs = slice(c * P, (c + 1) * P)
-                pt_ps = psum.tile([P, NA * NB], F32, name="pt_ps", tag="big", bufs=2)
-                mx(pt_ps[:], wc[:, cs], ws[:, cs], xc[:], xs[:])
+                if rnd == 0:
+                    cs = slice(c * P, (c + 1) * P)
+                    bank = psum.tile([P, NA * NB], F32, name="pt_ps", tag="big")
+                    mx(bank[:], wc[:, cs], ws[:, cs], xc[:], xs[:])
+                else:
+                    bank = work1.tile([P, NA * NB], F32, name="prod", tag="prod", bufs=6)
+                    nc.vector.tensor_tensor(out=bank[:], in0=pb_ps[:].rearrange("p a b -> p (a b)"), in1=ptf[:, c, :], op=ALU.mult)
                 for a in range(NA):
                     bs = slice(a * NB, (a + 1) * NB)
                     col = (l * NA + a) * 4 + c
-                    nc.scalar.activation(out=ptf[:, c, bs], in_=pt_ps[:, bs], func=ACT.Copy, accum_out=scol[:, col:col + 1])
-
-        def weighted_sums(g, l, rnd):
-            scol = new_sums(g, rnd)
-            et = state[g][2]
-            ptf = tiles1[g * HG + l]
-            pb_ps = psum.tile([P, NA, NB], F32, name="pb_ps", tag="pb", bufs=2)
-            for a in range(NA):
-                t = l * NA + a
-                nc.tensor.transpose(pb_ps[:, a, :], et[:, t:t + 1].to_broadcast([P, P]), ident_f[:])
-            for c in range(4):
-                prod = work1.tile([P, NA * NB], F32, name="prod", tag="prod", bufs=6)
-                nc.vector.tensor_tensor(out=prod[:], in0=pb_ps[:].rearrange("p a b -> p (a b)"), in1=ptf[:, c, :], op=ALU.mult)
-                for a in range(NA):
-                    col = (l * NA + a) * 4 + c
-                    waste_s = work1.tile([P, NB], BF16, name="waste_s", tag="waste_s")
-                    nc.scalar.activation(out=waste_s[:], in_=prod[:, a * NB:(a + 1) * NB], func=ACT.Copy, accum_out=scol[:, col:col + 1])
+                    if rnd == 0:
+                        kept = ptf[:, c, bs]
+                    else:
+                        waste = work1.tile([P, NB], BF16, name="waste", tag="waste")
+                        kept = waste[:]
+                    nc.scalar.activation(out=kept, in_=bank[:, bs], func=ACT.Copy, accum_out=scol[:, col:col + 1])
 
         def scale(g, l, rnd):
             scol = sums[(g, rnd)]
@@ -291,200 +234,183 @@ def tile_capsulelayer_kernel(tc, x, route_weights1, route_weights, out):
                 t = l * NA + a
                 bs = slice(a * NB, (a + 1) * NB)
                 scaled = work1.tile([P, 4, NB], F32, name="scaled", tag="scaled", bufs=12)
-                held[("scaled", g, l, a)] = scaled
+                scaleds[(g, l, a)] = scaled
                 for c in range(4):
                     sc = scol[:, t * 4 + c:t * 4 + c + 1]
-                    if SCALERS[(rnd * NT + t) % len(SCALERS)] == "V":
-                        nc.vector.tensor_scalar(out=scaled[:, c, :], in0=ptf[:, c, bs], scalar1=sc, scalar2=None, op0=ALU.mult)
-                    else:
+                    if by_scalar(t):
                         nc.scalar.activation(out=scaled[:, c, :], in_=ptf[:, c, bs], func=ACT.Copy, scale=sc)
+                    else:
+                        nc.vector.tensor_scalar(out=scaled[:, c, :], in0=ptf[:, c, bs], scalar1=sc, scalar2=None, op0=ALU.mult)
 
-        def fold(g, l):
-            fold_ps = psum.tile([P, NA, P], F32, name="fold_ps", tag="fold", bufs=2)
-            held[("fold", g, l)] = fold_ps
+        def fold(g, l, rnd):
+            fold_ps = psum.tile([P, NA, P], F32, name="fold_ps", tag="fold")
+            folds[(g, l)] = fold_ps
             for a in range(NA):
-                scaled = held[("scaled", g, l, a)]
                 for c in range(4):
-                    nc.tensor.matmul(fold_ps[:, a, :], lhsT=scaled[:, c, :], rhs=ident_f[:], is_transpose=True, start=(c == 0), stop=(c == 3))
+                    nc.tensor.matmul(fold_ps[:, a, :], lhsT=scaleds[(g, l, a)][:, c, :], rhs=ident_f[:], is_transpose=True, start=(c == 0), stop=(c == 3))
 
         def agreement(g, l, rnd):
             ucol = ucols[(2 * g + rnd) % len(ucols)]
-            nc.vector.tensor_reduce(out=ucol[:, l * NA:(l + 1) * NA], in_=held[("fold", g, l)][:], axis=AX.X, op=ALU.add)
+            nc.vector.tensor_reduce(out=ucol[:, l * NA:(l + 1) * NA], in_=folds[(g, l)][:], axis=AX.X, op=ALU.add)
 
-        def squash_steps(g, rnd):
-            key = (g, rnd)
+        def chain_of(g, rnd):
+            scol = sums[(g, rnd)]
             sqc = sqcs[(3 * g + rnd) % len(sqcs)]
-
-            def step1():
-                sq = work1.tile([P, NT, 4], F32, name="sq1", tag="sq1", bufs=3)
-                held[("sq", key)] = sq
-                nc.scalar.activation(out=sq[:].rearrange("p t f -> p (t f)"), in_=sums[key][:], func=ACT.Square)
-
-            def step2():
-                nc.vector.tensor_reduce(out=sqc[:, 0:NT], in_=held[("sq", key)][:], axis=AX.X, op=ALU.add)
-                n_ps = psum.tile([P, 2], F32, name="n_ps1", tag="t", bufs=2)
-                held[("n", key)] = n_ps
-                nc.tensor.matmul(n_ps[:], lhsT=sqc[:], rhs=ones_f[:], start=True, stop=True)
-
-            def step3():
-                z = z_one if rnd == 0 else state[g][1]
-                n_sb = work1.tile([P, 1], F32, name="n_sb", tag="n_sb", bufs=6)
-                nc.vector.tensor_copy(out=n_sb[:], in_=held[("n", key)][:, 0:1])
-                rt = work1.tile([P, 1], F32, name="rt", tag="rt", bufs=6)
-                held[("rt", key)] = rt
-                nc.gpsimd.tensor_tensor(out=rt[:], in0=n_sb[:], in1=half[:], op=ALU.pow)
-                den = work1.tile([P, 1], F32, name="den", tag="den", bufs=6)
-                nc.vector.tensor_scalar(out=den[:], in0=z[:], scalar1=z[:, 0:1], scalar2=n_sb[:, 0:1], op0=ALU.mult, op1=ALU.add)
-                rden = work1.tile([P, 1], F32, name="rden", tag="rden", bufs=6)
-                held[("rden", key)] = rden
-                nc.vector.reciprocal(out=rden[:], in_=den[:])
-
-            def step4():
-                f = work1.tile([P, 1], F32, name="f", tag="f", bufs=6)
-                factor[key] = f
-                nc.vector.tensor_tensor(out=f[:], in0=held[("rt", key)][:], in1=held[("rden", key)][:], op=ALU.mult)
-
-            return [step1, step2, step3, step4]
-
-        def softmax_steps(g, rnd):
-            key = (g, rnd)
-            ucol = ucols[(2 * g + rnd) % len(ucols)]
-
-            def step1():
-                ut_ps = psum.tile([P, P], F32, name="ut_ps", tag="t", bufs=2)
-                held[("ut", key)] = ut_ps
-                nc.tensor.transpose(ut_ps[:], ucol[:], ident_f[:])
-
-            def step2():
-                lt = lt_zero if rnd == 0 else state[g][0]
+            f = work1.tile([P, 1], F32, name="f", tag="f", bufs=8)
+            z_old = z_one if rnd == 0 else state[g][1]
+            steps = squash_steps(work1, scol[:], lambda sq: sq.rearrange("p (t c) -> p t c", c=4), sqc, sqc[:, 0:NT], z_old, f)
+            if rnd < 2:
+                lt_old = lt_zero if rnd == 0 else state[g][0]
                 lt_new = carry.tile([P, P], F32, name="lt1", tag="lt1")
-                held[("lt", key)] = lt_new
-                nc.vector.scalar_tensor_tensor(out=lt_new[:], in0=held[("ut", key)][:], scalar=factor[key][:, 0:1], in1=lt[:], op0=ALU.mult, op1=ALU.add)
-                negmax = work1.tile([P, 1], F32, name="negmax", tag="negmax", bufs=6)
-                held[("negmax", key)] = negmax
-                nc.vector.tensor_reduce(out=negmax[:], in_=lt_new[:], axis=AX.X, op=ALU.max, negate=True)
-
-            def step3():
-                e_sb = work1.tile([P, P], F32, name="e_sb", tag="e_sb", bufs=3)
                 z = carry.tile([P, 1], F32, name="z1", tag="z1")
-                held[("z", key)] = z
-                nc.scalar.activation(out=e_sb[:], in_=held[("lt", key)][:], func=ACT.Exp, bias=held[("negmax", key)][:, 0:1], scale=1.0, accum_out=z[:])
-                et_ps = psum.tile([P, P], F32, name="et_ps", tag="t", bufs=2)
-                held[("et", key)] = et_ps
-                nc.tensor.transpose(et_ps[:], e_sb[:], ident_f[:])
-
-            def step4():
                 et = carry.tile([P, NT], F32, name="et1", tag="et1")
-                nc.vector.tensor_copy(out=et[:], in_=held[("et", key)][:, 0:NT])
-                state[g] = (held[("lt", key)], held[("z", key)], et)
-                done[key] = True
 
-            return [step1, step2, step3, step4]
+                def take_weights(et_ps):
+                    nc.vector.tensor_copy(out=et[:], in_=et_ps[:, 0:NT])
+                    state[g] = (lt_new, z, et)
 
-        def finish_steps(g):
-            def step1():
-                fb_ps = psum.tile([P, P], F32, name="fb_ps1", tag="t", bufs=2)
-                held[("fb", g)] = fb_ps
-                nc.tensor.transpose(fb_ps[:], factor[(g, 2)][:, 0:1].to_broadcast([P, P]), ident_f[:])
+                return steps + softmax_steps(work1, ucols[(2 * g + rnd) % len(ucols)], f, lt_old, lt_new, z, take_weights)
+            got = {}
 
-            def step2():
+            def spread():
+                fb_ps = psum.tile([P, P], F32, name="fb_ps", tag="t")
+                got["fb"] = fb_ps
+                nc.tensor.transpose(fb_ps[:], f[:, 0:1].to_broadcast([P, P]), ident_f[:])
+
+            def squash():
                 nc.vector.tensor_tensor(
                     out=og[:].rearrange("p (a h) c -> p h a c", a=NA)[:, g * HG:(g + 1) * HG],
-                    in0=sums[(g, 2)][:].rearrange("p (l a f) -> p l a f", l=HG, a=NA),
-                    in1=held[("fb", g)][:, 0:NT].rearrange("p (l a) -> p l a", a=NA).unsqueeze(3).to_broadcast([P, HG, NA, 4]),
+                    in0=scol[:].rearrange("p (l a c) -> p l a c", l=HG, a=NA),
+                    in1=got["fb"][:, 0:NT].rearrange("p (l a) -> p l a", a=NA).unsqueeze(3).to_broadcast([P, HG, NA, 4]),
                     op=ALU.mult)
-                done[(g, 2)] = True
 
-            return [step1, step2]
-
-        n_groups = NH // HG
-        items = []
-        for k in range(n_groups + 2):
-            for rnd in range(3):
-                if 0 <= k - rnd < n_groups:
-                    items.extend([(k - rnd, l, rnd) for l in range(HG)])
+            return steps + [spread, squash]
 
         with tc.tile_pool(name="work1", bufs=2) as work1, tc.manual_schedule():
-            placed = {}
-            nxt = 0
-            tick = 0
-            while len(done) < 3 * n_groups:
-                if tick % PREP_EVERY == 0:
-                    for stage_no in (2, 1, 0):
-                        prep(stage_no)
-                if nxt < len(items):
-                    g, l, rnd = items[nxt]
-                    if rnd == 0 or (g, rnd - 1) in done:
-                        if rnd == 0:
-                            first_sums(g, l)
-                        else:
-                            weighted_sums(g, l, rnd)
-                        placed[tick] = items[nxt]
-                        nxt += 1
-                        if l == HG - 1:
-                            steps = squash_steps(g, rnd)
-                            for i in range(len(steps)):
-                                at(tick + 2 + i, steps[i])
-                            if rnd == 2:
-                                steps = finish_steps(g)
-                                for i in range(len(steps)):
-                                    at(tick + 6 + i, steps[i])
-                            else:
-                                steps = softmax_steps(g, rnd)
-                                for i in range(len(steps)):
-                                    at(tick + 6 + i, steps[i])
+            ahead = HG + 2
+            for n in range(ahead):
+                weights_step(n)
+            for i in range((NG + 2) * TURNS + 10):
+                if i % 2 == 0:
+                    weights_step(ahead + i // 2)
+                if turn(i):
+                    sums_of(*turn(i))
                 for lag, stage_fn in ((2, scale), (3, fold), (4, agreement)):
-                    if tick - lag in placed and placed[tick - lag][2] < 2:
-                        g, l, rnd = placed[tick - lag]
-                        if lag == 3:
-                            fold(g, l)
-                        else:
-                            stage_fn(g, l, rnd)
-                for step in later.get(tick, []):
-                    step()
-                tick += 1
-            while prepared[2] < len(jobs):
-                for stage_no in range(3):
-                    prep(stage_no)
+                    if turn(i - lag) and turn(i - lag)[2] < 2:
+                        stage_fn(*turn(i - lag))
+                for j in range(7, -1, -1):
+                    last = turn(i - 2 - j)
+                    if last and last[1] == HG - 1:
+                        g, l, rnd = last
+                        if j == 0:
+                            chains[(g, rnd)] = chain_of(g, rnd)
+                        if j < len(chains[(g, rnd)]):
+                            chains[(g, rnd)][j]()
 
-        small = ctx.enter_context(tc.tile_pool(name="small", bufs=2))
         nc.vector.quantize_mx(out=oc[:].bitcast(FP8X4), scales=os_[:], in_=og[:].rearrange("p w t -> p (w t)"))
-        tiles2 = {}
-        for q in range(NC2 // 8):
-            qn = [split.tile([P, 8, NE], BF16, name="qn%d" % i, tag="ptf") for i in range(3)]
-            qt = [split.tile([P, 8, NE], BF16, name="qt%d" % i, tag="ptf") for i in range(3)]
-            tiles2[q] = (qn, qt)
-            for i in range(8):
-                c = 8 * q + i
-                q_ps = psum.tile([P, NE], F32, name="q_ps", tag="big", bufs=2)
-                mx(q_ps[:], oc[:], os_[:], w2c[:, c, :], w2s[:, c, :])
-                split_bank(q_ps[:], [w[:, i, :] for w in qn])
-                qt_ps = psum.tile([P, 4, P], F32, name="qt_ps", tag="big", bufs=2)
-                for fc in range(4):
-                    cs = slice(fc * P, (fc + 1) * P)
-                    mx(qt_ps[:, fc, :], w2c[:, c, cs], w2s[:, c, cs], oc[:], os_[:])
-                split_bank(qt_ps[:].rearrange("p k j -> p (k j)"), [w[:, i, :] for w in qt])
+        small = ctx.enter_context(tc.tile_pool(name="small", bufs=2))
+        ucol2 = ucols[0]
+        sqc2 = sqcs[0]
 
-        def stat2(t, fc, part):
-            return tiles2[t // 8][0][part][:, t % 8, fc * P:(fc + 1) * P]
+        def segments(ap):
+            return ap.rearrange("p k (a h) -> p k a h", a=NA)
 
-        def stat2_t(t, fc, part):
-            return tiles2[t // 8][1][part][:, t % 8, fc * P:(fc + 1) * P]
+        def own(tile_ap):
+            return tile_ap.rearrange("p (n c) -> p c n", c=32)[:, 0:NC2, :]
 
-        def finish2(scol, fb_ps):
+        def bank_features(c):
+            qt_ps = psum.tile([P, 4, P], F32, name="qt_ps", tag="big")
+            for fc in range(4):
+                cs = slice(fc * P, (fc + 1) * P)
+                mx(qt_ps[:, fc, :], w2c[:, c, cs], w2s[:, c, cs], oc[:], os_[:])
+            return qt_ps
+
+        def first_sums2(scol):
+            for c in range(NC2):
+                nc.vector.tensor_reduce(out=scol[:, c * 4:(c + 1) * 4, :], in_=segments(bank_features(c)[:]), axis=AX.X, op=ALU.add)
+
+        def weighted_sums2(scol, e2):
+            ys = {}
+            turned = {}
+            for i in range(NC2 + 4):
+                if i < NC2:
+                    q_ps = psum.tile([P, NE], F32, name="q_ps", tag="big")
+                    mx(q_ps[:], oc[:], os_[:], w2c[:, i, :], w2s[:, i, :])
+                    y = small.tile([P, NE], F32, name="y", tag="y", bufs=4)
+                    ys[i] = y
+                    nc.scalar.activation(out=y[:], in_=q_ps[:], func=ACT.Copy, scale=e2[:, i:i + 1])
+                if 0 <= i - 2 < NC2:
+                    tr_ps = psum.tile([P, 4, P], F32, name="tr_ps", tag="pb")
+                    turned[i - 2] = tr_ps
+                    for fc in range(4):
+                        nc.tensor.transpose(tr_ps[:, fc, :], ys[i - 2][:, fc * P:(fc + 1) * P], ident_f[:])
+                if 0 <= i - 4 < NC2:
+                    c = i - 4
+                    nc.vector.tensor_reduce(out=scol[:, c * 4:(c + 1) * 4, :], in_=segments(turned[c][:]), axis=AX.X, op=ALU.add)
+
+        def agreement2(scol, u2, steps):
+            scaled2s = {}
+            fold2s = {}
+            for i in range(NC2 + 4):
+                if i % 2 == 1 and i // 2 < len(steps):
+                    steps[i // 2]()
+                if i < NC2:
+                    bank = bank_features(i)
+                    scaled = small.tile([P, 4, P], F32, name="scaled2", tag="scaled2", bufs=4)
+                    scaled2s[i] = scaled
+                    nc.vector.tensor_tensor(out=segments(scaled[:]), in0=segments(bank[:]),
+                                            in1=scol[:, i * 4:(i + 1) * 4, :].unsqueeze(3).to_broadcast([P, 4, NA, NH]), op=ALU.mult)
+                if 0 <= i - 2 < NC2:
+                    c = i - 2
+                    if c % 4 == 0:
+                        fold_ps = psum.tile([P, 4, P], F32, name="fold2_ps", tag="fold")
+                        fold2s[c // 4] = fold_ps
+                    for fc in range(4):
+                        nc.tensor.matmul(fold2s[c // 4][:, c % 4, :], lhsT=scaled2s[c][:, fc, :], rhs=ident_f[:], is_transpose=True, start=(fc == 0), stop=(fc == 3))
+                if 0 <= i - 4 < NC2 and (i - 4) % 4 == 3:
+                    q = (i - 4) // 4
+                    nc.vector.tensor_reduce(out=u2[:, q * 4:(q + 1) * 4], in_=fold2s[q][:], axis=AX.X, op=ALU.add)
+
+        with tc.manual_schedule():
+            z = z_blk
+            lt = lt_blk
+            e2 = None
+            for rnd in range(3):
+                scol = small.tile([P, NC2 * 4, NA], F32, name="scol", tag="scol")
+                if rnd == 0:
+                    first_sums2(scol)
+                else:
+                    weighted_sums2(scol, e2)
+                f = small.tile([P, 1], F32, name="f2", tag="f2")
+                steps = squash_steps(small, scol[:], lambda sq: sq.rearrange("p (t k) n -> p t n k", k=4), sqc2, own(sqc2[:]), z, f)
+                if rnd == 2:
+                    for step in steps:
+                        step()
+                    break
+                u2 = small.tile([P, NC2], F32, name="u2", tag="u2")
+                agreement2(scol, u2, steps)
+                nc.vector.tensor_copy(out=own(ucol2[:]), in_=u2[:].unsqueeze(2).to_broadcast([P, NC2, NA]))
+                lt_new = small.tile([P, P], F32, name="lt_new", tag="lt")
+                z = small.tile([P, 1], F32, name="z", tag="z")
+                e2 = small.tile([P, NC2], F32, name="e2", tag="e2")
+
+                def take_weights2(et_ps):
+                    nc.vector.tensor_reduce(out=e2[:], in_=own(et_ps[:]), axis=AX.X, op=ALU.add)
+
+                for step in softmax_steps(small, ucol2, f, lt, lt_new, z, take_weights2):
+                    step()
+                lt = lt_new
+
+            fb_ps = psum.tile([P, P], F32, name="fb2_ps", tag="t")
+            nc.tensor.transpose(fb_ps[:], f[:, 0:1].to_broadcast([P, P]), ident_f[:])
             o_sb = small.tile([P, NC2, NA, 4], F32, name="o_sb", tag="o_sb", bufs=1)
-            nc.vector.tensor_tensor(
-                out=o_sb[:],
-                in0=scol[:].rearrange("p (t f) n -> p t n f", f=4),
-                in1=fb_ps[:].rearrange("p (n c) -> p c n", c=32)[:, 0:NC2, :].unsqueeze(3).to_broadcast([P, NC2, NA, 4]),
-                op=ALU.mult)
-            o_flat = o_sb[:].rearrange("p t n f -> p (t n f)")
+            nc.vector.tensor_tensor(out=o_sb[:], in0=scol[:].rearrange("p (t k) n -> p t n k", k=4),
+                                    in1=own(fb_ps[:]).unsqueeze(3).to_broadcast([P, NC2, NA, 4]), op=ALU.mult)
+            o_flat = o_sb[:].rearrange("p t n k -> p (t n k)")
             out_rows = out.rearrange("c a (k f) -> (c a k) f", f=P)
             for i in range(2):
-                ot_ps = psum.tile([P, P], F32, name="ot_ps", tag="t", bufs=2)
+                ot_ps = psum.tile([P, P], F32, name="ot_ps", tag="t")
                 nc.tensor.transpose(ot_ps[:], o_flat[:, i * P:(i + 1) * P], ident_f[:])
                 res = small.tile([P, P], F32, name="res", tag="res")
                 nc.scalar.copy(out=res[:], in_=ot_ps[:])
                 nc.sync.dma_start(out=out_rows[i * P:(i + 1) * P, :], in_=res[:])
-
-        routing(NC2, NA, stat2, stat2_t, ev_blk, z_blk, lt_blk, 0, finish2)

@@ -16,23 +16,17 @@ P = 128
 NA, NB, ND, NE, NH, NC2 = 4, 128, 512, 512, 32, 16
 FLOPS = 2 * (NA * NB * ND * NE * NH + NA * NH * NE * NE * NC2)
 
+NJ = 4
 HG = 4
-NT = HG * NA
 NG = NH // HG
-TURNS = 3 * HG
-HELD = 13
-SCALAR_SCALES = 4
-ON_VECTOR = 8
+HELD = 16
+ROUND1, ROUND2 = 27, 57
 
 
 def tile_capsulelayer_kernel(tc, x, route_weights1, route_weights, out):
     nc = tc.nc
     with ExitStack() as ctx:
         const = ctx.enter_context(tc.tile_pool(name="const", bufs=1))
-        stage = ctx.enter_context(tc.tile_pool(name="stage", bufs=2))
-        priors1 = ctx.enter_context(tc.tile_pool(name="priors1", bufs=HELD))
-        carry = ctx.enter_context(tc.tile_pool(name="carry", bufs=8))
-        psum = ctx.enter_context(tc.psum_pool(name="psum", bufs=2))
 
         ident_f = const.tile([P, P], F32, name="ident_f")
         make_identity(nc, ident_f[:])
@@ -42,26 +36,20 @@ def tile_capsulelayer_kernel(tc, x, route_weights1, route_weights, out):
         nc.vector.memset(ones_f[:], 1.0)
         half = const.tile([P, 1], F32, name="half")
         nc.vector.memset(half[:], 0.5)
-        z_one = const.tile([P, 1], F32, name="z_one")
-        nc.vector.memset(z_one[:], float(NB))
-        lt_zero = const.tile([P, P], F32, name="lt_zero")
-        nc.vector.memset(lt_zero[:], 0.0)
+        blk_ones = const.tile([P, P], F32, name="blk_ones")
+        nc.vector.memset(blk_ones[:], 0.0)
         lt_blk = const.tile([P, P], F32, name="lt_blk")
         nc.vector.memset(lt_blk[:], -1.0e30)
         for a in range(NA):
             blk = slice(32 * a, 32 * a + 32)
             nc.vector.memset(lt_blk[blk, blk], 0.0)
+            nc.vector.memset(blk_ones[blk, blk], 1.0)
         z_blk = const.tile([P, 1], F32, name="z_blk")
         nc.vector.memset(z_blk[:], float(NH))
-        ucols = []
-        sqcs = []
-        for i in range(4):
-            ucol = const.tile([P, P], F32, name="ucol%d" % i)
-            nc.vector.memset(ucol[:], 0.0)
-            ucols.append(ucol)
-            sqc = const.tile([P, P], F32, name="sqc%d" % i)
-            nc.vector.memset(sqc[:], 0.0)
-            sqcs.append(sqc)
+        ucol2 = const.tile([P, P], F32, name="ucol2")
+        nc.vector.memset(ucol2[:], 0.0)
+        sqc2 = const.tile([P, P], F32, name="sqc2")
+        nc.vector.memset(sqc2[:], 0.0)
 
         xc = const.tile([P, NA * NB], U32, name="xc", align_bytes=64)
         xs = const.tile([P, NA * NB], U8, name="xs", align_bytes=64)
@@ -71,9 +59,285 @@ def tile_capsulelayer_kernel(tc, x, route_weights1, route_weights, out):
         oc = const.tile([P, NA * NH], U32, name="oc", align_bytes=64)
         os_ = const.tile([P, NA * NH], U8, name="os_", align_bytes=64)
 
-        def mx(out_ps, l_codes, l_scales, r_codes, r_scales):
+        def mx(out_ps, l_codes, l_scales, r_codes, r_scales, start=True, stop=True):
             nc.tensor.matmul_mx(out=out_ps, lhsT=l_codes.bitcast(FP8X4), lhsT_scale=l_scales,
-                                rhs=r_codes.bitcast(FP8X4), rhs_scale=r_scales, start=True, stop=True)
+                                rhs=r_codes.bitcast(FP8X4), rhs_scale=r_scales, start=start, stop=stop)
+
+        with ExitStack() as first:
+            stage = first.enter_context(tc.tile_pool(name="stage", bufs=2))
+            priors = first.enter_context(tc.tile_pool(name="priors", bufs=HELD))
+            work = first.enter_context(tc.tile_pool(name="work", bufs=2))
+            psum = first.enter_context(tc.psum_pool(name="psum1", bufs=2))
+
+            lt0 = work.tile([P, P], F32, name="lt0", bufs=1, align_bytes=64)
+            nc.vector.memset(lt0[:], 0.0)
+            e0 = work.tile([P, P], F32, name="e0", bufs=1, align_bytes=64)
+            nc.vector.memset(e0[:], 1.0)
+            z0 = work.tile([P, 1], F32, name="z0", bufs=1)
+            nc.vector.memset(z0[:], float(NB))
+            us = []
+            for i in range(2):
+                u = work.tile([P, P], F32, name="u%d" % i, bufs=1, align_bytes=64)
+                nc.vector.memset(u[:], 0.0)
+                us.append(u)
+            s2 = work.tile([P, NA * NH, 4], F32, name="s2", bufs=1)
+            sqc = work.tile([P, NA * NH], F32, name="sqc", bufs=1)
+            state = {0: (lt0, e0, z0, None)}
+
+            x_sb = stage.tile([P, NA, ND], BF16, name="x_sb", tag="raw", bufs=3)
+            nc.sync.dma_start(out=x_sb[:], in_=x.rearrange("a b d -> b a d"))
+            xg = stage.tile([P, NA * NB, 4], BF16, name="xg", tag="grouped", align_bytes=64)
+            for a in range(NA):
+                xt_ps = psum.tile([P, 4, NB], BF16, name="xt_ps", tag="big", bufs=3)
+                for t in range(4):
+                    nc.tensor.transpose(xt_ps[:, t, :], x_sb[:, a, :].rearrange("b (p t) -> b t p", t=4)[:, t, :], ident_b[:])
+                nc.vector.tensor_copy(out=xg[:].rearrange("p (j a q) t -> p a j q t", j=NJ, a=NA)[:, a],
+                                      in_=xt_ps[:].rearrange("p t (j q) -> p j q t", j=NJ))
+            nc.vector.quantize_mx(out=xc[:].bitcast(FP8X4), scales=xs[:], in_=xg[:].rearrange("p w t -> p (w t)"))
+
+            raws = {}
+            groupeds = {}
+            codes = {}
+            tiles = {}
+            banks = {}
+            ys = {}
+            sbs = {}
+            scols = {}
+
+            def load(kind, m):
+                raw = stage.tile([P, 4, NE], BF16, name="raw", tag="raw", bufs=3)
+                raws[(kind, m)] = raw
+                rows = route_weights1[m].rearrange("(p t) e -> p t e", t=4) if kind == 1 else route_weights[m].rearrange("(t p) f -> p t f", p=P)
+                nc.sync.dma_start(out=raw[:], in_=rows)
+
+            def regroup(kind, m):
+                grouped = stage.tile([P, NE, 4], BF16, name="grouped", tag="grouped", align_bytes=64)
+                groupeds[(kind, m)] = grouped
+                raw = raws[(kind, m)]
+                if kind == 1 and m < 2:
+                    nc.vector.tensor_copy(out=grouped[:].rearrange("p (c i) t -> p c t i", i=4), in_=raw[:].rearrange("p t (c i) -> p c t i", i=4))
+                else:
+                    nc.gpsimd.tensor_scalar(out=grouped[:], in0=raw[:].rearrange("p t c -> p c t"), scalar1=1.0, scalar2=0.0, op0=ALU.mult, op1=ALU.add)
+
+            def quantize(kind, m):
+                if kind == 1:
+                    wc = stage.tile([P, NE], U32, name="wc", tag="wc", align_bytes=64)
+                    ws = stage.tile([P, NE], U8, name="ws", tag="ws", align_bytes=64)
+                    codes[m] = (wc, ws)
+                    cw, sw = wc[:], ws[:]
+                else:
+                    cw, sw = w2c[:, m, :], w2s[:, m, :]
+                nc.vector.quantize_mx(out=cw.bitcast(FP8X4), scales=sw, in_=groupeds[(kind, m)][:].rearrange("p w t -> p (w t)"))
+
+            def x_block(j):
+                return xc[:, j * P:(j + 1) * P], xs[:, j * P:(j + 1) * P]
+
+            def total_mx(h):
+                q_ps = psum.tile([P, NE], F32, name="q_ps", tag="fold", bufs=3)
+                banks[("q", h)] = q_ps
+                wc, ws = codes[h]
+                for j in range(NJ):
+                    mx(q_ps[:], *x_block(j), wc[:], ws[:], start=(j == 0), stop=(j == NJ - 1))
+
+            def total_copy(h):
+                q_sb = work.tile([P, NE], F32, name="q_sb", tag="q_sb")
+                ys[("q", h)] = q_sb
+                nc.scalar.copy(out=q_sb[:], in_=banks[("q", h)][:])
+
+            def total_spread(h):
+                sb_ps = psum.tile([P, NE], F32, name="sb_ps", tag="sb")
+                sbs[(h, 0)] = sb_ps
+                nc.tensor.matmul(sb_ps[:], lhsT=blk_ones[:], rhs=ys[("q", h)][:], start=True, stop=True)
+
+            def prior_mx(h, j):
+                p_ps = psum.tile([P, NE], F32, name="p_ps", tag="big", bufs=3)
+                banks[("p", h, j)] = p_ps
+                wc, ws = codes[h]
+                mx(p_ps[:], *x_block(j), wc[:], ws[:])
+
+            def prior_copy(h, j):
+                if j == 0:
+                    pn = priors.tile([P, NJ, NE], F32, name="pn", tag="pn")
+                    tiles[h] = pn
+                nc.scalar.copy(out=tiles[h][:, j, :], in_=banks[("p", h, j)][:])
+
+            def weights_of(h, rnd, j):
+                m = h // HG + (1 if rnd == 1 else 3)
+                return state[m][3][:, j * 32 + h:j * 32 + h + 1]
+
+            def scale(h, rnd, j):
+                src = tiles[h][:, j, :]
+                if rnd == 1:
+                    y = work.tile([P, NE], F32, name="y", tag="y", bufs=6)
+                    dst = y[:]
+                else:
+                    dst = src
+                ys[(h, rnd, j)] = dst
+                if j == 0:
+                    nc.gpsimd.tensor_scalar(out=dst, in0=src, scalar1=weights_of(h, rnd, j), scalar2=0.0, op0=ALU.mult, op1=ALU.add)
+                else:
+                    nc.scalar.activation(out=dst, in_=src, func=ACT.Copy, scale=weights_of(h, rnd, j))
+
+            def fold(h, rnd):
+                f_ps = psum.tile([P, 4, P], F32, name="f_ps", tag="fold", bufs=3)
+                banks[("f", h, rnd)] = f_ps
+                for c in range(4):
+                    for j in range(NJ):
+                        nc.tensor.matmul(f_ps[:, c, :], lhsT=ys[(h, rnd, j)][:, c * P:(c + 1) * P], rhs=ident_f[:], is_transpose=True, start=(j == 0), stop=(j == NJ - 1))
+
+            def sums(h, rnd):
+                f_ps = banks[("f", h, rnd)]
+                if rnd == 1:
+                    scol = work.tile([P, 4, NA], F32, name="scol", tag="scol")
+                    scols[h] = scol
+                    dst = scol[:]
+                else:
+                    dst = s2[:].rearrange("p (a h) c -> p h c a", a=NA)[:, h]
+                nc.vector.tensor_reduce(out=dst, in_=f_ps[:].rearrange("p c (a q) -> p c a q", a=NA), axis=AX.X, op=ALU.add)
+
+            def repeat(h):
+                bc = work.tile([P, 4, NA, 32], F32, name="bc", tag="bc")
+                ys[("bc", h)] = bc
+                nc.scalar.copy(out=bc[:], in_=scols[h][:].unsqueeze(3).to_broadcast([P, 4, NA, 32]))
+
+            def spread(h):
+                sb_ps = psum.tile([P, NE], F32, name="sb_ps", tag="sb")
+                sbs[(h, 1)] = sb_ps
+                bc = ys[("bc", h)]
+                for c in range(4):
+                    nc.tensor.transpose(sb_ps[:, c * P:(c + 1) * P], bc[:, c].rearrange("p a q -> p (a q)"), ident_f[:])
+
+            def agree(h, rnd, j):
+                u = us[h // HG % 2]
+                waste = work.tile([P, NE], BF16, name="waste", tag="waste")
+                nc.vector.scalar_tensor_tensor(out=waste[:], in0=tiles[h][:, j, :], scalar=1.0, in1=sbs[(h, rnd)][:], op0=ALU.mult, op1=ALU.mult,
+                                               accum_out=u[:, j * 32 + h:j * 32 + h + 1])
+
+            small = {}
+
+            def softmax_step(m, k):
+                lt_old, e_old, z_old = state[m - 1][0], state[m - 1][1], state[m - 1][2]
+                u = us[(m - 1) % 2]
+                if k == 0:
+                    ut = work.tile([P, P], F32, name="ut", tag="ut", align_bytes=64)
+                    small["ut"] = ut
+                    nc.vector.transpose(ut[:], u[:])
+                    nc.gpsimd.memset(u[:], 0.0)
+                elif k == 1:
+                    n = work.tile([P, 1], F32, name="n", tag="n")
+                    small["n"] = n
+                    eu = work.tile([P, P], F32, name="eu", tag="eu")
+                    nc.vector.scalar_tensor_tensor(out=eu[:], in0=small["ut"][:], scalar=1.0, in1=e_old[:], op0=ALU.mult, op1=ALU.mult, accum_out=n[:])
+                elif k == 2:
+                    rt = work.tile([P, 1], F32, name="rt", tag="rt")
+                    small["rt"] = rt
+                    nc.gpsimd.tensor_tensor(out=rt[:], in0=small["n"][:], in1=half[:], op=ALU.pow)
+                    den = work.tile([P, 1], F32, name="den", tag="den")
+                    nc.vector.tensor_scalar(out=den[:], in0=z_old[:], scalar1=z_old[:, 0:1], scalar2=small["n"][:, 0:1], op0=ALU.mult, op1=ALU.add)
+                    rden = work.tile([P, 1], F32, name="rden", tag="rden")
+                    small["rden"] = rden
+                    nc.vector.reciprocal(out=rden[:], in_=den[:])
+                elif k == 4:
+                    f = work.tile([P, 1], F32, name="f", tag="f")
+                    nc.vector.tensor_tensor(out=f[:], in0=small["rt"][:], in1=small["rden"][:], op=ALU.mult)
+                    lt = work.tile([P, P], F32, name="lt", tag="lt")
+                    small["lt"] = lt
+                    nc.vector.scalar_tensor_tensor(out=lt[:], in0=small["ut"][:], scalar=f[:, 0:1], in1=lt_old[:], op0=ALU.mult, op1=ALU.add)
+                    negmax = work.tile([P, 1], F32, name="negmax", tag="negmax")
+                    small["negmax"] = negmax
+                    nc.vector.tensor_reduce(out=negmax[:], in_=lt[:], axis=AX.X, op=ALU.max, negate=True)
+                elif k == 5:
+                    e = work.tile([P, P], F32, name="e", tag="e", align_bytes=64)
+                    small["e"] = e
+                    z = work.tile([P, 1], F32, name="z", tag="z")
+                    small["z"] = z
+                    nc.scalar.activation(out=e[:], in_=small["lt"][:], func=ACT.Exp, bias=small["negmax"][:, 0:1], scale=1.0, accum_out=z[:])
+                elif k == 6:
+                    et = work.tile([P, P], F32, name="et", tag="et", bufs=4, align_bytes=64)
+                    nc.vector.transpose(et[:], small["e"][:])
+                    state[m] = (small["lt"], small["e"], small["z"], et)
+
+            def squares(g):
+                of_group = s2[:].rearrange("p (a h) c -> p a h c", a=NA)[:, :, g * HG:(g + 1) * HG, :]
+                sq = work.tile([P, NA, HG, 4], F32, name="sq", tag="sq")
+                nc.scalar.activation(out=sq[:], in_=of_group, func=ACT.Square)
+                nc.vector.tensor_reduce(out=sqc[:].rearrange("p (a h) -> p a h", a=NA)[:, :, g * HG:(g + 1) * HG], in_=sq[:], axis=AX.X, op=ALU.add)
+
+            def at(tick, offset):
+                h, r = divmod(tick - offset, 4)
+                return h if r == 0 and 0 <= h < NH else None
+
+            with tc.manual_schedule():
+                w2_load, w2_first = 24, 24 * 4
+                load(1, 0)
+                load(1, 1)
+                for tick in range(-9, 4 * (NH - 1) + ROUND2 + 8):
+                    def run(fn, offset, *more):
+                        h = at(tick, offset)
+                        if h is not None:
+                            fn(h, *more)
+
+                    def run2(fn, offset):
+                        m, r = divmod(tick - w2_first - offset, 4)
+                        if r == 0 and 0 <= m < NC2:
+                            fn(2, m)
+
+                    h = at(tick, -9)
+                    if h is not None and h >= 2:
+                        load(1, h)
+                    run2(load, -6)
+                    run(sums, ROUND1 + 5, 1)
+                    run(sums, ROUND2 + 5, 2)
+                    m, k = divmod(tick - 2, 16)
+                    if 1 <= m <= NG + 2 and k <= 6:
+                        softmax_step(m, k)
+                    run(total_copy, 1)
+                    run(total_spread, 2)
+                    run(spread, ROUND1 + 6)
+                    run(total_mx, 0)
+                    for j in range(NJ):
+                        run(prior_mx, j, j)
+                    run(fold, ROUND1 + 4, 1)
+                    run(fold, ROUND2 + 4, 2)
+                    for j in range(NJ):
+                        run(scale, ROUND1 + j, 1, j)
+                        run(scale, ROUND2 + j, 2, j)
+                    for j in range(NJ):
+                        run(prior_copy, j, j)
+                    run(repeat, ROUND1 + 5)
+                    for j in range(NJ):
+                        run(agree, 4 + j // 2, 0, j)
+                        run(agree, ROUND1 + 7 + j // 2, 1, j)
+                    h = at(tick, -5)
+                    if h is not None:
+                        regroup(1, h)
+                    run2(regroup, -3)
+                    h = at(tick, -1)
+                    if h is not None:
+                        quantize(1, h)
+                    run2(quantize, 1)
+                    h = at(tick, ROUND2 + 6)
+                    if h is not None and h % HG == HG - 1:
+                        squares(h // HG)
+
+                z = state[NG + 2][2]
+                n_ps = psum.tile([P, 2], F32, name="n_ps", tag="sb")
+                nc.tensor.matmul(n_ps[:], lhsT=sqc[:], rhs=ones_f[:], start=True, stop=True)
+                n = work.tile([P, 1], F32, name="n", tag="n")
+                nc.vector.tensor_copy(out=n[:], in_=n_ps[:, 0:1])
+                rt = work.tile([P, 1], F32, name="rt", tag="rt")
+                nc.gpsimd.tensor_tensor(out=rt[:], in0=n[:], in1=half[:], op=ALU.pow)
+                den = work.tile([P, 1], F32, name="den", tag="den")
+                nc.vector.tensor_scalar(out=den[:], in0=z[:], scalar1=z[:, 0:1], scalar2=n[:, 0:1], op0=ALU.mult, op1=ALU.add)
+                rden = work.tile([P, 1], F32, name="rden", tag="rden")
+                nc.vector.reciprocal(out=rden[:], in_=den[:])
+                f = work.tile([P, 1], F32, name="f", tag="f")
+                nc.vector.tensor_tensor(out=f[:], in0=rt[:], in1=rden[:], op=ALU.mult)
+                fb_ps = psum.tile([P, P], F32, name="fb_ps", tag="sb")
+                nc.tensor.transpose(fb_ps[:], f[:, 0:1].to_broadcast([P, P]), ident_f[:])
+                nc.vector.tensor_tensor(out=og[:], in0=s2[:], in1=fb_ps[:].unsqueeze(2).to_broadcast([P, NA * NH, 4]), op=ALU.mult)
+
+        psum = ctx.enter_context(tc.psum_pool(name="psum2", bufs=2))
 
         def squash_steps(pool, s_flat, by_problem, sqc, sqc_own, z, f):
             sq = pool.tile(list(s_flat.shape), F32, name="sq", tag="sq", bufs=4)
@@ -128,189 +392,8 @@ def tile_capsulelayer_kernel(tc, x, route_weights1, route_weights, out):
 
             return [step1, step2, step3, step4]
 
-        x_sb = stage.tile([P, NA, ND], BF16, name="x_sb", tag="raw")
-        nc.sync.dma_start(out=x_sb[:], in_=x.rearrange("a b d -> b a d"))
-        xg = stage.tile([P, NA * NB, 4], BF16, name="xg", tag="grouped", align_bytes=64)
-        for a in range(NA):
-            xt_ps = psum.tile([P, 4, NB], BF16, name="xt_ps", tag="t")
-            for t in range(4):
-                nc.tensor.transpose(xt_ps[:, t, :], x_sb[:, a, :].rearrange("b (p t) -> b t p", t=4)[:, t, :], ident_b[:])
-            nc.vector.tensor_copy(out=xg[:, a * NB:(a + 1) * NB, :], in_=xt_ps[:].rearrange("p t b -> p b t"))
-        nc.vector.quantize_mx(out=xc[:].bitcast(FP8X4), scales=xs[:], in_=xg[:].rearrange("p w t -> p (w t)"))
-
-        per_group = NC2 // NG
-        jobs = [("w1", h) for h in range(HG)]
-        for g in range(1, NG + 1):
-            jobs.extend([("w2", (g - 1) * per_group + i) for i in range(per_group)])
-            if g < NG:
-                jobs.extend([("w1", g * HG + l) for l in range(HG)])
-        raws = {}
-        groupeds = {}
-        codes = {}
-
-        def weights_step(n):
-            if 0 <= n < len(jobs):
-                kind, m = jobs[n]
-                raw = stage.tile([P, 4, NE], BF16, name="raw", tag="raw")
-                raws[n] = raw
-                rows = route_weights1[m].rearrange("(p t) e -> p t e", t=4) if kind == "w1" else route_weights[m].rearrange("(t p) f -> p t f", p=P)
-                nc.sync.dma_start(out=raw[:], in_=rows)
-            if 0 <= n - 1 < len(jobs):
-                grouped = stage.tile([P, NE, 4], BF16, name="grouped", tag="grouped", align_bytes=64)
-                groupeds[n - 1] = grouped
-                dst = grouped[:].rearrange("p (c i) t -> p c t i", i=4)
-                src = raws[n - 1][:].rearrange("p t (c i) -> p c t i", i=4)
-                if n - 1 < ON_VECTOR:
-                    nc.vector.tensor_copy(out=dst, in_=src)
-                else:
-                    nc.gpsimd.tensor_scalar(out=dst, in0=src, scalar1=1.0, scalar2=0.0, op0=ALU.mult, op1=ALU.add)
-            if 0 <= n - 2 < len(jobs):
-                kind, m = jobs[n - 2]
-                if kind == "w1":
-                    wc = stage.tile([P, NE], U32, name="wc", tag="wc", bufs=HG + 1, align_bytes=64)
-                    ws = stage.tile([P, NE], U8, name="ws", tag="ws", bufs=HG + 1, align_bytes=64)
-                    codes[m] = (wc, ws)
-                    cw, sw = wc[:], ws[:]
-                else:
-                    cw, sw = w2c[:, m, :], w2s[:, m, :]
-                nc.vector.quantize_mx(out=cw.bitcast(FP8X4), scales=sw, in_=groupeds[n - 2][:].rearrange("p w t -> p (w t)"))
-
-        tiles1 = {}
-        sums = {}
-        scaleds = {}
-        folds = {}
-        state = {}
-        factor = {}
-        chains = {}
-
-        def turn(i):
-            step_no, r = divmod(i, TURNS)
-            rnd, l = divmod(r, HG)
-            g = step_no - rnd
-            return (g, l, rnd) if i >= 0 and 0 <= g < NG else None
-
-        def by_scalar(t):
-            return t % SCALAR_SCALES == SCALAR_SCALES - 1
-
-        def sums_of(g, l, rnd):
-            if l == 0:
-                scol_new = carry.tile([P, NT * 4], F32, name="scol1", tag="scol1", bufs=10)
-                sums[(g, rnd)] = scol_new
-            scol = sums[(g, rnd)]
-            h = g * HG + l
-            if rnd == 0:
-                wc, ws = codes[h]
-                ptf = priors1.tile([P, 4, NA * NB], F32, name="ptf", tag="ptf")
-                tiles1[h] = ptf
-            else:
-                ptf = tiles1[h]
-                et = state[g][2]
-                pb_ps = psum.tile([P, NA, NB], F32, name="pb_ps", tag="pb")
-                for a in range(NA):
-                    t = l * NA + a
-                    nc.tensor.transpose(pb_ps[:, a, :], et[:, t:t + 1].to_broadcast([P, P]), ident_f[:])
-            for c in range(4):
-                if rnd == 0:
-                    cs = slice(c * P, (c + 1) * P)
-                    bank = psum.tile([P, NA * NB], F32, name="pt_ps", tag="big")
-                    mx(bank[:], wc[:, cs], ws[:, cs], xc[:], xs[:])
-                else:
-                    bank = work1.tile([P, NA * NB], F32, name="prod", tag="prod", bufs=6)
-                    nc.vector.tensor_tensor(out=bank[:], in0=pb_ps[:].rearrange("p a b -> p (a b)"), in1=ptf[:, c, :], op=ALU.mult)
-                for a in range(NA):
-                    bs = slice(a * NB, (a + 1) * NB)
-                    col = (l * NA + a) * 4 + c
-                    if rnd == 0:
-                        kept = ptf[:, c, bs]
-                    else:
-                        waste = work1.tile([P, NB], BF16, name="waste", tag="waste")
-                        kept = waste[:]
-                    nc.scalar.activation(out=kept, in_=bank[:, bs], func=ACT.Copy, accum_out=scol[:, col:col + 1])
-
-        def scale(g, l, rnd):
-            scol = sums[(g, rnd)]
-            ptf = tiles1[g * HG + l]
-            for a in range(NA):
-                t = l * NA + a
-                bs = slice(a * NB, (a + 1) * NB)
-                scaled = work1.tile([P, 4, NB], F32, name="scaled", tag="scaled", bufs=12)
-                scaleds[(g, l, a)] = scaled
-                for c in range(4):
-                    sc = scol[:, t * 4 + c:t * 4 + c + 1]
-                    if by_scalar(t):
-                        nc.scalar.activation(out=scaled[:, c, :], in_=ptf[:, c, bs], func=ACT.Copy, scale=sc)
-                    else:
-                        nc.vector.tensor_scalar(out=scaled[:, c, :], in0=ptf[:, c, bs], scalar1=sc, scalar2=None, op0=ALU.mult)
-
-        def fold(g, l, rnd):
-            fold_ps = psum.tile([P, NA, P], F32, name="fold_ps", tag="fold")
-            folds[(g, l)] = fold_ps
-            for a in range(NA):
-                for c in range(4):
-                    nc.tensor.matmul(fold_ps[:, a, :], lhsT=scaleds[(g, l, a)][:, c, :], rhs=ident_f[:], is_transpose=True, start=(c == 0), stop=(c == 3))
-
-        def agreement(g, l, rnd):
-            ucol = ucols[(2 * g + rnd) % len(ucols)]
-            nc.vector.tensor_reduce(out=ucol[:, l * NA:(l + 1) * NA], in_=folds[(g, l)][:], axis=AX.X, op=ALU.add)
-
-        def chain_of(g, rnd):
-            scol = sums[(g, rnd)]
-            sqc = sqcs[(3 * g + rnd) % len(sqcs)]
-            f = work1.tile([P, 1], F32, name="f", tag="f", bufs=8)
-            z_old = z_one if rnd == 0 else state[g][1]
-            steps = squash_steps(work1, scol[:], lambda sq: sq.rearrange("p (t c) -> p t c", c=4), sqc, sqc[:, 0:NT], z_old, f)
-            if rnd < 2:
-                lt_old = lt_zero if rnd == 0 else state[g][0]
-                lt_new = carry.tile([P, P], F32, name="lt1", tag="lt1")
-                z = carry.tile([P, 1], F32, name="z1", tag="z1")
-                et = carry.tile([P, NT], F32, name="et1", tag="et1")
-
-                def take_weights(et_ps):
-                    nc.vector.tensor_copy(out=et[:], in_=et_ps[:, 0:NT])
-                    state[g] = (lt_new, z, et)
-
-                return steps + softmax_steps(work1, ucols[(2 * g + rnd) % len(ucols)], f, lt_old, lt_new, z, take_weights)
-            got = {}
-
-            def spread():
-                fb_ps = psum.tile([P, P], F32, name="fb_ps", tag="t")
-                got["fb"] = fb_ps
-                nc.tensor.transpose(fb_ps[:], f[:, 0:1].to_broadcast([P, P]), ident_f[:])
-
-            def squash():
-                nc.vector.tensor_tensor(
-                    out=og[:].rearrange("p (a h) c -> p h a c", a=NA)[:, g * HG:(g + 1) * HG],
-                    in0=scol[:].rearrange("p (l a c) -> p l a c", l=HG, a=NA),
-                    in1=got["fb"][:, 0:NT].rearrange("p (l a) -> p l a", a=NA).unsqueeze(3).to_broadcast([P, HG, NA, 4]),
-                    op=ALU.mult)
-
-            return steps + [spread, squash]
-
-        with tc.tile_pool(name="work1", bufs=2) as work1, tc.manual_schedule():
-            ahead = HG + 2
-            for n in range(ahead):
-                weights_step(n)
-            for i in range((NG + 2) * TURNS + 10):
-                if i % 2 == 0:
-                    weights_step(ahead + i // 2)
-                if turn(i):
-                    sums_of(*turn(i))
-                for lag, stage_fn in ((2, scale), (3, fold), (4, agreement)):
-                    if turn(i - lag) and turn(i - lag)[2] < 2:
-                        stage_fn(*turn(i - lag))
-                for j in range(7, -1, -1):
-                    last = turn(i - 2 - j)
-                    if last and last[1] == HG - 1:
-                        g, l, rnd = last
-                        if j == 0:
-                            chains[(g, rnd)] = chain_of(g, rnd)
-                        if j < len(chains[(g, rnd)]):
-                            chains[(g, rnd)][j]()
-
         nc.vector.quantize_mx(out=oc[:].bitcast(FP8X4), scales=os_[:], in_=og[:].rearrange("p w t -> p (w t)"))
         small = ctx.enter_context(tc.tile_pool(name="small", bufs=2))
-        ucol2 = ucols[0]
-        sqc2 = sqcs[0]
 
         def segments(ap):
             return ap.rearrange("p k (a h) -> p k a h", a=NA)

@@ -36,14 +36,11 @@ def tile_capsulelayer_kernel(tc, x, route_weights1, route_weights, out):
         nc.vector.memset(ones_f[:], 1.0)
         half = const.tile([P, 1], F32, name="half")
         nc.vector.memset(half[:], 0.5)
-        blk_ones = const.tile([P, P], F32, name="blk_ones")
-        nc.vector.memset(blk_ones[:], 0.0)
         lt_blk = const.tile([P, P], F32, name="lt_blk")
         nc.vector.memset(lt_blk[:], -1.0e30)
         for a in range(NA):
             blk = slice(32 * a, 32 * a + 32)
             nc.vector.memset(lt_blk[blk, blk], 0.0)
-            nc.vector.memset(blk_ones[blk, blk], 1.0)
         z_blk = const.tile([P, 1], F32, name="z_blk")
         nc.vector.memset(z_blk[:], float(NH))
         ucol2 = const.tile([P, P], F32, name="ucol2")
@@ -88,7 +85,7 @@ def tile_capsulelayer_kernel(tc, x, route_weights1, route_weights, out):
             nc.sync.dma_start(out=x_sb[:], in_=x.rearrange("a b d -> b a d"))
             xg = stage.tile([P, NA * NB, 4], BF16, name="xg", tag="grouped", align_bytes=64)
             for a in range(NA):
-                xt_ps = psum.tile([P, 4, NB], BF16, name="xt_ps", tag="big", bufs=3)
+                xt_ps = psum.tile([P, 4, NB], BF16, name="xt_ps", tag="big")
                 for t in range(4):
                     nc.tensor.transpose(xt_ps[:, t, :], x_sb[:, a, :].rearrange("b (p t) -> b t p", t=4)[:, t, :], ident_b[:])
                 nc.vector.tensor_copy(out=xg[:].rearrange("p (j a q) t -> p a j q t", j=NJ, a=NA)[:, a],
@@ -121,8 +118,8 @@ def tile_capsulelayer_kernel(tc, x, route_weights1, route_weights, out):
 
             def quantize(kind, m):
                 if kind == 1:
-                    wc = stage.tile([P, NE], U32, name="wc", tag="wc", align_bytes=64)
-                    ws = stage.tile([P, NE], U8, name="ws", tag="ws", align_bytes=64)
+                    wc = stage.tile([P, NE], U32, name="wc", tag="wc", bufs=3, align_bytes=64)
+                    ws = stage.tile([P, NE], U8, name="ws", tag="ws", bufs=3, align_bytes=64)
                     codes[m] = (wc, ws)
                     cw, sw = wc[:], ws[:]
                 else:
@@ -132,25 +129,17 @@ def tile_capsulelayer_kernel(tc, x, route_weights1, route_weights, out):
             def x_block(j):
                 return xc[:, j * P:(j + 1) * P], xs[:, j * P:(j + 1) * P]
 
-            def total_mx(h):
-                q_ps = psum.tile([P, NE], F32, name="q_ps", tag="fold", bufs=3)
-                banks[("q", h)] = q_ps
+            def total_mx(h, c):
+                if c == 0:
+                    t_ps = psum.tile([P, 4, P], F32, name="t_ps", tag="tot")
+                    banks[("f", h, 0)] = t_ps
                 wc, ws = codes[h]
+                cs = slice(c * P, (c + 1) * P)
                 for j in range(NJ):
-                    mx(q_ps[:], *x_block(j), wc[:], ws[:], start=(j == 0), stop=(j == NJ - 1))
-
-            def total_copy(h):
-                q_sb = work.tile([P, NE], F32, name="q_sb", tag="q_sb")
-                ys[("q", h)] = q_sb
-                nc.scalar.copy(out=q_sb[:], in_=banks[("q", h)][:])
-
-            def total_spread(h):
-                sb_ps = psum.tile([P, NE], F32, name="sb_ps", tag="sb")
-                sbs[(h, 0)] = sb_ps
-                nc.tensor.matmul(sb_ps[:], lhsT=blk_ones[:], rhs=ys[("q", h)][:], start=True, stop=True)
+                    mx(banks[("f", h, 0)][:, c, :], wc[:, cs], ws[:, cs], *x_block(j), start=(j == 0), stop=(j == NJ - 1))
 
             def prior_mx(h, j):
-                p_ps = psum.tile([P, NE], F32, name="p_ps", tag="big", bufs=3)
+                p_ps = psum.tile([P, NE], F32, name="p_ps", tag="big")
                 banks[("p", h, j)] = p_ps
                 wc, ws = codes[h]
                 mx(p_ps[:], *x_block(j), wc[:], ws[:])
@@ -179,7 +168,7 @@ def tile_capsulelayer_kernel(tc, x, route_weights1, route_weights, out):
                     nc.scalar.activation(out=dst, in_=src, func=ACT.Copy, scale=weights_of(h, rnd, j))
 
             def fold(h, rnd):
-                f_ps = psum.tile([P, 4, P], F32, name="f_ps", tag="fold", bufs=3)
+                f_ps = psum.tile([P, 4, P], F32, name="f_ps", tag="fold")
                 banks[("f", h, rnd)] = f_ps
                 for c in range(4):
                     for j in range(NJ):
@@ -187,23 +176,23 @@ def tile_capsulelayer_kernel(tc, x, route_weights1, route_weights, out):
 
             def sums(h, rnd):
                 f_ps = banks[("f", h, rnd)]
-                if rnd == 1:
-                    scol = work.tile([P, 4, NA], F32, name="scol", tag="scol")
-                    scols[h] = scol
+                if rnd < 2:
+                    scol = work.tile([P, 4, NA], F32, name="scol", tag="scol", bufs=3)
+                    scols[(h, rnd)] = scol
                     dst = scol[:]
                 else:
                     dst = s2[:].rearrange("p (a h) c -> p h c a", a=NA)[:, h]
                 nc.vector.tensor_reduce(out=dst, in_=f_ps[:].rearrange("p c (a q) -> p c a q", a=NA), axis=AX.X, op=ALU.add)
 
-            def repeat(h):
+            def repeat(h, rnd):
                 bc = work.tile([P, 4, NA, 32], F32, name="bc", tag="bc")
-                ys[("bc", h)] = bc
-                nc.scalar.copy(out=bc[:], in_=scols[h][:].unsqueeze(3).to_broadcast([P, 4, NA, 32]))
+                ys[("bc", h, rnd)] = bc
+                nc.scalar.copy(out=bc[:], in_=scols[(h, rnd)][:].unsqueeze(3).to_broadcast([P, 4, NA, 32]))
 
-            def spread(h):
+            def spread(h, rnd):
                 sb_ps = psum.tile([P, NE], F32, name="sb_ps", tag="sb")
-                sbs[(h, 1)] = sb_ps
-                bc = ys[("bc", h)]
+                sbs[(h, rnd)] = sb_ps
+                bc = ys[("bc", h, rnd)]
                 for c in range(4):
                     nc.tensor.transpose(sb_ps[:, c * P:(c + 1) * P], bc[:, c].rearrange("p a q -> p (a q)"), ident_f[:])
 
@@ -282,21 +271,28 @@ def tile_capsulelayer_kernel(tc, x, route_weights1, route_weights, out):
                         if r == 0 and 0 <= m < NC2:
                             fn(2, m)
 
-                    h = at(tick, -9)
+                    h = at(tick, -13)
                     if h is not None and h >= 2:
                         load(1, h)
                     run2(load, -6)
-                    run(sums, ROUND1 + 5, 1)
-                    run(sums, ROUND2 + 5, 2)
                     m, k = divmod(tick - 2, 16)
                     if 1 <= m <= NG + 2 and k <= 6:
                         softmax_step(m, k)
-                    run(total_copy, 1)
-                    run(total_spread, 2)
-                    run(spread, ROUND1 + 6)
-                    run(total_mx, 0)
+                    for j in (0, 2):
+                        run(agree, 4 + j // 2, 0, j)
+                        run(agree, ROUND1 + 7 + j // 2, 1, j)
+                    run(sums, 1, 0)
+                    run(sums, ROUND1 + 5, 1)
+                    run(sums, ROUND2 + 5, 2)
+                    for j in (1, 3):
+                        run(agree, 4 + j // 2, 0, j)
+                        run(agree, ROUND1 + 7 + j // 2, 1, j)
+                    for c in range(4):
+                        run(total_mx, c - 3, c)
                     for j in range(NJ):
                         run(prior_mx, j, j)
+                    run(spread, 2, 0)
+                    run(spread, ROUND1 + 6, 1)
                     run(fold, ROUND1 + 4, 1)
                     run(fold, ROUND2 + 4, 2)
                     for j in range(NJ):
@@ -304,15 +300,13 @@ def tile_capsulelayer_kernel(tc, x, route_weights1, route_weights, out):
                         run(scale, ROUND2 + j, 2, j)
                     for j in range(NJ):
                         run(prior_copy, j, j)
-                    run(repeat, ROUND1 + 5)
-                    for j in range(NJ):
-                        run(agree, 4 + j // 2, 0, j)
-                        run(agree, ROUND1 + 7 + j // 2, 1, j)
-                    h = at(tick, -5)
+                    run(repeat, 1, 0)
+                    run(repeat, ROUND1 + 5, 1)
+                    h = at(tick, -9)
                     if h is not None:
                         regroup(1, h)
                     run2(regroup, -3)
-                    h = at(tick, -1)
+                    h = at(tick, -5)
                     if h is not None:
                         quantize(1, h)
                     run2(quantize, 1)

@@ -19,8 +19,9 @@ FLOPS = 2 * (NA * NB * ND * NE * NH + NA * NH * NE * NE * NC2)
 NJ = 4
 HG = 4
 NG = NH // HG
+PIECES = 4
 HELD = 16
-ROUND1, ROUND2 = 27, 57
+ROUND1, ROUND2 = 27, 56
 
 
 def tile_capsulelayer_kernel(tc, x, route_weights1, route_weights, out):
@@ -36,18 +37,6 @@ def tile_capsulelayer_kernel(tc, x, route_weights1, route_weights, out):
         nc.vector.memset(ones_f[:], 1.0)
         half = const.tile([P, 1], F32, name="half")
         nc.vector.memset(half[:], 0.5)
-        lt_blk = const.tile([P, P], F32, name="lt_blk")
-        nc.vector.memset(lt_blk[:], -1.0e30)
-        for a in range(NA):
-            blk = slice(32 * a, 32 * a + 32)
-            nc.vector.memset(lt_blk[blk, blk], 0.0)
-        z_blk = const.tile([P, 1], F32, name="z_blk")
-        nc.vector.memset(z_blk[:], float(NH))
-        ucol2 = const.tile([P, P], F32, name="ucol2")
-        nc.vector.memset(ucol2[:], 0.0)
-        sqc2 = const.tile([P, P], F32, name="sqc2")
-        nc.vector.memset(sqc2[:], 0.0)
-
         xc = const.tile([P, NA * NB], U32, name="xc", align_bytes=64)
         xs = const.tile([P, NA * NB], U8, name="xs", align_bytes=64)
         w2c = const.tile([P, NC2, NE], U32, name="w2c", align_bytes=64)
@@ -59,6 +48,10 @@ def tile_capsulelayer_kernel(tc, x, route_weights1, route_weights, out):
         def mx(out_ps, l_codes, l_scales, r_codes, r_scales, start=True, stop=True):
             nc.tensor.matmul_mx(out=out_ps, lhsT=l_codes.bitcast(FP8X4), lhsT_scale=l_scales,
                                 rhs=r_codes.bitcast(FP8X4), rhs_scale=r_scales, start=start, stop=stop)
+
+        def keep_clock(codes_512, scales_512, tag):
+            idle_ps = psum.tile([P, NE], F32, name="idle_ps", tag=tag)
+            mx(idle_ps[:], xc[:, 0:P], xs[:, 0:P], codes_512, scales_512)
 
         with ExitStack() as first:
             stage = first.enter_context(tc.tile_pool(name="stage", bufs=2))
@@ -114,7 +107,9 @@ def tile_capsulelayer_kernel(tc, x, route_weights1, route_weights, out):
                 if kind == 1 and m < 2:
                     nc.vector.tensor_copy(out=grouped[:].rearrange("p (c i) t -> p c t i", i=4), in_=raw[:].rearrange("p t (c i) -> p c t i", i=4))
                 else:
-                    nc.gpsimd.tensor_scalar(out=grouped[:], in0=raw[:].rearrange("p t c -> p c t"), scalar1=1.0, scalar2=0.0, op0=ALU.mult, op1=ALU.add)
+                    for s in range(PIECES):
+                        cs = slice(s * NE // PIECES, (s + 1) * NE // PIECES)
+                        nc.gpsimd.tensor_scalar(out=grouped[:, cs, :], in0=raw[:, :, cs].rearrange("p t c -> p c t"), scalar1=1.0, scalar2=0.0, op0=ALU.mult, op1=ALU.add)
 
             def quantize(kind, m):
                 if kind == 1:
@@ -143,6 +138,7 @@ def tile_capsulelayer_kernel(tc, x, route_weights1, route_weights, out):
                 banks[("p", h, j)] = p_ps
                 wc, ws = codes[h]
                 mx(p_ps[:], *x_block(j), wc[:], ws[:])
+                mx(p_ps[:], *x_block(j), wc[:], ws[:])
 
             def prior_copy(h, j):
                 if j == 0:
@@ -164,6 +160,8 @@ def tile_capsulelayer_kernel(tc, x, route_weights1, route_weights, out):
                 ys[(h, rnd, j)] = dst
                 if j == 0:
                     nc.gpsimd.tensor_scalar(out=dst, in0=src, scalar1=weights_of(h, rnd, j), scalar2=0.0, op0=ALU.mult, op1=ALU.add)
+                elif j == 1 and rnd == 2 and h >= NH - 7:
+                    nc.vector.tensor_scalar(out=dst, in0=src, scalar1=weights_of(h, rnd, j), scalar2=None, op0=ALU.mult)
                 else:
                     nc.scalar.activation(out=dst, in_=src, func=ACT.Copy, scale=weights_of(h, rnd, j))
 
@@ -212,12 +210,11 @@ def tile_capsulelayer_kernel(tc, x, route_weights1, route_weights, out):
                     small["ut"] = ut
                     nc.vector.transpose(ut[:], u[:])
                     nc.gpsimd.memset(u[:], 0.0)
-                elif k == 1:
                     n = work.tile([P, 1], F32, name="n", tag="n")
                     small["n"] = n
                     eu = work.tile([P, P], F32, name="eu", tag="eu")
                     nc.vector.scalar_tensor_tensor(out=eu[:], in0=small["ut"][:], scalar=1.0, in1=e_old[:], op0=ALU.mult, op1=ALU.mult, accum_out=n[:])
-                elif k == 2:
+                elif k == 1:
                     rt = work.tile([P, 1], F32, name="rt", tag="rt")
                     small["rt"] = rt
                     nc.gpsimd.tensor_tensor(out=rt[:], in0=small["n"][:], in1=half[:], op=ALU.pow)
@@ -226,7 +223,7 @@ def tile_capsulelayer_kernel(tc, x, route_weights1, route_weights, out):
                     rden = work.tile([P, 1], F32, name="rden", tag="rden")
                     small["rden"] = rden
                     nc.vector.reciprocal(out=rden[:], in_=den[:])
-                elif k == 4:
+                elif k == 3:
                     f = work.tile([P, 1], F32, name="f", tag="f")
                     nc.vector.tensor_tensor(out=f[:], in0=small["rt"][:], in1=small["rden"][:], op=ALU.mult)
                     lt = work.tile([P, P], F32, name="lt", tag="lt")
@@ -235,13 +232,13 @@ def tile_capsulelayer_kernel(tc, x, route_weights1, route_weights, out):
                     negmax = work.tile([P, 1], F32, name="negmax", tag="negmax")
                     small["negmax"] = negmax
                     nc.vector.tensor_reduce(out=negmax[:], in_=lt[:], axis=AX.X, op=ALU.max, negate=True)
-                elif k == 5:
+                elif k == 4:
                     e = work.tile([P, P], F32, name="e", tag="e", align_bytes=64)
                     small["e"] = e
                     z = work.tile([P, 1], F32, name="z", tag="z")
                     small["z"] = z
                     nc.scalar.activation(out=e[:], in_=small["lt"][:], func=ACT.Exp, bias=small["negmax"][:, 0:1], scale=1.0, accum_out=z[:])
-                elif k == 6:
+                elif k == 5:
                     et = work.tile([P, P], F32, name="et", tag="et", bufs=4, align_bytes=64)
                     nc.vector.transpose(et[:], small["e"][:])
                     state[m] = (small["lt"], small["e"], small["z"], et)
@@ -257,7 +254,7 @@ def tile_capsulelayer_kernel(tc, x, route_weights1, route_weights, out):
                 return h if r == 0 and 0 <= h < NH else None
 
             with tc.manual_schedule():
-                w2_load, w2_first = 24, 24 * 4
+                w2_first = 4 * 30
                 load(1, 0)
                 load(1, 1)
                 for tick in range(-9, 4 * (NH - 1) + ROUND2 + 8):
@@ -276,7 +273,7 @@ def tile_capsulelayer_kernel(tc, x, route_weights1, route_weights, out):
                         load(1, h)
                     run2(load, -6)
                     m, k = divmod(tick - 2, 16)
-                    if 1 <= m <= NG + 2 and k <= 6:
+                    if 1 <= m <= NG + 2 and k <= 5:
                         softmax_step(m, k)
                     for j in (0, 2):
                         run(agree, 4 + j // 2, 0, j)
@@ -291,6 +288,9 @@ def tile_capsulelayer_kernel(tc, x, route_weights1, route_weights, out):
                         run(total_mx, c - 3, c)
                     for j in range(NJ):
                         run(prior_mx, j, j)
+                    if tick >= 4 * NH:
+                        keep_clock(xc[:], xs[:], "tot")
+                        keep_clock(xc[:], xs[:], "tot")
                     run(spread, 2, 0)
                     run(spread, ROUND1 + 6, 1)
                     run(fold, ROUND1 + 4, 1)
@@ -331,163 +331,174 @@ def tile_capsulelayer_kernel(tc, x, route_weights1, route_weights, out):
                 nc.tensor.transpose(fb_ps[:], f[:, 0:1].to_broadcast([P, P]), ident_f[:])
                 nc.vector.tensor_tensor(out=og[:], in0=s2[:], in1=fb_ps[:].unsqueeze(2).to_broadcast([P, NA * NH, 4]), op=ALU.mult)
 
-        psum = ctx.enter_context(tc.psum_pool(name="psum2", bufs=2))
-
-        def squash_steps(pool, s_flat, by_problem, sqc, sqc_own, z, f):
-            sq = pool.tile(list(s_flat.shape), F32, name="sq", tag="sq", bufs=4)
-            n_sb = pool.tile([P, 1], F32, name="n_sb", tag="n_sb", bufs=6)
-            rt = pool.tile([P, 1], F32, name="rt", tag="rt", bufs=6)
-            den = pool.tile([P, 1], F32, name="den", tag="den", bufs=6)
-            rden = pool.tile([P, 1], F32, name="rden", tag="rden", bufs=6)
-            got = {}
-
-            def step1():
-                nc.scalar.activation(out=sq[:], in_=s_flat, func=ACT.Square)
-
-            def step2():
-                nc.vector.tensor_reduce(out=sqc_own, in_=by_problem(sq[:]), axis=AX.X, op=ALU.add)
-                n_ps = psum.tile([P, 2], F32, name="n_ps", tag="t")
-                got["n"] = n_ps
-                nc.tensor.matmul(n_ps[:], lhsT=sqc[:], rhs=ones_f[:], start=True, stop=True)
-
-            def step3():
-                nc.vector.tensor_copy(out=n_sb[:], in_=got["n"][:, 0:1])
-                nc.gpsimd.tensor_tensor(out=rt[:], in0=n_sb[:], in1=half[:], op=ALU.pow)
-                nc.vector.tensor_scalar(out=den[:], in0=z[:], scalar1=z[:, 0:1], scalar2=n_sb[:, 0:1], op0=ALU.mult, op1=ALU.add)
-                nc.vector.reciprocal(out=rden[:], in_=den[:])
-
-            def step4():
-                nc.vector.tensor_tensor(out=f[:], in0=rt[:], in1=rden[:], op=ALU.mult)
-
-            return [step1, step2, step3, step4]
-
-        def softmax_steps(pool, ucol, f, lt, lt_new, z, take_weights):
-            negmax = pool.tile([P, 1], F32, name="negmax", tag="negmax", bufs=6)
-            e_sb = pool.tile([P, P], F32, name="e_sb", tag="e_sb", bufs=4)
-            got = {}
-
-            def step1():
-                ut_ps = psum.tile([P, P], F32, name="ut_ps", tag="t")
-                got["ut"] = ut_ps
-                nc.tensor.transpose(ut_ps[:], ucol[:], ident_f[:])
-
-            def step2():
-                nc.vector.scalar_tensor_tensor(out=lt_new[:], in0=got["ut"][:], scalar=f[:, 0:1], in1=lt[:], op0=ALU.mult, op1=ALU.add)
-                nc.vector.tensor_reduce(out=negmax[:], in_=lt_new[:], axis=AX.X, op=ALU.max, negate=True)
-
-            def step3():
-                nc.scalar.activation(out=e_sb[:], in_=lt_new[:], func=ACT.Exp, bias=negmax[:, 0:1], scale=1.0, accum_out=z[:])
-                et_ps = psum.tile([P, P], F32, name="et_ps", tag="t")
-                got["et"] = et_ps
-                nc.tensor.transpose(et_ps[:], e_sb[:], ident_f[:])
-
-            def step4():
-                take_weights(got["et"])
-
-            return [step1, step2, step3, step4]
-
         nc.vector.quantize_mx(out=oc[:].bitcast(FP8X4), scales=os_[:], in_=og[:].rearrange("p w t -> p (w t)"))
-        small = ctx.enter_context(tc.tile_pool(name="small", bufs=2))
+        psum = ctx.enter_context(tc.psum_pool(name="psum2", bufs=2))
+        second = ctx.enter_context(tc.tile_pool(name="second", bufs=2))
+        HALF = NC2 // 2
+        priors2 = second.tile([P, NC2, NE], F32, name="priors2", bufs=1)
+        lt0 = second.tile([P, 32], F32, name="lt0b", bufs=1, align_bytes=64)
+        nc.vector.memset(lt0[:], 0.0)
+        e0 = second.tile([P, 32], F32, name="e0b", bufs=1, align_bytes=64)
+        nc.vector.memset(e0[:], 1.0)
+        z0 = second.tile([P, 1], F32, name="z0b", bufs=1)
+        nc.vector.memset(z0[:], float(NH))
+        state2 = {0: (lt0, e0, z0, None)}
+        us2 = {}
+        for m in range(1, 5):
+            u = second.tile([P, 32], F32, name="ub%d" % m, bufs=1, align_bytes=64)
+            nc.vector.memset(u[:], 0.0)
+            us2[m] = u
+        sqcs = []
+        s2s = []
+        for half_no in range(2):
+            sqc = second.tile([P, P], F32, name="sqcb%d" % half_no, bufs=1)
+            nc.vector.memset(sqc[:], 0.0)
+            sqcs.append(sqc)
+            s2 = second.tile([P, HALF, 4, NA], F32, name="s2b%d" % half_no, bufs=1)
+            s2s.append(s2)
+        fbanks = {}
+        nbanks = {}
+        y2s = {}
+        scol2s = {}
+        bc2s = {}
+        sb2s = {}
 
-        def segments(ap):
-            return ap.rearrange("p k (a h) -> p k a h", a=NA)
+        def softmax_no(rnd, c):
+            return 2 * rnd + c // HALF + 1
 
-        def own(tile_ap):
-            return tile_ap.rearrange("p (n c) -> p c n", c=32)[:, 0:NC2, :]
+        def open2(rnd, c):
+            if rnd == 0:
+                qt_ps = psum.tile([P, 4, P], F32, name="qt_ps", tag="f", bufs=3)
+                fbanks[(rnd, c)] = qt_ps
+                for k in range(4):
+                    cs = slice(k * P, (k + 1) * P)
+                    mx(qt_ps[:, k, :], w2c[:, c, cs], w2s[:, c, cs], oc[:], os_[:])
+                q_ps = psum.tile([P, NE], F32, name="q_ps", tag="n")
+                mx(q_ps[:], oc[:], os_[:], w2c[:, c, :], w2s[:, c, :])
+                nbanks[c] = q_ps
+            else:
+                y = second.tile([P, NE], F32, name="y2", tag="y2", bufs=3)
+                y2s[(rnd, c)] = y
+                w = state2[softmax_no(rnd - 1, c)][3][:, c:c + 1]
+                if c % 2:
+                    nc.gpsimd.tensor_scalar(out=y[:], in0=priors2[:, c, :], scalar1=w, scalar2=0.0, op0=ALU.mult, op1=ALU.add)
+                else:
+                    nc.scalar.activation(out=y[:], in_=priors2[:, c, :], func=ACT.Copy, scale=w)
 
-        def bank_features(c):
-            qt_ps = psum.tile([P, 4, P], F32, name="qt_ps", tag="big")
-            for fc in range(4):
-                cs = slice(fc * P, (fc + 1) * P)
-                mx(qt_ps[:, fc, :], w2c[:, c, cs], w2s[:, c, cs], oc[:], os_[:])
-            return qt_ps
+        def turn2(rnd, c):
+            if rnd == 0:
+                nc.scalar.copy(out=priors2[:, c, :], in_=nbanks[c][:])
+            else:
+                tr_ps = psum.tile([P, 4, P], F32, name="tr_ps", tag="f", bufs=3)
+                fbanks[(rnd, c)] = tr_ps
+                for k in range(4):
+                    nc.tensor.transpose(tr_ps[:, k, :], y2s[(rnd, c)][:, k * P:(k + 1) * P], ident_f[:])
+                if rnd == 1:
+                    keep_clock(w2c[:, c, :], w2s[:, c, :], "n")
+                    keep_clock(w2c[:, c, :], w2s[:, c, :], "n")
 
-        def first_sums2(scol):
-            for c in range(NC2):
-                nc.vector.tensor_reduce(out=scol[:, c * 4:(c + 1) * 4, :], in_=segments(bank_features(c)[:]), axis=AX.X, op=ALU.add)
+        def sums2(rnd, c):
+            if rnd < 2:
+                scol = second.tile([P, 4, NA], F32, name="scol2", tag="scol2", bufs=3)
+                scol2s[(rnd, c)] = scol
+                dst = scol[:]
+            else:
+                dst = s2s[c // HALF][:, c % HALF]
+            nc.vector.tensor_reduce(out=dst, in_=fbanks[(rnd, c)][:].rearrange("p k (a h) -> p k a h", a=NA), axis=AX.X, op=ALU.add)
 
-        def weighted_sums2(scol, e2):
-            ys = {}
-            turned = {}
-            for i in range(NC2 + 4):
-                if i < NC2:
-                    q_ps = psum.tile([P, NE], F32, name="q_ps", tag="big")
-                    mx(q_ps[:], oc[:], os_[:], w2c[:, i, :], w2s[:, i, :])
-                    y = small.tile([P, NE], F32, name="y", tag="y", bufs=4)
-                    ys[i] = y
-                    nc.scalar.activation(out=y[:], in_=q_ps[:], func=ACT.Copy, scale=e2[:, i:i + 1])
-                if 0 <= i - 2 < NC2:
-                    tr_ps = psum.tile([P, 4, P], F32, name="tr_ps", tag="pb")
-                    turned[i - 2] = tr_ps
-                    for fc in range(4):
-                        nc.tensor.transpose(tr_ps[:, fc, :], ys[i - 2][:, fc * P:(fc + 1) * P], ident_f[:])
-                if 0 <= i - 4 < NC2:
-                    c = i - 4
-                    nc.vector.tensor_reduce(out=scol[:, c * 4:(c + 1) * 4, :], in_=segments(turned[c][:]), axis=AX.X, op=ALU.add)
+        def repeat2(rnd, c):
+            if rnd < 2:
+                bc = second.tile([P, 4, NA, 32], F32, name="bc2", tag="bc2", bufs=3)
+                bc2s[(rnd, c)] = bc
+                nc.scalar.copy(out=bc[:], in_=scol2s[(rnd, c)][:].unsqueeze(3).to_broadcast([P, 4, NA, 32]))
 
-        def agreement2(scol, u2, steps):
-            scaled2s = {}
-            fold2s = {}
-            for i in range(NC2 + 4):
-                if i % 2 == 1 and i // 2 < len(steps):
-                    steps[i // 2]()
-                if i < NC2:
-                    bank = bank_features(i)
-                    scaled = small.tile([P, 4, P], F32, name="scaled2", tag="scaled2", bufs=4)
-                    scaled2s[i] = scaled
-                    nc.vector.tensor_tensor(out=segments(scaled[:]), in0=segments(bank[:]),
-                                            in1=scol[:, i * 4:(i + 1) * 4, :].unsqueeze(3).to_broadcast([P, 4, NA, NH]), op=ALU.mult)
-                if 0 <= i - 2 < NC2:
-                    c = i - 2
-                    if c % 4 == 0:
-                        fold_ps = psum.tile([P, 4, P], F32, name="fold2_ps", tag="fold")
-                        fold2s[c // 4] = fold_ps
-                    for fc in range(4):
-                        nc.tensor.matmul(fold2s[c // 4][:, c % 4, :], lhsT=scaled2s[c][:, fc, :], rhs=ident_f[:], is_transpose=True, start=(fc == 0), stop=(fc == 3))
-                if 0 <= i - 4 < NC2 and (i - 4) % 4 == 3:
-                    q = (i - 4) // 4
-                    nc.vector.tensor_reduce(out=u2[:, q * 4:(q + 1) * 4], in_=fold2s[q][:], axis=AX.X, op=ALU.add)
+        def spread2(rnd, c):
+            if rnd < 2:
+                sb_ps = psum.tile([P, NE], F32, name="sb_ps2", tag="sb")
+                sb2s[(rnd, c)] = sb_ps
+                for k in range(4):
+                    nc.tensor.transpose(sb_ps[:, k * P:(k + 1) * P], bc2s[(rnd, c)][:, k].rearrange("p a h -> p (a h)"), ident_f[:])
+
+        def agree2(rnd, c):
+            if rnd < 2:
+                waste = second.tile([P, NE], BF16, name="waste2", tag="waste2")
+                nc.vector.scalar_tensor_tensor(out=waste[:], in0=priors2[:, c, :], scalar=1.0, in1=sb2s[(rnd, c)][:], op0=ALU.mult, op1=ALU.mult,
+                                               accum_out=us2[softmax_no(rnd, c)][:, c:c + 1])
+
+        tiny = {}
+
+        def factor2(n, z_old):
+            rt = second.tile([P, 1], F32, name="rtb", tag="rtb")
+            nc.gpsimd.tensor_tensor(out=rt[:], in0=n[:], in1=half[:], op=ALU.pow)
+            den = second.tile([P, 1], F32, name="denb", tag="denb")
+            nc.vector.tensor_scalar(out=den[:], in0=z_old[:], scalar1=z_old[:, 0:1], scalar2=n[:, 0:1], op0=ALU.mult, op1=ALU.add)
+            rden = second.tile([P, 1], F32, name="rdenb", tag="rdenb")
+            nc.vector.reciprocal(out=rden[:], in_=den[:])
+            f = second.tile([P, 1], F32, name="fb", tag="fb")
+            nc.vector.tensor_tensor(out=f[:], in0=rt[:], in1=rden[:], op=ALU.mult)
+            return f
+
+        def softmax2_step(m, k):
+            lt_old, e_old, z_old = state2[m - 1][0], state2[m - 1][1], state2[m - 1][2]
+            if k == 0:
+                ut = second.tile([P, 32], F32, name="utb", tag="utb", align_bytes=64)
+                tiny["ut"] = ut
+                nc.vector.transpose(ut[:], us2[m][:])
+                n = second.tile([P, 1], F32, name="nb", tag="nb")
+                tiny["n"] = n
+                eu = second.tile([P, 32], F32, name="eub", tag="eub")
+                nc.vector.scalar_tensor_tensor(out=eu[:], in0=ut[:], scalar=1.0, in1=e_old[:], op0=ALU.mult, op1=ALU.mult, accum_out=n[:])
+            elif k == 1:
+                tiny["f"] = factor2(tiny["n"], z_old)
+            elif k == 2:
+                lt = second.tile([P, 32], F32, name="ltb", tag="ltb")
+                nc.vector.scalar_tensor_tensor(out=lt[:], in0=tiny["ut"][:], scalar=tiny["f"][:, 0:1], in1=lt_old[:], op0=ALU.mult, op1=ALU.add)
+                negmax = second.tile([P, 1], F32, name="negmaxb", tag="negmaxb")
+                nc.vector.tensor_reduce(out=negmax[:], in_=lt[:], axis=AX.X, op=ALU.max, negate=True)
+                e = second.tile([P, 32], F32, name="eb", tag="eb", align_bytes=64)
+                z = second.tile([P, 1], F32, name="zb", tag="zb")
+                nc.scalar.activation(out=e[:], in_=lt[:], func=ACT.Exp, bias=negmax[:, 0:1], scale=1.0, accum_out=z[:])
+                tiny["new"] = (lt, e, z)
+            else:
+                et = second.tile([P, 32], F32, name="etb", tag="etb", bufs=3, align_bytes=64)
+                nc.vector.transpose(et[:], tiny["new"][1][:])
+                state2[m] = tiny["new"] + (et,)
+
+        out_rows = out.rearrange("c a (k f) -> (c a k) f", f=P)
+
+        def finish(half_no):
+            s2, sqc = s2s[half_no], sqcs[half_no]
+            sq = second.tile([P, HALF, 4, NA], F32, name="sqb", tag="sqb")
+            nc.scalar.activation(out=sq[:], in_=s2[:], func=ACT.Square)
+            nc.vector.tensor_reduce(out=sqc[:].rearrange("p (a c) -> p a c", a=NA)[:, :, half_no * HALF:(half_no + 1) * HALF],
+                                    in_=sq[:].rearrange("p c k a -> p a c k"), axis=AX.X, op=ALU.add)
+            n_ps = psum.tile([P, 2], F32, name="n2_ps", tag="t", bufs=1)
+            nc.tensor.matmul(n_ps[:], lhsT=sqc[:], rhs=ones_f[:], start=True, stop=True)
+            n = second.tile([P, 1], F32, name="nb", tag="nb")
+            nc.vector.tensor_copy(out=n[:], in_=n_ps[:, 0:1])
+            f = factor2(n, state2[4][2])
+            fb_ps = psum.tile([P, P], F32, name="fb2_ps", tag="t", bufs=1)
+            nc.tensor.transpose(fb_ps[:], f[:, 0:1].to_broadcast([P, P]), ident_f[:])
+            o = second.tile([P, HALF, NA, 4], F32, name="o", tag="o")
+            own = fb_ps[:].rearrange("p (a c) -> p c a", a=NA)[:, half_no * HALF:(half_no + 1) * HALF, :]
+            nc.vector.tensor_tensor(out=o[:], in0=s2[:].rearrange("p c k a -> p c a k"), in1=own.unsqueeze(3).to_broadcast([P, HALF, NA, 4]), op=ALU.mult)
+            ot_ps = psum.tile([P, P], F32, name="ot_ps", tag="t", bufs=1)
+            nc.tensor.transpose(ot_ps[:], o[:].rearrange("p c a k -> p (c a k)"), ident_f[:])
+            res = second.tile([P, P], F32, name="res", tag="res")
+            nc.scalar.copy(out=res[:], in_=ot_ps[:])
+            nc.sync.dma_start(out=out_rows[half_no * P:(half_no + 1) * P, :], in_=res[:])
 
         with tc.manual_schedule():
-            z = z_blk
-            lt = lt_blk
-            e2 = None
-            for rnd in range(3):
-                scol = small.tile([P, NC2 * 4, NA], F32, name="scol", tag="scol")
-                if rnd == 0:
-                    first_sums2(scol)
-                else:
-                    weighted_sums2(scol, e2)
-                f = small.tile([P, 1], F32, name="f2", tag="f2")
-                steps = squash_steps(small, scol[:], lambda sq: sq.rearrange("p (t k) n -> p t n k", k=4), sqc2, own(sqc2[:]), z, f)
-                if rnd == 2:
-                    for step in steps:
-                        step()
-                    break
-                u2 = small.tile([P, NC2], F32, name="u2", tag="u2")
-                agreement2(scol, u2, steps)
-                nc.vector.tensor_copy(out=own(ucol2[:]), in_=u2[:].unsqueeze(2).to_broadcast([P, NC2, NA]))
-                lt_new = small.tile([P, P], F32, name="lt_new", tag="lt")
-                z = small.tile([P, 1], F32, name="z", tag="z")
-                e2 = small.tile([P, NC2], F32, name="e2", tag="e2")
+            for tick in range(3 * NC2 + 2):
+                def item(n):
+                    return divmod(n, NC2) if 0 <= n < 3 * NC2 else None
 
-                def take_weights2(et_ps):
-                    nc.vector.tensor_reduce(out=e2[:], in_=own(et_ps[:]), axis=AX.X, op=ALU.add)
-
-                for step in softmax_steps(small, ucol2, f, lt, lt_new, z, take_weights2):
-                    step()
-                lt = lt_new
-
-            fb_ps = psum.tile([P, P], F32, name="fb2_ps", tag="t")
-            nc.tensor.transpose(fb_ps[:], f[:, 0:1].to_broadcast([P, P]), ident_f[:])
-            o_sb = small.tile([P, NC2, NA, 4], F32, name="o_sb", tag="o_sb", bufs=1)
-            nc.vector.tensor_tensor(out=o_sb[:], in0=scol[:].rearrange("p (t k) n -> p t n k", k=4),
-                                    in1=own(fb_ps[:]).unsqueeze(3).to_broadcast([P, NC2, NA, 4]), op=ALU.mult)
-            o_flat = o_sb[:].rearrange("p t n k -> p (t n k)")
-            out_rows = out.rearrange("c a (k f) -> (c a k) f", f=P)
-            for i in range(2):
-                ot_ps = psum.tile([P, P], F32, name="ot_ps", tag="t")
-                nc.tensor.transpose(ot_ps[:], o_flat[:, i * P:(i + 1) * P], ident_f[:])
-                res = small.tile([P, P], F32, name="res", tag="res")
-                nc.scalar.copy(out=res[:], in_=ot_ps[:])
-                nc.sync.dma_start(out=out_rows[i * P:(i + 1) * P, :], in_=res[:])
+                m, k = divmod(tick - 5, HALF)
+                if 1 <= m <= 4 and k < 4:
+                    softmax2_step(m, k)
+                for lag, fn in ((2, sums2), (5, agree2), (3, repeat2), (4, spread2), (1, turn2), (0, open2)):
+                    if item(tick - lag):
+                        fn(*item(tick - lag))
+                if tick == 2 * NC2 + HALF + 4:
+                    finish(0)
+            finish(1)

@@ -20,8 +20,10 @@ NJ = 4
 HG = 4
 NG = NH // HG
 PIECES = 4
+PAIRED = 6
+W2_FIRST = 4 * 24
 HELD = 16
-ROUND1, ROUND2 = 27, 56
+ROUND1, ROUND2 = 23, 56
 
 
 def tile_capsulelayer_kernel(tc, x, route_weights1, route_weights, out):
@@ -50,7 +52,7 @@ def tile_capsulelayer_kernel(tc, x, route_weights1, route_weights, out):
                                 rhs=r_codes.bitcast(FP8X4), rhs_scale=r_scales, start=start, stop=stop)
 
         def keep_clock(codes_512, scales_512, tag):
-            idle_ps = psum.tile([P, NE], F32, name="idle_ps", tag=tag)
+            idle_ps = psum.tile([P, NE], F32, name="idle_ps", tag=tag, bufs=1 if tag == "tot" else 2)
             mx(idle_ps[:], xc[:, 0:P], xs[:, 0:P], codes_512, scales_512)
 
         with ExitStack() as first:
@@ -126,7 +128,7 @@ def tile_capsulelayer_kernel(tc, x, route_weights1, route_weights, out):
 
             def total_mx(h, c):
                 if c == 0:
-                    t_ps = psum.tile([P, 4, P], F32, name="t_ps", tag="tot")
+                    t_ps = psum.tile([P, 4, P], F32, name="t_ps", tag="tot", bufs=1)
                     banks[("f", h, 0)] = t_ps
                 wc, ws = codes[h]
                 cs = slice(c * P, (c + 1) * P)
@@ -137,8 +139,8 @@ def tile_capsulelayer_kernel(tc, x, route_weights1, route_weights, out):
                 p_ps = psum.tile([P, NE], F32, name="p_ps", tag="big")
                 banks[("p", h, j)] = p_ps
                 wc, ws = codes[h]
-                mx(p_ps[:], *x_block(j), wc[:], ws[:])
-                mx(p_ps[:], *x_block(j), wc[:], ws[:])
+                for i in range(2):
+                    mx(p_ps[:], *x_block(j), wc[:], ws[:])
 
             def prior_copy(h, j):
                 if j == 0:
@@ -150,6 +152,9 @@ def tile_capsulelayer_kernel(tc, x, route_weights1, route_weights, out):
                 m = h // HG + (1 if rnd == 1 else 3)
                 return state[m][3][:, j * 32 + h:j * 32 + h + 1]
 
+            def paired(h, rnd):
+                return rnd == 2 and h >= NH - PAIRED
+
             def scale(h, rnd, j):
                 src = tiles[h][:, j, :]
                 if rnd == 1:
@@ -158,19 +163,20 @@ def tile_capsulelayer_kernel(tc, x, route_weights1, route_weights, out):
                 else:
                     dst = src
                 ys[(h, rnd, j)] = dst
-                if j == 0:
+                if paired(h, rnd) and j >= 2:
+                    nc.vector.scalar_tensor_tensor(out=dst, in0=src, scalar=weights_of(h, rnd, j), in1=ys[(h, rnd, j - 2)], op0=ALU.mult, op1=ALU.add)
+                elif j == 0:
                     nc.gpsimd.tensor_scalar(out=dst, in0=src, scalar1=weights_of(h, rnd, j), scalar2=0.0, op0=ALU.mult, op1=ALU.add)
-                elif j == 1 and rnd == 2 and h >= NH - 7:
-                    nc.vector.tensor_scalar(out=dst, in0=src, scalar1=weights_of(h, rnd, j), scalar2=None, op0=ALU.mult)
                 else:
                     nc.scalar.activation(out=dst, in_=src, func=ACT.Copy, scale=weights_of(h, rnd, j))
 
             def fold(h, rnd):
-                f_ps = psum.tile([P, 4, P], F32, name="f_ps", tag="fold")
+                f_ps = psum.tile([P, 4, P], F32, name="f_ps", tag="fold", bufs=3)
                 banks[("f", h, rnd)] = f_ps
+                first_j = 2 if paired(h, rnd) else 0
                 for c in range(4):
-                    for j in range(NJ):
-                        nc.tensor.matmul(f_ps[:, c, :], lhsT=ys[(h, rnd, j)][:, c * P:(c + 1) * P], rhs=ident_f[:], is_transpose=True, start=(j == 0), stop=(j == NJ - 1))
+                    for j in range(first_j, NJ):
+                        nc.tensor.matmul(f_ps[:, c, :], lhsT=ys[(h, rnd, j)][:, c * P:(c + 1) * P], rhs=ident_f[:], is_transpose=True, start=(j == first_j), stop=(j == NJ - 1))
 
             def sums(h, rnd):
                 f_ps = banks[("f", h, rnd)]
@@ -249,70 +255,85 @@ def tile_capsulelayer_kernel(tc, x, route_weights1, route_weights, out):
                 nc.scalar.activation(out=sq[:], in_=of_group, func=ACT.Square)
                 nc.vector.tensor_reduce(out=sqc[:].rearrange("p (a h) -> p a h", a=NA)[:, :, g * HG:(g + 1) * HG], in_=sq[:], axis=AX.X, op=ALU.add)
 
-            def at(tick, offset):
-                h, r = divmod(tick - offset, 4)
-                return h if r == 0 and 0 <= h < NH else None
+            def begin(h, rnd):
+                if rnd == 0:
+                    return 4 * h
+                if rnd == 1:
+                    return 4 * h + ROUND1
+                return 4 * h + ROUND2
+
+            def softmax_begin(m):
+                return 16 * m + 2 if m <= NG else 16 * (m - 3) + 12 + ROUND1 + 9
+
+            def at(tick, rnd, offset):
+                return [h for h in range(NH) if begin(h, rnd) + offset == tick]
 
             with tc.manual_schedule():
-                w2_first = 4 * 30
                 load(1, 0)
                 load(1, 1)
-                for tick in range(-9, 4 * (NH - 1) + ROUND2 + 8):
-                    def run(fn, offset, *more):
-                        h = at(tick, offset)
-                        if h is not None:
+                for tick in range(-10, begin(NH - 1, 2) + 8):
+                    def run(fn, rnd, offset, *more):
+                        for h in at(tick, rnd, offset):
                             fn(h, *more)
 
                     def run2(fn, offset):
-                        m, r = divmod(tick - w2_first - offset, 4)
+                        m, r = divmod(tick - W2_FIRST - offset, 4)
                         if r == 0 and 0 <= m < NC2:
                             fn(2, m)
 
-                    h = at(tick, -13)
-                    if h is not None and h >= 2:
-                        load(1, h)
+                    for h in at(tick, 0, -14):
+                        if h >= 2:
+                            load(1, h)
                     run2(load, -6)
-                    m, k = divmod(tick - 2, 16)
-                    if 1 <= m <= NG + 2 and k <= 5:
-                        softmax_step(m, k)
+                    for m in range(1, NG + 3):
+                        if 0 <= tick - softmax_begin(m) <= 5:
+                            softmax_step(m, tick - softmax_begin(m))
+                    for h in at(tick, 2, 1):
+                        if paired(h, 2):
+                            scale(h, 2, 2)
+                            scale(h, 2, 3)
                     for j in (0, 2):
-                        run(agree, 4 + j // 2, 0, j)
-                        run(agree, ROUND1 + 7 + j // 2, 1, j)
-                    run(sums, 1, 0)
-                    run(sums, ROUND1 + 5, 1)
-                    run(sums, ROUND2 + 5, 2)
+                        run(agree, 0, 4 + j // 2, 0, j)
+                        run(agree, 1, 7 + j // 2, 1, j)
+                    run(sums, 0, -1, 0)
+                    run(sums, 1, 5, 1)
+                    run(sums, 2, 5, 2)
                     for j in (1, 3):
-                        run(agree, 4 + j // 2, 0, j)
-                        run(agree, ROUND1 + 7 + j // 2, 1, j)
+                        run(agree, 0, 4 + j // 2, 0, j)
+                        run(agree, 1, 7 + j // 2, 1, j)
                     for c in range(4):
-                        run(total_mx, c - 3, c)
+                        run(total_mx, 0, c // 2 - 3, c)
                     for j in range(NJ):
-                        run(prior_mx, j, j)
+                        run(prior_mx, 0, j, j)
                     if tick >= 4 * NH:
-                        keep_clock(xc[:], xs[:], "tot")
-                        keep_clock(xc[:], xs[:], "tot")
-                    run(spread, 2, 0)
-                    run(spread, ROUND1 + 6, 1)
-                    run(fold, ROUND1 + 4, 1)
-                    run(fold, ROUND2 + 4, 2)
+                        for i in range(2 if tick < 4 * NH + ROUND1 + 4 and tick % 4 in (0, 3) else 1):
+                            keep_clock(xc[:], xs[:], "tot")
+                    run(spread, 0, 2, 0)
+                    run(spread, 1, 6, 1)
+                    run(fold, 1, 4, 1)
+                    run(fold, 2, 4, 2)
                     for j in range(NJ):
-                        run(scale, ROUND1 + j, 1, j)
-                        run(scale, ROUND2 + j, 2, j)
+                        run(scale, 1, j, 1, j)
+                        for h in at(tick, 2, j):
+                            if not paired(h, 2):
+                                scale(h, 2, j)
+                    for h in at(tick, 2, 0):
+                        if paired(h, 2):
+                            scale(h, 2, 0)
+                            scale(h, 2, 1)
                     for j in range(NJ):
-                        run(prior_copy, j, j)
-                    run(repeat, 1, 0)
-                    run(repeat, ROUND1 + 5, 1)
-                    h = at(tick, -9)
-                    if h is not None:
+                        run(prior_copy, 0, j, j)
+                    run(repeat, 0, -1, 0)
+                    run(repeat, 1, 5, 1)
+                    for h in at(tick, 0, -10):
                         regroup(1, h)
                     run2(regroup, -3)
-                    h = at(tick, -5)
-                    if h is not None:
+                    for h in at(tick, 0, -6):
                         quantize(1, h)
-                    run2(quantize, 1)
-                    h = at(tick, ROUND2 + 6)
-                    if h is not None and h % HG == HG - 1:
-                        squares(h // HG)
+                    run2(quantize, 2)
+                    for h in at(tick, 2, 6):
+                        if h % HG == HG - 1:
+                            squares(h // HG)
 
                 z = state[NG + 2][2]
                 n_ps = psum.tile([P, 2], F32, name="n_ps", tag="sb")

@@ -51,10 +51,6 @@ def tile_capsulelayer_kernel(tc, x, route_weights1, route_weights, out):
             nc.tensor.matmul_mx(out=out_ps, lhsT=l_codes.bitcast(FP8X4), lhsT_scale=l_scales,
                                 rhs=r_codes.bitcast(FP8X4), rhs_scale=r_scales, start=start, stop=stop)
 
-        def keep_clock(codes_512, scales_512, tag):
-            idle_ps = psum.tile([P, NE], F32, name="idle_ps", tag=tag, bufs=1 if tag == "tot" else 2)
-            mx(idle_ps[:], xc[:, 0:P], xs[:, 0:P], codes_512, scales_512)
-
         with ExitStack() as first:
             stage = first.enter_context(tc.tile_pool(name="stage", bufs=2))
             priors = first.enter_context(tc.tile_pool(name="priors", bufs=HELD))
@@ -102,16 +98,17 @@ def tile_capsulelayer_kernel(tc, x, route_weights1, route_weights, out):
                 rows = route_weights1[m].rearrange("(p t) e -> p t e", t=4) if kind == 1 else route_weights[m].rearrange("(t p) f -> p t f", p=P)
                 nc.sync.dma_start(out=raw[:], in_=rows)
 
-            def regroup(kind, m):
-                grouped = stage.tile([P, NE, 4], BF16, name="grouped", tag="grouped", align_bytes=64)
-                groupeds[(kind, m)] = grouped
+            def regroup(kind, m, piece):
+                if piece == 0:
+                    grouped_new = stage.tile([P, NE, 4], BF16, name="grouped", tag="grouped", align_bytes=64)
+                    groupeds[(kind, m)] = grouped_new
+                grouped = groupeds[(kind, m)]
                 raw = raws[(kind, m)]
+                cs = slice(piece * NE // PIECES, (piece + 1) * NE // PIECES)
                 if kind == 1 and m < 2:
-                    nc.vector.tensor_copy(out=grouped[:].rearrange("p (c i) t -> p c t i", i=4), in_=raw[:].rearrange("p t (c i) -> p c t i", i=4))
+                    nc.vector.tensor_copy(out=grouped[:, cs, :].rearrange("p (c i) t -> p c t i", i=4), in_=raw[:, :, cs].rearrange("p t (c i) -> p c t i", i=4))
                 else:
-                    for s in range(PIECES):
-                        cs = slice(s * NE // PIECES, (s + 1) * NE // PIECES)
-                        nc.gpsimd.tensor_scalar(out=grouped[:, cs, :], in0=raw[:, :, cs].rearrange("p t c -> p c t"), scalar1=1.0, scalar2=0.0, op0=ALU.mult, op1=ALU.add)
+                    nc.gpsimd.tensor_scalar(out=grouped[:, cs, :], in0=raw[:, :, cs].rearrange("p t c -> p c t"), scalar1=1.0, scalar2=0.0, op0=ALU.mult, op1=ALU.add)
 
             def quantize(kind, m):
                 if kind == 1:
@@ -128,7 +125,7 @@ def tile_capsulelayer_kernel(tc, x, route_weights1, route_weights, out):
 
             def total_mx(h, c):
                 if c == 0:
-                    t_ps = psum.tile([P, 4, P], F32, name="t_ps", tag="tot", bufs=1)
+                    t_ps = psum.tile([P, 4, P], F32, name="t_ps", tag="tot")
                     banks[("f", h, 0)] = t_ps
                 wc, ws = codes[h]
                 cs = slice(c * P, (c + 1) * P)
@@ -139,8 +136,7 @@ def tile_capsulelayer_kernel(tc, x, route_weights1, route_weights, out):
                 p_ps = psum.tile([P, NE], F32, name="p_ps", tag="big")
                 banks[("p", h, j)] = p_ps
                 wc, ws = codes[h]
-                for i in range(2):
-                    mx(p_ps[:], *x_block(j), wc[:], ws[:])
+                mx(p_ps[:], *x_block(j), wc[:], ws[:])
 
             def prior_copy(h, j):
                 if j == 0:
@@ -158,23 +154,23 @@ def tile_capsulelayer_kernel(tc, x, route_weights1, route_weights, out):
             def scale(h, rnd, j):
                 src = tiles[h][:, j, :]
                 if rnd == 1:
-                    y = work.tile([P, NE], F32, name="y", tag="y", bufs=6)
+                    y = work.tile([P, NE], F32, name="y", tag="y", bufs=8)
                     dst = y[:]
                 else:
                     dst = src
                 ys[(h, rnd, j)] = dst
                 if paired(h, rnd) and j >= 2:
                     nc.vector.scalar_tensor_tensor(out=dst, in0=src, scalar=weights_of(h, rnd, j), in1=ys[(h, rnd, j - 2)], op0=ALU.mult, op1=ALU.add)
-                elif j == 0:
-                    nc.gpsimd.tensor_scalar(out=dst, in0=src, scalar1=weights_of(h, rnd, j), scalar2=0.0, op0=ALU.mult, op1=ALU.add)
                 else:
                     nc.scalar.activation(out=dst, in_=src, func=ACT.Copy, scale=weights_of(h, rnd, j))
 
-            def fold(h, rnd):
-                f_ps = psum.tile([P, 4, P], F32, name="f_ps", tag="fold", bufs=3)
-                banks[("f", h, rnd)] = f_ps
+            def fold(h, rnd, part):
+                if part == 0:
+                    new_ps = psum.tile([P, 4, P], F32, name="new_ps", tag="fold")
+                    banks[("f", h, rnd)] = new_ps
+                f_ps = banks[("f", h, rnd)]
                 first_j = 2 if paired(h, rnd) else 0
-                for c in range(4):
+                for c in (2 * part, 2 * part + 1):
                     for j in range(first_j, NJ):
                         nc.tensor.matmul(f_ps[:, c, :], lhsT=ys[(h, rnd, j)][:, c * P:(c + 1) * P], rhs=ident_f[:], is_transpose=True, start=(j == first_j), stop=(j == NJ - 1))
 
@@ -263,7 +259,7 @@ def tile_capsulelayer_kernel(tc, x, route_weights1, route_weights, out):
                 return 4 * h + ROUND2
 
             def softmax_begin(m):
-                return 16 * m + 2 if m <= NG else 16 * (m - 3) + 12 + ROUND1 + 9
+                return 16 * m + 2 if m <= NG else 16 * (m - 3) + 12 + ROUND1 + 13
 
             def at(tick, rnd, offset):
                 return [h for h in range(NH) if begin(h, rnd) + offset == tick]
@@ -271,20 +267,20 @@ def tile_capsulelayer_kernel(tc, x, route_weights1, route_weights, out):
             with tc.manual_schedule():
                 load(1, 0)
                 load(1, 1)
-                for tick in range(-10, begin(NH - 1, 2) + 8):
+                for tick in range(-11, begin(NH - 1, 2) + 11):
                     def run(fn, rnd, offset, *more):
                         for h in at(tick, rnd, offset):
                             fn(h, *more)
 
-                    def run2(fn, offset):
+                    def run2(fn, offset, *more):
                         m, r = divmod(tick - W2_FIRST - offset, 4)
                         if r == 0 and 0 <= m < NC2:
-                            fn(2, m)
+                            fn(2, m, *more)
 
-                    for h in at(tick, 0, -14):
+                    for h in at(tick, 0, -15):
                         if h >= 2:
                             load(1, h)
-                    run2(load, -6)
+                    run2(load, -13)
                     for m in range(1, NG + 3):
                         if 0 <= tick - softmax_begin(m) <= 5:
                             softmax_step(m, tick - softmax_begin(m))
@@ -294,24 +290,22 @@ def tile_capsulelayer_kernel(tc, x, route_weights1, route_weights, out):
                             scale(h, 2, 3)
                     for j in (0, 2):
                         run(agree, 0, 4 + j // 2, 0, j)
-                        run(agree, 1, 7 + j // 2, 1, j)
+                        run(agree, 1, 11 + j // 2, 1, j)
                     run(sums, 0, -1, 0)
-                    run(sums, 1, 5, 1)
-                    run(sums, 2, 5, 2)
+                    run(sums, 1, 7, 1)
+                    run(sums, 2, 8, 2)
                     for j in (1, 3):
                         run(agree, 0, 4 + j // 2, 0, j)
-                        run(agree, 1, 7 + j // 2, 1, j)
+                        run(agree, 1, 11 + j // 2, 1, j)
                     for c in range(4):
-                        run(total_mx, 0, c // 2 - 3, c)
+                        run(total_mx, 0, c - 5, c)
                     for j in range(NJ):
                         run(prior_mx, 0, j, j)
-                    if tick >= 4 * NH:
-                        for i in range(2 if tick < 4 * NH + ROUND1 + 4 and tick % 4 in (0, 3) else 1):
-                            keep_clock(xc[:], xs[:], "tot")
                     run(spread, 0, 2, 0)
-                    run(spread, 1, 6, 1)
-                    run(fold, 1, 4, 1)
-                    run(fold, 2, 4, 2)
+                    run(spread, 1, 10, 1)
+                    for part in range(2):
+                        run(fold, 1, 5 + part, 1, part)
+                        run(fold, 2, 6 + part, 2, part)
                     for j in range(NJ):
                         run(scale, 1, j, 1, j)
                         for h in at(tick, 2, j):
@@ -321,17 +315,18 @@ def tile_capsulelayer_kernel(tc, x, route_weights1, route_weights, out):
                         if paired(h, 2):
                             scale(h, 2, 0)
                             scale(h, 2, 1)
+                    run(repeat, 0, 0, 0)
+                    run(repeat, 1, 8, 1)
                     for j in range(NJ):
                         run(prior_copy, 0, j, j)
-                    run(repeat, 0, -1, 0)
-                    run(repeat, 1, 5, 1)
-                    for h in at(tick, 0, -10):
-                        regroup(1, h)
-                    run2(regroup, -3)
-                    for h in at(tick, 0, -6):
+                    for h in at(tick, 0, -7):
                         quantize(1, h)
-                    run2(quantize, 2)
-                    for h in at(tick, 2, 6):
+                    run2(quantize, -5)
+                    for s in range(PIECES):
+                        for h in at(tick, 0, -11 + s // 2):
+                            regroup(1, h, s)
+                        run2(regroup, -9 + s // 2, s)
+                    for h in at(tick, 2, 9):
                         if h % HG == HG - 1:
                             squares(h // HG)
 
@@ -414,9 +409,6 @@ def tile_capsulelayer_kernel(tc, x, route_weights1, route_weights, out):
                 fbanks[(rnd, c)] = tr_ps
                 for k in range(4):
                     nc.tensor.transpose(tr_ps[:, k, :], y2s[(rnd, c)][:, k * P:(k + 1) * P], ident_f[:])
-                if rnd == 1:
-                    keep_clock(w2c[:, c, :], w2s[:, c, :], "n")
-                    keep_clock(w2c[:, c, :], w2s[:, c, :], "n")
 
         def sums2(rnd, c):
             if rnd < 2:

@@ -39,6 +39,14 @@ def tile_capsulelayer_kernel(tc, x, route_weights1, route_weights, out):
         nc.vector.memset(ones_f[:], 1.0)
         half = const.tile([P, 1], F32, name="half")
         nc.vector.memset(half[:], 0.5)
+        minus_one = const.tile([P, 1], F32, name="minus_one")
+        nc.vector.memset(minus_one[:], -1.0)
+        blk_ones = const.tile([P, P], F32, name="blk_ones")
+        nc.vector.memset(blk_ones[:], 0.0)
+        for a in range(NA):
+            blk = slice(32 * a, 32 * a + 32)
+            nc.vector.memset(blk_ones[blk, blk], 1.0)
+
         xc = const.tile([P, NA * NB], U32, name="xc", align_bytes=64)
         xs = const.tile([P, NA * NB], U8, name="xs", align_bytes=64)
         w2c = const.tile([P, NC2, NE], U32, name="w2c", align_bytes=64)
@@ -50,6 +58,17 @@ def tile_capsulelayer_kernel(tc, x, route_weights1, route_weights, out):
         def mx(out_ps, l_codes, l_scales, r_codes, r_scales, start=True, stop=True):
             nc.tensor.matmul_mx(out=out_ps, lhsT=l_codes.bitcast(FP8X4), lhsT_scale=l_scales,
                                 rhs=r_codes.bitcast(FP8X4), rhs_scale=r_scales, start=start, stop=stop)
+
+        def factor(pool, n, z):
+            den = pool.tile([P, 1], F32, name="den", tag="den")
+            nc.gpsimd.tensor_scalar(out=den[:], in0=z[:], scalar1=z[:, 0:1], scalar2=n[:, 0:1], op0=ALU.mult, op1=ALU.add)
+            rden = pool.tile([P, 1], F32, name="rden", tag="rden")
+            nc.gpsimd.tensor_tensor(out=rden[:], in0=den[:], in1=minus_one[:], op=ALU.pow)
+            rt = pool.tile([P, 1], F32, name="rt", tag="rt")
+            nc.gpsimd.tensor_tensor(out=rt[:], in0=n[:], in1=half[:], op=ALU.pow)
+            f = pool.tile([P, 1], F32, name="f", tag="f")
+            nc.gpsimd.tensor_tensor(out=f[:], in0=rt[:], in1=rden[:], op=ALU.mult)
+            return f
 
         with ExitStack() as first:
             stage = first.enter_context(tc.tile_pool(name="stage", bufs=2))
@@ -79,8 +98,12 @@ def tile_capsulelayer_kernel(tc, x, route_weights1, route_weights, out):
                 xt_ps = psum.tile([P, 4, NB], BF16, name="xt_ps", tag="big")
                 for t in range(4):
                     nc.tensor.transpose(xt_ps[:, t, :], x_sb[:, a, :].rearrange("b (p t) -> b t p", t=4)[:, t, :], ident_b[:])
-                nc.vector.tensor_copy(out=xg[:].rearrange("p (j a q) t -> p a j q t", j=NJ, a=NA)[:, a],
-                                      in_=xt_ps[:].rearrange("p t (j q) -> p j q t", j=NJ))
+                dst = xg[:].rearrange("p (j a q) t -> p a j q t", j=NJ, a=NA)[:, a]
+                src = xt_ps[:].rearrange("p t (j q) -> p j q t", j=NJ)
+                if a % 2:
+                    nc.scalar.copy(out=dst, in_=src)
+                else:
+                    nc.vector.tensor_copy(out=dst, in_=src)
             nc.vector.quantize_mx(out=xc[:].bitcast(FP8X4), scales=xs[:], in_=xg[:].rearrange("p w t -> p (w t)"))
 
             raws = {}
@@ -105,7 +128,7 @@ def tile_capsulelayer_kernel(tc, x, route_weights1, route_weights, out):
                 grouped = groupeds[(kind, m)]
                 raw = raws[(kind, m)]
                 cs = slice(piece * NE // PIECES, (piece + 1) * NE // PIECES)
-                if kind == 1 and m < 2:
+                if kind == 1 and m < 3:
                     nc.vector.tensor_copy(out=grouped[:, cs, :].rearrange("p (c i) t -> p c t i", i=4), in_=raw[:, :, cs].rearrange("p t (c i) -> p c t i", i=4))
                 else:
                     nc.gpsimd.tensor_scalar(out=grouped[:, cs, :], in0=raw[:, :, cs].rearrange("p t c -> p c t"), scalar1=1.0, scalar2=0.0, op0=ALU.mult, op1=ALU.add)
@@ -204,52 +227,48 @@ def tile_capsulelayer_kernel(tc, x, route_weights1, route_weights, out):
 
             small = {}
 
-            def softmax_step(m, k):
+            def softmax_step(m, k, part):
                 lt_old, e_old, z_old = state[m - 1][0], state[m - 1][1], state[m - 1][2]
                 u = us[(m - 1) % 2]
-                if k == 0:
+                if (k, part) == (0, 0):
                     ut = work.tile([P, P], F32, name="ut", tag="ut", align_bytes=64)
                     small["ut"] = ut
                     nc.vector.transpose(ut[:], u[:])
                     nc.gpsimd.memset(u[:], 0.0)
+                elif (k, part) == (0, 1):
                     n = work.tile([P, 1], F32, name="n", tag="n")
                     small["n"] = n
                     eu = work.tile([P, P], F32, name="eu", tag="eu")
                     nc.vector.scalar_tensor_tensor(out=eu[:], in0=small["ut"][:], scalar=1.0, in1=e_old[:], op0=ALU.mult, op1=ALU.mult, accum_out=n[:])
-                elif k == 1:
-                    rt = work.tile([P, 1], F32, name="rt", tag="rt")
-                    small["rt"] = rt
-                    nc.gpsimd.tensor_tensor(out=rt[:], in0=small["n"][:], in1=half[:], op=ALU.pow)
-                    den = work.tile([P, 1], F32, name="den", tag="den")
-                    nc.vector.tensor_scalar(out=den[:], in0=z_old[:], scalar1=z_old[:, 0:1], scalar2=small["n"][:, 0:1], op0=ALU.mult, op1=ALU.add)
-                    rden = work.tile([P, 1], F32, name="rden", tag="rden")
-                    small["rden"] = rden
-                    nc.vector.reciprocal(out=rden[:], in_=den[:])
-                elif k == 3:
-                    f = work.tile([P, 1], F32, name="f", tag="f")
-                    nc.vector.tensor_tensor(out=f[:], in0=small["rt"][:], in1=small["rden"][:], op=ALU.mult)
+                elif (k, part) == (1, 2):
+                    small["f"] = factor(work, small["n"], z_old)
+                elif (k, part) == (3, 0):
                     lt = work.tile([P, P], F32, name="lt", tag="lt")
                     small["lt"] = lt
-                    nc.vector.scalar_tensor_tensor(out=lt[:], in0=small["ut"][:], scalar=f[:, 0:1], in1=lt_old[:], op0=ALU.mult, op1=ALU.add)
+                    nc.vector.scalar_tensor_tensor(out=lt[:], in0=small["ut"][:], scalar=small["f"][:, 0:1], in1=lt_old[:], op0=ALU.mult, op1=ALU.add)
+                elif (k, part) == (3, 1):
                     negmax = work.tile([P, 1], F32, name="negmax", tag="negmax")
                     small["negmax"] = negmax
-                    nc.vector.tensor_reduce(out=negmax[:], in_=lt[:], axis=AX.X, op=ALU.max, negate=True)
-                elif k == 4:
+                    nc.vector.tensor_reduce(out=negmax[:], in_=small["lt"][:], axis=AX.X, op=ALU.max, negate=True)
+                elif (k, part) == (3, 3):
                     e = work.tile([P, P], F32, name="e", tag="e", align_bytes=64)
                     small["e"] = e
                     z = work.tile([P, 1], F32, name="z", tag="z")
                     small["z"] = z
                     nc.scalar.activation(out=e[:], in_=small["lt"][:], func=ACT.Exp, bias=small["negmax"][:, 0:1], scale=1.0, accum_out=z[:])
-                elif k == 5:
+                elif (k, part) == (4, 1):
                     et = work.tile([P, P], F32, name="et", tag="et", bufs=4, align_bytes=64)
                     nc.vector.transpose(et[:], small["e"][:])
                     state[m] = (small["lt"], small["e"], small["z"], et)
 
-            def squares(g):
+            def squares(g, part):
                 of_group = s2[:].rearrange("p (a h) c -> p a h c", a=NA)[:, :, g * HG:(g + 1) * HG, :]
-                sq = work.tile([P, NA, HG, 4], F32, name="sq", tag="sq")
-                nc.scalar.activation(out=sq[:], in_=of_group, func=ACT.Square)
-                nc.vector.tensor_reduce(out=sqc[:].rearrange("p (a h) -> p a h", a=NA)[:, :, g * HG:(g + 1) * HG], in_=sq[:], axis=AX.X, op=ALU.add)
+                if part == 0:
+                    sq = work.tile([P, NA, HG, 4], F32, name="sq", tag="sq")
+                    small["sq"] = sq
+                    nc.scalar.activation(out=sq[:], in_=of_group, func=ACT.Square)
+                    return
+                nc.vector.tensor_reduce(out=sqc[:].rearrange("p (a h) -> p a h", a=NA)[:, :, g * HG:(g + 1) * HG], in_=small["sq"][:], axis=AX.X, op=ALU.add)
 
             def begin(h, rnd):
                 if rnd == 0:
@@ -281,9 +300,12 @@ def tile_capsulelayer_kernel(tc, x, route_weights1, route_weights, out):
                         if h >= 2:
                             load(1, h)
                     run2(load, -13)
-                    for m in range(1, NG + 3):
-                        if 0 <= tick - softmax_begin(m) <= 5:
-                            softmax_step(m, tick - softmax_begin(m))
+                    def softmax(part):
+                        for m in range(1, NG + 3):
+                            if 0 <= tick - softmax_begin(m) <= 4:
+                                softmax_step(m, tick - softmax_begin(m), part)
+
+                    softmax(0)
                     for h in at(tick, 2, 1):
                         if paired(h, 2):
                             scale(h, 2, 2)
@@ -291,6 +313,7 @@ def tile_capsulelayer_kernel(tc, x, route_weights1, route_weights, out):
                     for j in (0, 2):
                         run(agree, 0, 4 + j // 2, 0, j)
                         run(agree, 1, 11 + j // 2, 1, j)
+                    softmax(1)
                     run(sums, 0, -1, 0)
                     run(sums, 1, 7, 1)
                     run(sums, 2, 8, 2)
@@ -306,6 +329,7 @@ def tile_capsulelayer_kernel(tc, x, route_weights1, route_weights, out):
                     for part in range(2):
                         run(fold, 1, 5 + part, 1, part)
                         run(fold, 2, 6 + part, 2, part)
+                    softmax(2)
                     for j in range(NJ):
                         run(scale, 1, j, 1, j)
                         for h in at(tick, 2, j):
@@ -319,6 +343,7 @@ def tile_capsulelayer_kernel(tc, x, route_weights1, route_weights, out):
                     run(repeat, 1, 8, 1)
                     for j in range(NJ):
                         run(prior_copy, 0, j, j)
+                    softmax(3)
                     for h in at(tick, 0, -7):
                         quantize(1, h)
                     run2(quantize, -5)
@@ -326,9 +351,10 @@ def tile_capsulelayer_kernel(tc, x, route_weights1, route_weights, out):
                         for h in at(tick, 0, -11 + s // 2):
                             regroup(1, h, s)
                         run2(regroup, -9 + s // 2, s)
-                    for h in at(tick, 2, 9):
-                        if h % HG == HG - 1:
-                            squares(h // HG)
+                    for part in range(2):
+                        for h in at(tick, 2, 9 + part):
+                            if h % HG == HG - 1:
+                                squares(h // HG, part)
 
                 z = state[NG + 2][2]
                 n_ps = psum.tile([P, 2], F32, name="n_ps", tag="sb")
@@ -382,16 +408,25 @@ def tile_capsulelayer_kernel(tc, x, route_weights1, route_weights, out):
         def softmax_no(rnd, c):
             return 2 * rnd + c // HALF + 1
 
+        def direct(rnd, c):
+            return rnd == 1
+
         def open2(rnd, c):
             if rnd == 0:
-                qt_ps = psum.tile([P, 4, P], F32, name="qt_ps", tag="f", bufs=3)
-                fbanks[(rnd, c)] = qt_ps
-                for k in range(4):
+                if not direct(rnd, c):
+                    qt_ps = psum.tile([P, 4, P], F32, name="qt_ps", tag="f", bufs=3)
+                    fbanks[(rnd, c)] = qt_ps
+                for k in range(0 if direct(rnd, c) else 4):
                     cs = slice(k * P, (k + 1) * P)
-                    mx(qt_ps[:, k, :], w2c[:, c, cs], w2s[:, c, cs], oc[:], os_[:])
+                    mx(fbanks[(rnd, c)][:, k, :], w2c[:, c, cs], w2s[:, c, cs], oc[:], os_[:])
                 q_ps = psum.tile([P, NE], F32, name="q_ps", tag="n")
                 mx(q_ps[:], oc[:], os_[:], w2c[:, c, :], w2s[:, c, :])
                 nbanks[c] = q_ps
+            elif direct(rnd, c):
+                w = state2[softmax_no(rnd - 1, c)][3][:, c:c + 1]
+                wblk = second.tile([P, P], F32, name="wblk", tag="wblk", bufs=6)
+                y2s[(rnd, c)] = wblk
+                nc.scalar.activation(out=wblk[:], in_=blk_ones[:], func=ACT.Copy, scale=w)
             else:
                 y = second.tile([P, NE], F32, name="y2", tag="y2", bufs=3)
                 y2s[(rnd, c)] = y
@@ -404,13 +439,15 @@ def tile_capsulelayer_kernel(tc, x, route_weights1, route_weights, out):
         def turn2(rnd, c):
             if rnd == 0:
                 nc.scalar.copy(out=priors2[:, c, :], in_=nbanks[c][:])
-            else:
+            elif not direct(rnd, c):
                 tr_ps = psum.tile([P, 4, P], F32, name="tr_ps", tag="f", bufs=3)
                 fbanks[(rnd, c)] = tr_ps
                 for k in range(4):
                     nc.tensor.transpose(tr_ps[:, k, :], y2s[(rnd, c)][:, k * P:(k + 1) * P], ident_f[:])
 
         def sums2(rnd, c):
+            if direct(rnd, c):
+                return
             if rnd < 2:
                 scol = second.tile([P, 4, NA], F32, name="scol2", tag="scol2", bufs=3)
                 scol2s[(rnd, c)] = scol
@@ -420,7 +457,7 @@ def tile_capsulelayer_kernel(tc, x, route_weights1, route_weights, out):
             nc.vector.tensor_reduce(out=dst, in_=fbanks[(rnd, c)][:].rearrange("p k (a h) -> p k a h", a=NA), axis=AX.X, op=ALU.add)
 
         def repeat2(rnd, c):
-            if rnd < 2:
+            if rnd < 2 and not direct(rnd, c):
                 bc = second.tile([P, 4, NA, 32], F32, name="bc2", tag="bc2", bufs=3)
                 bc2s[(rnd, c)] = bc
                 nc.scalar.copy(out=bc[:], in_=scol2s[(rnd, c)][:].unsqueeze(3).to_broadcast([P, 4, NA, 32]))
@@ -429,7 +466,9 @@ def tile_capsulelayer_kernel(tc, x, route_weights1, route_weights, out):
             if rnd < 2:
                 sb_ps = psum.tile([P, NE], F32, name="sb_ps2", tag="sb")
                 sb2s[(rnd, c)] = sb_ps
-                for k in range(4):
+                if direct(rnd, c):
+                    nc.tensor.matmul(sb_ps[:], lhsT=(y2s[(rnd, c)] if rnd else blk_ones)[:], rhs=priors2[:, c, :], start=True, stop=True)
+                for k in range(0 if direct(rnd, c) else 4):
                     nc.tensor.transpose(sb_ps[:, k * P:(k + 1) * P], bc2s[(rnd, c)][:, k].rearrange("p a h -> p (a h)"), ident_f[:])
 
         def agree2(rnd, c):

@@ -20,7 +20,7 @@ NJ = 4
 HG = 4
 NG = NH // HG
 PIECES = 4
-PAIRED = 6
+PAIRED = 5
 W2_FIRST = 4 * 24
 HELD = 16
 ROUND1, ROUND2 = 23, 56
@@ -130,6 +130,8 @@ def tile_capsulelayer_kernel(tc, x, route_weights1, route_weights, out):
                 cs = slice(piece * NE // PIECES, (piece + 1) * NE // PIECES)
                 if kind == 1 and m < 3:
                     nc.vector.tensor_copy(out=grouped[:, cs, :].rearrange("p (c i) t -> p c t i", i=4), in_=raw[:, :, cs].rearrange("p t (c i) -> p c t i", i=4))
+                elif kind == 2 and piece == PIECES - 1:
+                    nc.scalar.copy(out=grouped[:, cs, :].rearrange("p (c i) t -> p c t i", i=4), in_=raw[:, :, cs].rearrange("p t (c i) -> p c t i", i=4))
                 else:
                     nc.gpsimd.tensor_scalar(out=grouped[:, cs, :], in0=raw[:, :, cs].rearrange("p t c -> p c t"), scalar1=1.0, scalar2=0.0, op0=ALU.mult, op1=ALU.add)
 
@@ -146,14 +148,22 @@ def tile_capsulelayer_kernel(tc, x, route_weights1, route_weights, out):
             def x_block(j):
                 return xc[:, j * P:(j + 1) * P], xs[:, j * P:(j + 1) * P]
 
-            def total_mx(h, c):
-                if c == 0:
-                    t_ps = psum.tile([P, 4, P], F32, name="t_ps", tag="tot")
-                    banks[("f", h, 0)] = t_ps
+            def total_mx(h, j):
+                if j == 0:
+                    t_ps = psum.tile([P, NE], F32, name="t_ps", tag="tot")
+                    banks[("t", h)] = t_ps
                 wc, ws = codes[h]
-                cs = slice(c * P, (c + 1) * P)
-                for j in range(NJ):
-                    mx(banks[("f", h, 0)][:, c, :], wc[:, cs], ws[:, cs], *x_block(j), start=(j == 0), stop=(j == NJ - 1))
+                mx(banks[("t", h)][:], *x_block(j), wc[:], ws[:], start=(j == 0), stop=(j == NJ - 1))
+
+            def total_copy(h):
+                tot = work.tile([P, NE], F32, name="tot", tag="bc")
+                ys[("tot", h)] = tot
+                nc.scalar.copy(out=tot[:], in_=banks[("t", h)][:])
+
+            def total_spread(h):
+                sb_ps = psum.tile([P, NE], F32, name="sb_ps", tag="sb")
+                sbs[(h, 0)] = sb_ps
+                nc.tensor.matmul(sb_ps[:], lhsT=blk_ones[:], rhs=ys[("tot", h)][:], start=True, stop=True)
 
             def prior_mx(h, j):
                 p_ps = psum.tile([P, NE], F32, name="p_ps", tag="big")
@@ -314,21 +324,20 @@ def tile_capsulelayer_kernel(tc, x, route_weights1, route_weights, out):
                         run(agree, 0, 4 + j // 2, 0, j)
                         run(agree, 1, 11 + j // 2, 1, j)
                     softmax(1)
-                    run(sums, 0, -1, 0)
                     run(sums, 1, 7, 1)
                     run(sums, 2, 8, 2)
                     for j in (1, 3):
                         run(agree, 0, 4 + j // 2, 0, j)
                         run(agree, 1, 11 + j // 2, 1, j)
-                    for c in range(4):
-                        run(total_mx, 0, c - 5, c)
                     for j in range(NJ):
                         run(prior_mx, 0, j, j)
-                    run(spread, 0, 2, 0)
-                    run(spread, 1, 10, 1)
                     for part in range(2):
                         run(fold, 1, 5 + part, 1, part)
                         run(fold, 2, 6 + part, 2, part)
+                    run(total_spread, 0, 2)
+                    run(spread, 1, 10, 1)
+                    for j in range(NJ):
+                        run(total_mx, 0, j - 5, j)
                     softmax(2)
                     for j in range(NJ):
                         run(scale, 1, j, 1, j)
@@ -339,7 +348,7 @@ def tile_capsulelayer_kernel(tc, x, route_weights1, route_weights, out):
                         if paired(h, 2):
                             scale(h, 2, 0)
                             scale(h, 2, 1)
-                    run(repeat, 0, 0, 0)
+                    run(total_copy, 0, 0)
                     run(repeat, 1, 8, 1)
                     for j in range(NJ):
                         run(prior_copy, 0, j, j)

@@ -21,7 +21,7 @@ HG = 4
 NG = NH // HG
 PIECES = 4
 PAIRED = 5
-W2_FIRST = 4 * 24
+W2_FIRST = 4 * 27
 HELD = 16
 ROUND1, ROUND2 = 23, 56
 
@@ -54,6 +54,19 @@ def tile_capsulelayer_kernel(tc, x, route_weights1, route_weights, out):
         og = const.tile([P, NA * NH, 4], BF16, name="og", align_bytes=64)
         oc = const.tile([P, NA * NH], U32, name="oc", align_bytes=64)
         os_ = const.tile([P, NA * NH], U8, name="os_", align_bytes=64)
+
+        def late_factor(pool, n_ps, zz):
+            n = pool.tile([P, 1], F32, name="n", tag="n")
+            nc.vector.tensor_copy(out=n[:], in_=n_ps[:, 0:1])
+            rt = pool.tile([P, 1], F32, name="rt", tag="rt")
+            nc.gpsimd.tensor_tensor(out=rt[:], in0=n[:], in1=half[:], op=ALU.pow)
+            den = pool.tile([P, 1], F32, name="den", tag="den")
+            nc.vector.tensor_scalar(out=den[:], in0=n_ps[:, 0:1], scalar1=1.0, scalar2=zz[:, 0:1], op0=ALU.mult, op1=ALU.add)
+            rden = pool.tile([P, 1], F32, name="rden", tag="rden")
+            nc.vector.reciprocal(out=rden[:], in_=den[:])
+            f = pool.tile([P, 1], F32, name="f", tag="f")
+            nc.vector.tensor_tensor(out=f[:], in0=rt[:], in1=rden[:], op=ALU.mult)
+            return f
 
         def mx(out_ps, l_codes, l_scales, r_codes, r_scales, start=True, stop=True):
             nc.tensor.matmul_mx(out=out_ps, lhsT=l_codes.bitcast(FP8X4), lhsT_scale=l_scales,
@@ -91,16 +104,17 @@ def tile_capsulelayer_kernel(tc, x, route_weights1, route_weights, out):
             sqc = work.tile([P, NA * NH], F32, name="sqc", bufs=1)
             state = {0: (lt0, e0, z0, None)}
 
-            x_sb = stage.tile([P, NA, ND], BF16, name="x_sb", tag="raw", bufs=3)
-            nc.sync.dma_start(out=x_sb[:], in_=x.rearrange("a b d -> b a d"))
-            xg = stage.tile([P, NA * NB, 4], BF16, name="xg", tag="grouped", align_bytes=64)
+            x_sb = stage.tile([P, NJ, ND], BF16, name="x_sb", tag="raw", bufs=3)
             for a in range(NA):
-                xt_ps = psum.tile([P, 4, NB], BF16, name="xt_ps", tag="big")
+                nc.sync.dma_start(out=x_sb[32 * a:32 * a + 32], in_=x[a].rearrange("(j q) d -> q j d", j=NJ))
+            xg = stage.tile([P, NA * NB, 4], BF16, name="xg", tag="grouped", align_bytes=64)
+            for j in range(NJ):
+                xt_ps = psum.tile([P, 4, P], BF16, name="xt_ps", tag="fold" if j % 2 else "big")
                 for t in range(4):
-                    nc.tensor.transpose(xt_ps[:, t, :], x_sb[:, a, :].rearrange("b (p t) -> b t p", t=4)[:, t, :], ident_b[:])
-                dst = xg[:].rearrange("p (j a q) t -> p a j q t", j=NJ, a=NA)[:, a]
-                src = xt_ps[:].rearrange("p t (j q) -> p j q t", j=NJ)
-                if a % 2:
+                    nc.tensor.transpose(xt_ps[:, t, :], x_sb[:, j, :].rearrange("b (p t) -> b t p", t=4)[:, t, :], ident_b[:])
+                dst = xg[:, j * P:(j + 1) * P, :]
+                src = xt_ps[:].rearrange("p t w -> p w t")
+                if j % 2:
                     nc.scalar.copy(out=dst, in_=src)
                 else:
                     nc.vector.tensor_copy(out=dst, in_=src)
@@ -128,9 +142,9 @@ def tile_capsulelayer_kernel(tc, x, route_weights1, route_weights, out):
                 grouped = groupeds[(kind, m)]
                 raw = raws[(kind, m)]
                 cs = slice(piece * NE // PIECES, (piece + 1) * NE // PIECES)
-                if kind == 1 and m < 3:
+                if kind == 1 and m < 3 and piece < PIECES // 2:
                     nc.vector.tensor_copy(out=grouped[:, cs, :].rearrange("p (c i) t -> p c t i", i=4), in_=raw[:, :, cs].rearrange("p t (c i) -> p c t i", i=4))
-                elif kind == 2 and piece == PIECES - 1:
+                elif kind == 1 and m < 3 or piece == PIECES - 1 and (kind == 2 or m < 8):
                     nc.scalar.copy(out=grouped[:, cs, :].rearrange("p (c i) t -> p c t i", i=4), in_=raw[:, :, cs].rearrange("p t (c i) -> p c t i", i=4))
                 else:
                     nc.gpsimd.tensor_scalar(out=grouped[:, cs, :], in0=raw[:, :, cs].rearrange("p t c -> p c t"), scalar1=1.0, scalar2=0.0, op0=ALU.mult, op1=ALU.add)
@@ -166,7 +180,7 @@ def tile_capsulelayer_kernel(tc, x, route_weights1, route_weights, out):
                 nc.tensor.matmul(sb_ps[:], lhsT=blk_ones[:], rhs=ys[("tot", h)][:], start=True, stop=True)
 
             def prior_mx(h, j):
-                p_ps = psum.tile([P, NE], F32, name="p_ps", tag="big")
+                p_ps = psum.tile([P, NE], F32, name="p_ps", tag="fold" if j % 2 and begin(h, 0) + j < begin(0, 1) - 3 else "big")
                 banks[("p", h, j)] = p_ps
                 wc, ws = codes[h]
                 mx(p_ps[:], *x_block(j), wc[:], ws[:])
@@ -244,14 +258,14 @@ def tile_capsulelayer_kernel(tc, x, route_weights1, route_weights, out):
                     ut = work.tile([P, P], F32, name="ut", tag="ut", align_bytes=64)
                     small["ut"] = ut
                     nc.vector.transpose(ut[:], u[:])
-                    nc.gpsimd.memset(u[:], 0.0)
                 elif (k, part) == (0, 1):
                     n = work.tile([P, 1], F32, name="n", tag="n")
                     small["n"] = n
                     eu = work.tile([P, P], F32, name="eu", tag="eu")
                     nc.vector.scalar_tensor_tensor(out=eu[:], in0=small["ut"][:], scalar=1.0, in1=e_old[:], op0=ALU.mult, op1=ALU.mult, accum_out=n[:])
-                elif (k, part) == (1, 2):
+                elif (k, part) == (0, 2):
                     small["f"] = factor(work, small["n"], z_old)
+                    nc.gpsimd.memset(u[:], 0.0)
                 elif (k, part) == (3, 0):
                     lt = work.tile([P, P], F32, name="lt", tag="lt")
                     small["lt"] = lt
@@ -335,7 +349,7 @@ def tile_capsulelayer_kernel(tc, x, route_weights1, route_weights, out):
                         run(fold, 1, 5 + part, 1, part)
                         run(fold, 2, 6 + part, 2, part)
                     run(total_spread, 0, 2)
-                    run(spread, 1, 10, 1)
+                    run(spread, 1, 9, 1)
                     for j in range(NJ):
                         run(total_mx, 0, j - 5, j)
                     softmax(2)
@@ -357,27 +371,20 @@ def tile_capsulelayer_kernel(tc, x, route_weights1, route_weights, out):
                         quantize(1, h)
                     run2(quantize, -5)
                     for s in range(PIECES):
-                        for h in at(tick, 0, -11 + s // 2):
+                        for h in at(tick, 0, -11):
                             regroup(1, h, s)
-                        run2(regroup, -9 + s // 2, s)
+                        run2(regroup, -9, s)
                     for part in range(2):
                         for h in at(tick, 2, 9 + part):
                             if h % HG == HG - 1:
                                 squares(h // HG, part)
 
                 z = state[NG + 2][2]
+                zz = work.tile([P, 1], F32, name="zz", bufs=1)
+                nc.vector.tensor_tensor(out=zz[:], in0=z[:], in1=z[:], op=ALU.mult)
                 n_ps = psum.tile([P, 2], F32, name="n_ps", tag="sb")
                 nc.tensor.matmul(n_ps[:], lhsT=sqc[:], rhs=ones_f[:], start=True, stop=True)
-                n = work.tile([P, 1], F32, name="n", tag="n")
-                nc.vector.tensor_copy(out=n[:], in_=n_ps[:, 0:1])
-                rt = work.tile([P, 1], F32, name="rt", tag="rt")
-                nc.gpsimd.tensor_tensor(out=rt[:], in0=n[:], in1=half[:], op=ALU.pow)
-                den = work.tile([P, 1], F32, name="den", tag="den")
-                nc.vector.tensor_scalar(out=den[:], in0=z[:], scalar1=z[:, 0:1], scalar2=n[:, 0:1], op0=ALU.mult, op1=ALU.add)
-                rden = work.tile([P, 1], F32, name="rden", tag="rden")
-                nc.vector.reciprocal(out=rden[:], in_=den[:])
-                f = work.tile([P, 1], F32, name="f", tag="f")
-                nc.vector.tensor_tensor(out=f[:], in0=rt[:], in1=rden[:], op=ALU.mult)
+                f = late_factor(work, n_ps, zz)
                 fb_ps = psum.tile([P, P], F32, name="fb_ps", tag="sb")
                 nc.tensor.transpose(fb_ps[:], f[:, 0:1].to_broadcast([P, P]), ident_f[:])
                 nc.vector.tensor_tensor(out=og[:], in0=s2[:], in1=fb_ps[:].unsqueeze(2).to_broadcast([P, NA * NH, 4]), op=ALU.mult)
@@ -399,14 +406,9 @@ def tile_capsulelayer_kernel(tc, x, route_weights1, route_weights, out):
             u = second.tile([P, 32], F32, name="ub%d" % m, bufs=1, align_bytes=64)
             nc.vector.memset(u[:], 0.0)
             us2[m] = u
-        sqcs = []
-        s2s = []
-        for half_no in range(2):
-            sqc = second.tile([P, P], F32, name="sqcb%d" % half_no, bufs=1)
-            nc.vector.memset(sqc[:], 0.0)
-            sqcs.append(sqc)
-            s2 = second.tile([P, HALF, 4, NA], F32, name="s2b%d" % half_no, bufs=1)
-            s2s.append(s2)
+        sqc = second.tile([P, P], F32, name="sqcb", bufs=1)
+        nc.vector.memset(sqc[:], 0.0)
+        s2 = second.tile([P, NC2, 4, NA], F32, name="s2b", bufs=1)
         fbanks = {}
         nbanks = {}
         y2s = {}
@@ -431,16 +433,18 @@ def tile_capsulelayer_kernel(tc, x, route_weights1, route_weights, out):
                 q_ps = psum.tile([P, NE], F32, name="q_ps", tag="n")
                 mx(q_ps[:], oc[:], os_[:], w2c[:, c, :], w2s[:, c, :])
                 nbanks[c] = q_ps
-            elif direct(rnd, c):
+
+        def scale2(rnd, c):
+            if direct(rnd, c):
                 w = state2[softmax_no(rnd - 1, c)][3][:, c:c + 1]
                 wblk = second.tile([P, P], F32, name="wblk", tag="wblk", bufs=6)
                 y2s[(rnd, c)] = wblk
                 nc.scalar.activation(out=wblk[:], in_=blk_ones[:], func=ACT.Copy, scale=w)
-            else:
-                y = second.tile([P, NE], F32, name="y2", tag="y2", bufs=3)
+            elif rnd:
+                y = second.tile([P, NE], F32, name="y2", tag="y2", bufs=5)
                 y2s[(rnd, c)] = y
                 w = state2[softmax_no(rnd - 1, c)][3][:, c:c + 1]
-                if c % 2:
+                if c % 2 and c >= HALF:
                     nc.gpsimd.tensor_scalar(out=y[:], in0=priors2[:, c, :], scalar1=w, scalar2=0.0, op0=ALU.mult, op1=ALU.add)
                 else:
                     nc.scalar.activation(out=y[:], in_=priors2[:, c, :], func=ACT.Copy, scale=w)
@@ -462,7 +466,7 @@ def tile_capsulelayer_kernel(tc, x, route_weights1, route_weights, out):
                 scol2s[(rnd, c)] = scol
                 dst = scol[:]
             else:
-                dst = s2s[c // HALF][:, c % HALF]
+                dst = s2[:, c]
             nc.vector.tensor_reduce(out=dst, in_=fbanks[(rnd, c)][:].rearrange("p k (a h) -> p k a h", a=NA), axis=AX.X, op=ALU.add)
 
         def repeat2(rnd, c):
@@ -488,17 +492,6 @@ def tile_capsulelayer_kernel(tc, x, route_weights1, route_weights, out):
 
         tiny = {}
 
-        def factor2(n, z_old):
-            rt = second.tile([P, 1], F32, name="rtb", tag="rtb")
-            nc.gpsimd.tensor_tensor(out=rt[:], in0=n[:], in1=half[:], op=ALU.pow)
-            den = second.tile([P, 1], F32, name="denb", tag="denb")
-            nc.vector.tensor_scalar(out=den[:], in0=z_old[:], scalar1=z_old[:, 0:1], scalar2=n[:, 0:1], op0=ALU.mult, op1=ALU.add)
-            rden = second.tile([P, 1], F32, name="rdenb", tag="rdenb")
-            nc.vector.reciprocal(out=rden[:], in_=den[:])
-            f = second.tile([P, 1], F32, name="fb", tag="fb")
-            nc.vector.tensor_tensor(out=f[:], in0=rt[:], in1=rden[:], op=ALU.mult)
-            return f
-
         def softmax2_step(m, k):
             lt_old, e_old, z_old = state2[m - 1][0], state2[m - 1][1], state2[m - 1][2]
             if k == 0:
@@ -510,56 +503,98 @@ def tile_capsulelayer_kernel(tc, x, route_weights1, route_weights, out):
                 eu = second.tile([P, 32], F32, name="eub", tag="eub")
                 nc.vector.scalar_tensor_tensor(out=eu[:], in0=ut[:], scalar=1.0, in1=e_old[:], op0=ALU.mult, op1=ALU.mult, accum_out=n[:])
             elif k == 1:
-                tiny["f"] = factor2(tiny["n"], z_old)
-            elif k == 2:
+                if m in (1, 2):
+                    tiny["f"] = factor(second, tiny["n"], z_old)
+                    return
+                rt = second.tile([P, 1], F32, name="rt", tag="rt")
+                nc.gpsimd.tensor_tensor(out=rt[:], in0=tiny["n"][:], in1=half[:], op=ALU.pow)
+                den = second.tile([P, 1], F32, name="den", tag="den")
+                nc.vector.tensor_scalar(out=den[:], in0=z_old[:], scalar1=z_old[:, 0:1], scalar2=tiny["n"][:, 0:1], op0=ALU.mult, op1=ALU.add)
+                rden = second.tile([P, 1], F32, name="rden", tag="rden")
+                nc.vector.reciprocal(out=rden[:], in_=den[:])
+                tiny["rt"], tiny["rden"] = rt, rden
+            elif k == 3:
+                if m not in (1, 2):
+                    f = second.tile([P, 1], F32, name="f", tag="f")
+                    nc.vector.tensor_tensor(out=f[:], in0=tiny["rt"][:], in1=tiny["rden"][:], op=ALU.mult)
+                    tiny["f"] = f
                 lt = second.tile([P, 32], F32, name="ltb", tag="ltb")
+                tiny["lt"] = lt
                 nc.vector.scalar_tensor_tensor(out=lt[:], in0=tiny["ut"][:], scalar=tiny["f"][:, 0:1], in1=lt_old[:], op0=ALU.mult, op1=ALU.add)
+            elif k == 4:
+                lt = tiny["lt"]
                 negmax = second.tile([P, 1], F32, name="negmaxb", tag="negmaxb")
                 nc.vector.tensor_reduce(out=negmax[:], in_=lt[:], axis=AX.X, op=ALU.max, negate=True)
                 e = second.tile([P, 32], F32, name="eb", tag="eb", align_bytes=64)
                 z = second.tile([P, 1], F32, name="zb", tag="zb")
                 nc.scalar.activation(out=e[:], in_=lt[:], func=ACT.Exp, bias=negmax[:, 0:1], scale=1.0, accum_out=z[:])
                 tiny["new"] = (lt, e, z)
-            else:
+            elif k == 5:
                 et = second.tile([P, 32], F32, name="etb", tag="etb", bufs=3, align_bytes=64)
                 nc.vector.transpose(et[:], tiny["new"][1][:])
                 state2[m] = tiny["new"] + (et,)
 
-        out_rows = out.rearrange("c a (k f) -> (c a k) f", f=P)
+        def squares2(half_no, part):
+            of_half = slice(half_no * HALF, (half_no + 1) * HALF)
+            if part == 0:
+                sq = second.tile([P, HALF, 4, NA], F32, name="sqb", tag="sqb")
+                tiny["sq"] = sq
+                nc.scalar.activation(out=sq[:], in_=s2[:, of_half], func=ACT.Square)
+            else:
+                nc.vector.tensor_reduce(out=sqc[:].rearrange("p (a c) -> p a c", a=NA)[:, :, of_half],
+                                        in_=tiny["sq"][:].rearrange("p c k a -> p a c k"), axis=AX.X, op=ALU.add)
 
-        def finish(half_no):
-            s2, sqc = s2s[half_no], sqcs[half_no]
-            sq = second.tile([P, HALF, 4, NA], F32, name="sqb", tag="sqb")
-            nc.scalar.activation(out=sq[:], in_=s2[:], func=ACT.Square)
-            nc.vector.tensor_reduce(out=sqc[:].rearrange("p (a c) -> p a c", a=NA)[:, :, half_no * HALF:(half_no + 1) * HALF],
-                                    in_=sq[:].rearrange("p c k a -> p a c k"), axis=AX.X, op=ALU.add)
+        def finish():
+            out_rows = out.rearrange("c a (k f) -> (c a k) f", f=P)
+            z = state2[4][2]
+            zz = second.tile([P, 1], F32, name="zz2", bufs=1)
+            nc.vector.tensor_tensor(out=zz[:], in0=z[:], in1=z[:], op=ALU.mult)
+            squares2(1, 0)
+            squares2(1, 1)
             n_ps = psum.tile([P, 2], F32, name="n2_ps", tag="t", bufs=1)
             nc.tensor.matmul(n_ps[:], lhsT=sqc[:], rhs=ones_f[:], start=True, stop=True)
-            n = second.tile([P, 1], F32, name="nb", tag="nb")
-            nc.vector.tensor_copy(out=n[:], in_=n_ps[:, 0:1])
-            f = factor2(n, state2[4][2])
+            f = late_factor(second, n_ps, zz)
             fb_ps = psum.tile([P, P], F32, name="fb2_ps", tag="t", bufs=1)
             nc.tensor.transpose(fb_ps[:], f[:, 0:1].to_broadcast([P, P]), ident_f[:])
-            o = second.tile([P, HALF, NA, 4], F32, name="o", tag="o")
-            own = fb_ps[:].rearrange("p (a c) -> p c a", a=NA)[:, half_no * HALF:(half_no + 1) * HALF, :]
-            nc.vector.tensor_tensor(out=o[:], in0=s2[:].rearrange("p c k a -> p c a k"), in1=own.unsqueeze(3).to_broadcast([P, HALF, NA, 4]), op=ALU.mult)
-            ot_ps = psum.tile([P, P], F32, name="ot_ps", tag="t", bufs=1)
-            nc.tensor.transpose(ot_ps[:], o[:].rearrange("p c a k -> p (c a k)"), ident_f[:])
-            res = second.tile([P, P], F32, name="res", tag="res")
-            nc.scalar.copy(out=res[:], in_=ot_ps[:])
-            nc.sync.dma_start(out=out_rows[half_no * P:(half_no + 1) * P, :], in_=res[:])
+            for half_no in range(2):
+                of_half = slice(half_no * HALF, (half_no + 1) * HALF)
+                o = second.tile([P, HALF, NA, 4], F32, name="o", tag="o")
+                own = fb_ps[:].rearrange("p (a c) -> p c a", a=NA)[:, of_half, :]
+                nc.vector.tensor_tensor(out=o[:], in0=s2[:, of_half].rearrange("p c k a -> p c a k"), in1=own.unsqueeze(3).to_broadcast([P, HALF, NA, 4]), op=ALU.mult)
+                ot_ps = psum.tile([P, P], F32, name="ot_ps", tag="n")
+                nc.tensor.transpose(ot_ps[:], o[:].rearrange("p c a k -> p (c a k)"), ident_f[:])
+                res = second.tile([P, P], F32, name="res", tag="res")
+                nc.scalar.copy(out=res[:], in_=ot_ps[:])
+                nc.sync.dma_start(out=out_rows[half_no * P:(half_no + 1) * P, :], in_=res[:])
 
+        LAGS = {open2: (0,), turn2: (1, 0, 1), sums2: (2, 2, 2), repeat2: (3, 3, 3), spread2: (4, 1, 4), agree2: (5, 2, 5), scale2: (0, 0, 0)}
         with tc.manual_schedule():
             for tick in range(3 * NC2 + 2):
-                def item(n):
-                    return divmod(n, NC2) if 0 <= n < 3 * NC2 else None
+                def run(fn):
+                    for rnd, lag in enumerate(LAGS[fn]):
+                        c = tick - lag - NC2 * rnd
+                        if 0 <= c < NC2:
+                            fn(rnd, c)
 
-                m, k = divmod(tick - 5, HALF)
-                if 1 <= m <= 4 and k < 4:
-                    softmax2_step(m, k)
-                for lag, fn in ((2, sums2), (5, agree2), (3, repeat2), (4, spread2), (1, turn2), (0, open2)):
-                    if item(tick - lag):
-                        fn(*item(tick - lag))
-                if tick == 2 * NC2 + HALF + 4:
-                    finish(0)
-            finish(1)
+                def softmax2(k, delay):
+                    for m in range(1, 5):
+                        if tick - delay == HALF * m + (5 if m < 3 else 2):
+                            softmax2_step(m, k)
+
+                softmax2(0, 0)
+                softmax2(3, 2)
+
+                run(sums2)
+                softmax2(4, 2)
+                run(agree2)
+                softmax2(5, 3)
+                softmax2(1, 0)
+                run(repeat2)
+                run(spread2)
+                run(turn2)
+                run(open2)
+                run(scale2)
+                for part in range(2):
+                    if tick == 2 * NC2 + HALF + 2 + part:
+                        squares2(0, part)
+            finish()

@@ -22,6 +22,7 @@ NG = NH // HG
 PIECES = 4
 PAIRED = 5
 W2_FIRST = 4 * 27
+LAST = 10
 HELD = 16
 ROUND1, ROUND2 = 23, 56
 
@@ -144,7 +145,7 @@ def tile_capsulelayer_kernel(tc, x, route_weights1, route_weights, out):
                 cs = slice(piece * NE // PIECES, (piece + 1) * NE // PIECES)
                 if kind == 1 and m < 3 and piece < PIECES // 2:
                     nc.vector.tensor_copy(out=grouped[:, cs, :].rearrange("p (c i) t -> p c t i", i=4), in_=raw[:, :, cs].rearrange("p t (c i) -> p c t i", i=4))
-                elif kind == 1 and m < 3 or piece == PIECES - 1 and (kind == 2 or m < 8):
+                elif kind == 1 and m < 3 or piece == PIECES - 1 and m < 8:
                     nc.scalar.copy(out=grouped[:, cs, :].rearrange("p (c i) t -> p c t i", i=4), in_=raw[:, :, cs].rearrange("p t (c i) -> p c t i", i=4))
                 else:
                     nc.gpsimd.tensor_scalar(out=grouped[:, cs, :], in0=raw[:, :, cs].rearrange("p t c -> p c t"), scalar1=1.0, scalar2=0.0, op0=ALU.mult, op1=ALU.add)
@@ -208,6 +209,8 @@ def tile_capsulelayer_kernel(tc, x, route_weights1, route_weights, out):
                 ys[(h, rnd, j)] = dst
                 if paired(h, rnd) and j >= 2:
                     nc.vector.scalar_tensor_tensor(out=dst, in0=src, scalar=weights_of(h, rnd, j), in1=ys[(h, rnd, j - 2)], op0=ALU.mult, op1=ALU.add)
+                elif rnd == 1 and j == 0 and h >= NH - LAST:
+                    nc.gpsimd.tensor_scalar(out=dst, in0=src, scalar1=weights_of(h, rnd, j), scalar2=0.0, op0=ALU.mult, op1=ALU.add)
                 else:
                     nc.scalar.activation(out=dst, in_=src, func=ACT.Copy, scale=weights_of(h, rnd, j))
 

from contextlib import ExitStack

import concourse.mybir as mybir
from concourse.masks import make_identity

FP8X4 = mybir.dt.float8_e4m3fn_x4
BF16 = mybir.dt.bfloat16
F32 = mybir.dt.float32
U32 = mybir.dt.uint32
U8 = mybir.dt.uint8
ALU = mybir.AluOpType
ACT = mybir.ActivationFunctionType
AX = mybir.AxisListType

P = 128
NA, NB, ND, NE, NH, NC2 = 4, 128, 512, 512, 32, 16
FLOPS = 2 * (NA * NB * ND * NE * NH + NA * NH * NE * NE * NC2)

NJ = 4
HG = 4
NG = NH // HG
PIECES = 4
PAIRED = 5
W2_FIRST = 4 * 27
LAST = 10
HELD = 16
ROUND1, ROUND2 = 23, 56


def tile_capsulelayer_kernel(tc, x, route_weights1, route_weights, out):
    nc = tc.nc
    with ExitStack() as ctx:
        const = ctx.enter_context(tc.tile_pool(name="const", bufs=1))

        ident_f = const.tile([P, P], F32, name="ident_f")
        make_identity(nc, ident_f[:])
        ident_b = const.tile([P, P], BF16, name="ident_b")
        make_identity(nc, ident_b[:])
        ones_f = const.tile([P, 2], F32, name="ones_f")
        nc.vector.memset(ones_f[:], 1.0)
        half = const.tile([P, 1], F32, name="half")
        nc.vector.memset(half[:], 0.5)
        minus_one = const.tile([P, 1], F32, name="minus_one")
        nc.vector.memset(minus_one[:], -1.0)
        blk_ones = const.tile([P, P], F32, name="blk_ones")
        nc.vector.memset(blk_ones[:], 0.0)
        for a in range(NA):
            blk = slice(32 * a, 32 * a + 32)
            nc.vector.memset(blk_ones[blk, blk], 1.0)

        xc = const.tile([P, NA * NB], U32, name="xc", align_bytes=64)
        xs = const.tile([P, NA * NB], U8, name="xs", align_bytes=64)
        w2c = const.tile([P, NC2, NE], U32, name="w2c", align_bytes=64)
        w2s = const.tile([P, NC2, NE], U8, name="w2s", align_bytes=64)
        og = const.tile([P, NA * NH, 4], BF16, name="og", align_bytes=64)
        oc = const.tile([P, NA * NH], U32, name="oc", align_bytes=64)
        os_ = const.tile([P, NA * NH], U8, name="os_", align_bytes=64)

        def late_factor(pool, n_ps, zz):
            n = pool.tile([P, 1], F32, name="n", tag="n")
            nc.vector.tensor_copy(out=n[:], in_=n_ps[:, 0:1])
            rt = pool.tile([P, 1], F32, name="rt", tag="rt")
            nc.gpsimd.tensor_tensor(out=rt[:], in0=n[:], in1=half[:], op=ALU.pow)
            den = pool.tile([P, 1], F32, name="den", tag="den")
            nc.vector.tensor_scalar(out=den[:], in0=n_ps[:, 0:1], scalar1=1.0, scalar2=zz[:, 0:1], op0=ALU.mult, op1=ALU.add)
            rden = pool.tile([P, 1], F32, name="rden", tag="rden")
            nc.vector.reciprocal(out=rden[:], in_=den[:])
            f = pool.tile([P, 1], F32, name="f", tag="f")
            nc.vector.tensor_tensor(out=f[:], in0=rt[:], in1=rden[:], op=ALU.mult)
            return f

        def mx(out_ps, l_codes, l_scales, r_codes, r_scales, start=True, stop=True):
            nc.tensor.matmul_mx(out=out_ps, lhsT=l_codes.bitcast(FP8X4), lhsT_scale=l_scales,
                                rhs=r_codes.bitcast(FP8X4), rhs_scale=r_scales, start=start, stop=stop)

        def factor(pool, n, z):
            den = pool.tile([P, 1], F32, name="den", tag="den")
            nc.gpsimd.tensor_scalar(out=den[:], in0=z[:], scalar1=z[:, 0:1], scalar2=n[:, 0:1], op0=ALU.mult, op1=ALU.add)
            rden = pool.tile([P, 1], F32, name="rden", tag="rden")
            nc.gpsimd.tensor_tensor(out=rden[:], in0=den[:], in1=minus_one[:], op=ALU.pow)
            rt = pool.tile([P, 1], F32, name="rt", tag="rt")
            nc.gpsimd.tensor_tensor(out=rt[:], in0=n[:], in1=half[:], op=ALU.pow)
            f = pool.tile([P, 1], F32, name="f", tag="f")
            nc.gpsimd.tensor_tensor(out=f[:], in0=rt[:], in1=rden[:], op=ALU.mult)
            return f

        with ExitStack() as first:
            stage = first.enter_context(tc.tile_pool(name="stage", bufs=2))
            priors = first.enter_context(tc.tile_pool(name="priors", bufs=HELD))
            work = first.enter_context(tc.tile_pool(name="work", bufs=2))
            psum = first.enter_context(tc.psum_pool(name="psum1", bufs=2))

            lt0 = work.tile([P, P], F32, name="lt0", bufs=1, align_bytes=64)
            nc.vector.memset(lt0[:], 0.0)
            e0 = work.tile([P, P], F32, name="e0", bufs=1, align_bytes=64)
            nc.vector.memset(e0[:], 1.0)
            z0 = work.tile([P, 1], F32, name="z0", bufs=1)
            nc.vector.memset(z0[:], float(NB))
            us = []
            for i in range(2):
                u = work.tile([P, P], F32, name="u%d" % i, bufs=1, align_bytes=64)
                nc.vector.memset(u[:], 0.0)
                us.append(u)
            s2 = work.tile([P, NA * NH, 4], F32, name="s2", bufs=1)
            sqc = work.tile([P, NA * NH], F32, name="sqc", bufs=1)
            state = {0: (lt0, e0, z0, None)}

            x_sb = stage.tile([P, NJ, ND], BF16, name="x_sb", tag="raw", bufs=3)
            for a in range(NA):
                nc.sync.dma_start(out=x_sb[32 * a:32 * a + 32], in_=x[a].rearrange("(j q) d -> q j d", j=NJ))
            xg = stage.tile([P, NA * NB, 4], BF16, name="xg", tag="grouped", align_bytes=64)
            for j in range(NJ):
                xt_ps = psum.tile([P, 4, P], BF16, name="xt_ps", tag="fold" if j % 2 else "big")
                for t in range(4):
                    nc.tensor.transpose(xt_ps[:, t, :], x_sb[:, j, :].rearrange("b (p t) -> b t p", t=4)[:, t, :], ident_b[:])
                dst = xg[:, j * P:(j + 1) * P, :]
                src = xt_ps[:].rearrange("p t w -> p w t")
                if j % 2:
                    nc.scalar.copy(out=dst, in_=src)
                else:
                    nc.vector.tensor_copy(out=dst, in_=src)
            nc.vector.quantize_mx(out=xc[:].bitcast(FP8X4), scales=xs[:], in_=xg[:].rearrange("p w t -> p (w t)"))

            raws = {}
            groupeds = {}
            codes = {}
            tiles = {}
            banks = {}
            ys = {}
            sbs = {}
            scols = {}

            def load(kind, m):
                raw = stage.tile([P, 4, NE], BF16, name="raw", tag="raw", bufs=3)
                raws[(kind, m)] = raw
                rows = route_weights1[m].rearrange("(p t) e -> p t e", t=4) if kind == 1 else route_weights[m].rearrange("(t p) f -> p t f", p=P)
                nc.sync.dma_start(out=raw[:], in_=rows)

            def regroup(kind, m, piece):
                if piece == 0:
                    grouped_new = stage.tile([P, NE, 4], BF16, name="grouped", tag="grouped", align_bytes=64)
                    groupeds[(kind, m)] = grouped_new
                grouped = groupeds[(kind, m)]
                raw = raws[(kind, m)]
                cs = slice(piece * NE // PIECES, (piece + 1) * NE // PIECES)
                if kind == 1 and m < 3 and piece < PIECES // 2:
                    nc.vector.tensor_copy(out=grouped[:, cs, :].rearrange("p (c i) t -> p c t i", i=4), in_=raw[:, :, cs].rearrange("p t (c i) -> p c t i", i=4))
                elif kind == 1 and m < 3 or piece == PIECES - 1 and m < 8:
                    nc.scalar.copy(out=grouped[:, cs, :].rearrange("p (c i) t -> p c t i", i=4), in_=raw[:, :, cs].rearrange("p t (c i) -> p c t i", i=4))
                else:
                    nc.gpsimd.tensor_scalar(out=grouped[:, cs, :], in0=raw[:, :, cs].rearrange("p t c -> p c t"), scalar1=1.0, scalar2=0.0, op0=ALU.mult, op1=ALU.add)

            def quantize(kind, m):
                if kind == 1:
                    wc = stage.tile([P, NE], U32, name="wc", tag="wc", bufs=3, align_bytes=64)
                    ws = stage.tile([P, NE], U8, name="ws", tag="ws", bufs=3, align_bytes=64)
                    codes[m] = (wc, ws)
                    cw, sw = wc[:], ws[:]
                else:
                    cw, sw = w2c[:, m, :], w2s[:, m, :]
                nc.vector.quantize_mx(out=cw.bitcast(FP8X4), scales=sw, in_=groupeds[(kind, m)][:].rearrange("p w t -> p (w t)"))

            def x_block(j):
                return xc[:, j * P:(j + 1) * P], xs[:, j * P:(j + 1) * P]

            def total_mx(h, j):
                if j == 0:
                    t_ps = psum.tile([P, NE], F32, name="t_ps", tag="tot")
                    banks[("t", h)] = t_ps
                wc, ws = codes[h]
                mx(banks[("t", h)][:], *x_block(j), wc[:], ws[:], start=(j == 0), stop=(j == NJ - 1))

            def total_copy(h):
                tot = work.tile([P, NE], F32, name="tot", tag="bc")
                ys[("tot", h)] = tot
                nc.scalar.copy(out=tot[:], in_=banks[("t", h)][:])

            def total_spread(h):
                sb_ps = psum.tile([P, NE], F32, name="sb_ps", tag="sb")
                sbs[(h, 0)] = sb_ps
                nc.tensor.matmul(sb_ps[:], lhsT=blk_ones[:], rhs=ys[("tot", h)][:], start=True, stop=True)

            def prior_mx(h, j):
                p_ps = psum.tile([P, NE], F32, name="p_ps", tag="fold" if j % 2 and begin(h, 0) + j < begin(0, 1) - 3 else "big")
                banks[("p", h, j)] = p_ps
                wc, ws = codes[h]
                mx(p_ps[:], *x_block(j), wc[:], ws[:])

            def prior_copy(h, j):
                if j == 0:
                    pn = priors.tile([P, NJ, NE], F32, name="pn", tag="pn")
                    tiles[h] = pn
                nc.scalar.copy(out=tiles[h][:, j, :], in_=banks[("p", h, j)][:])

            def weights_of(h, rnd, j):
                m = h // HG + (1 if rnd == 1 else 3)
                return state[m][3][:, j * 32 + h:j * 32 + h + 1]

            def paired(h, rnd):
                return rnd == 2 and h >= NH - PAIRED

            def scale(h, rnd, j):
                src = tiles[h][:, j, :]
                if rnd == 1:
                    y = work.tile([P, NE], F32, name="y", tag="y", bufs=8)
                    dst = y[:]
                else:
                    dst = src
                ys[(h, rnd, j)] = dst
                if paired(h, rnd) and j >= 2:
                    nc.vector.scalar_tensor_tensor(out=dst, in0=src, scalar=weights_of(h, rnd, j), in1=ys[(h, rnd, j - 2)], op0=ALU.mult, op1=ALU.add)
                elif rnd == 1 and j == 0 and h >= NH - LAST:
                    nc.gpsimd.tensor_scalar(out=dst, in0=src, scalar1=weights_of(h, rnd, j), scalar2=0.0, op0=ALU.mult, op1=ALU.add)
                else:
                    nc.scalar.activation(out=dst, in_=src, func=ACT.Copy, scale=weights_of(h, rnd, j))

            def fold(h, rnd, part):
                if part == 0:
                    new_ps = psum.tile([P, 4, P], F32, name="new_ps", tag="fold")
                    banks[("f", h, rnd)] = new_ps
                f_ps = banks[("f", h, rnd)]
                first_j = 2 if paired(h, rnd) else 0
                for c in (2 * part, 2 * part + 1):
                    for j in range(first_j, NJ):
                        nc.tensor.matmul(f_ps[:, c, :], lhsT=ys[(h, rnd, j)][:, c * P:(c + 1) * P], rhs=ident_f[:], is_transpose=True, start=(j == first_j), stop=(j == NJ - 1))

            def sums(h, rnd):
                f_ps = banks[("f", h, rnd)]
                if rnd < 2:
                    scol = work.tile([P, 4, NA], F32, name="scol", tag="scol", bufs=3)
                    scols[(h, rnd)] = scol
                    dst = scol[:]
                else:
                    dst = s2[:].rearrange("p (a h) c -> p h c a", a=NA)[:, h]
                nc.vector.tensor_reduce(out=dst, in_=f_ps[:].rearrange("p c (a q) -> p c a q", a=NA), axis=AX.X, op=ALU.add)

            def repeat(h, rnd):
                bc = work.tile([P, 4, NA, 32], F32, name="bc", tag="bc")
                ys[("bc", h, rnd)] = bc
                nc.scalar.copy(out=bc[:], in_=scols[(h, rnd)][:].unsqueeze(3).to_broadcast([P, 4, NA, 32]))

            def spread(h, rnd):
                sb_ps = psum.tile([P, NE], F32, name="sb_ps", tag="sb")
                sbs[(h, rnd)] = sb_ps
                bc = ys[("bc", h, rnd)]
                for c in range(4):
                    nc.tensor.transpose(sb_ps[:, c * P:(c + 1) * P], bc[:, c].rearrange("p a q -> p (a q)"), ident_f[:])

            def agree(h, rnd, j):
                u = us[h // HG % 2]
                waste = work.tile([P, NE], BF16, name="waste", tag="waste")
                nc.vector.scalar_tensor_tensor(out=waste[:], in0=tiles[h][:, j, :], scalar=1.0, in1=sbs[(h, rnd)][:], op0=ALU.mult, op1=ALU.mult,
                                               accum_out=u[:, j * 32 + h:j * 32 + h + 1])

            small = {}

            def softmax_step(m, k, part):
                lt_old, e_old, z_old = state[m - 1][0], state[m - 1][1], state[m - 1][2]
                u = us[(m - 1) % 2]
                if (k, part) == (0, 0):
                    ut = work.tile([P, P], F32, name="ut", tag="ut", align_bytes=64)
                    small["ut"] = ut
                    nc.vector.transpose(ut[:], u[:])
                elif (k, part) == (0, 1):
                    n = work.tile([P, 1], F32, name="n", tag="n")
                    small["n"] = n
                    eu = work.tile([P, P], F32, name="eu", tag="eu")
                    nc.vector.scalar_tensor_tensor(out=eu[:], in0=small["ut"][:], scalar=1.0, in1=e_old[:], op0=ALU.mult, op1=ALU.mult, accum_out=n[:])
                elif (k, part) == (0, 2):
                    small["f"] = factor(work, small["n"], z_old)
                    nc.gpsimd.memset(u[:], 0.0)
                elif (k, part) == (3, 0):
                    lt = work.tile([P, P], F32, name="lt", tag="lt")
                    small["lt"] = lt
                    nc.vector.scalar_tensor_tensor(out=lt[:], in0=small["ut"][:], scalar=small["f"][:, 0:1], in1=lt_old[:], op0=ALU.mult, op1=ALU.add)
                elif (k, part) == (3, 1):
                    negmax = work.tile([P, 1], F32, name="negmax", tag="negmax")
                    small["negmax"] = negmax
                    nc.vector.tensor_reduce(out=negmax[:], in_=small["lt"][:], axis=AX.X, op=ALU.max, negate=True)
                elif (k, part) == (3, 3):
                    e = work.tile([P, P], F32, name="e", tag="e", align_bytes=64)
                    small["e"] = e
                    z = work.tile([P, 1], F32, name="z", tag="z")
                    small["z"] = z
                    nc.scalar.activation(out=e[:], in_=small["lt"][:], func=ACT.Exp, bias=small["negmax"][:, 0:1], scale=1.0, accum_out=z[:])
                elif (k, part) == (4, 1):
                    et = work.tile([P, P], F32, name="et", tag="et", bufs=4, align_bytes=64)
                    nc.vector.transpose(et[:], small["e"][:])
                    state[m] = (small["lt"], small["e"], small["z"], et)

            def squares(g, part):
                of_group = s2[:].rearrange("p (a h) c -> p a h c", a=NA)[:, :, g * HG:(g + 1) * HG, :]
                if part == 0:
                    sq = work.tile([P, NA, HG, 4], F32, name="sq", tag="sq")
                    small["sq"] = sq
                    nc.scalar.activation(out=sq[:], in_=of_group, func=ACT.Square)
                    return
                nc.vector.tensor_reduce(out=sqc[:].rearrange("p (a h) -> p a h", a=NA)[:, :, g * HG:(g + 1) * HG], in_=small["sq"][:], axis=AX.X, op=ALU.add)

            def begin(h, rnd):
                if rnd == 0:
                    return 4 * h
                if rnd == 1:
                    return 4 * h + ROUND1
                return 4 * h + ROUND2

            def softmax_begin(m):
                return 16 * m + 2 if m <= NG else 16 * (m - 3) + 12 + ROUND1 + 13

            def at(tick, rnd, offset):
                return [h for h in range(NH) if begin(h, rnd) + offset == tick]

            with tc.manual_schedule():
                load(1, 0)
                load(1, 1)
                for tick in range(-11, begin(NH - 1, 2) + 11):
                    def run(fn, rnd, offset, *more):
                        for h in at(tick, rnd, offset):
                            fn(h, *more)

                    def run2(fn, offset, *more):
                        m, r = divmod(tick - W2_FIRST - offset, 4)
                        if r == 0 and 0 <= m < NC2:
                            fn(2, m, *more)

                    for h in at(tick, 0, -15):
                        if h >= 2:
                            load(1, h)
                    run2(load, -13)
                    def softmax(part):
                        for m in range(1, NG + 3):
                            if 0 <= tick - softmax_begin(m) <= 4:
                                softmax_step(m, tick - softmax_begin(m), part)

                    softmax(0)
                    for h in at(tick, 2, 1):
                        if paired(h, 2):
                            scale(h, 2, 2)
                            scale(h, 2, 3)
                    for j in (0, 2):
                        run(agree, 0, 4 + j // 2, 0, j)
                        run(agree, 1, 11 + j // 2, 1, j)
                    softmax(1)
                    run(sums, 1, 7, 1)
                    run(sums, 2, 8, 2)
                    for j in (1, 3):
                        run(agree, 0, 4 + j // 2, 0, j)
                        run(agree, 1, 11 + j // 2, 1, j)
                    for j in range(NJ):
                        run(prior_mx, 0, j, j)
                    for part in range(2):
                        run(fold, 1, 5 + part, 1, part)
                        run(fold, 2, 6 + part, 2, part)
                    run(total_spread, 0, 2)
                    run(spread, 1, 9, 1)
                    for j in range(NJ):
                        run(total_mx, 0, j - 5, j)
                    softmax(2)
                    for j in range(NJ):
                        run(scale, 1, j, 1, j)
                        for h in at(tick, 2, j):
                            if not paired(h, 2):
                                scale(h, 2, j)
                    for h in at(tick, 2, 0):
                        if paired(h, 2):
                            scale(h, 2, 0)
                            scale(h, 2, 1)
                    run(total_copy, 0, 0)
                    run(repeat, 1, 8, 1)
                    for j in range(NJ):
                        run(prior_copy, 0, j, j)
                    softmax(3)
                    for h in at(tick, 0, -7):
                        quantize(1, h)
                    run2(quantize, -5)
                    for s in range(PIECES):
                        for h in at(tick, 0, -11):
                            regroup(1, h, s)
                        run2(regroup, -9, s)
                    for part in range(2):
                        for h in at(tick, 2, 9 + part):
                            if h % HG == HG - 1:
                                squares(h // HG, part)

                z = state[NG + 2][2]
                zz = work.tile([P, 1], F32, name="zz", bufs=1)
                nc.vector.tensor_tensor(out=zz[:], in0=z[:], in1=z[:], op=ALU.mult)
                n_ps = psum.tile([P, 2], F32, name="n_ps", tag="sb")
                nc.tensor.matmul(n_ps[:], lhsT=sqc[:], rhs=ones_f[:], start=True, stop=True)
                f = late_factor(work, n_ps, zz)
                fb_ps = psum.tile([P, P], F32, name="fb_ps", tag="sb")
                nc.tensor.transpose(fb_ps[:], f[:, 0:1].to_broadcast([P, P]), ident_f[:])
                nc.vector.tensor_tensor(out=og[:], in0=s2[:], in1=fb_ps[:].unsqueeze(2).to_broadcast([P, NA * NH, 4]), op=ALU.mult)

        nc.vector.quantize_mx(out=oc[:].bitcast(FP8X4), scales=os_[:], in_=og[:].rearrange("p w t -> p (w t)"))
        psum = ctx.enter_context(tc.psum_pool(name="psum2", bufs=2))
        second = ctx.enter_context(tc.tile_pool(name="second", bufs=2))
        HALF = NC2 // 2
        priors2 = second.tile([P, NC2, NE], F32, name="priors2", bufs=1)
        lt0 = second.tile([P, 32], F32, name="lt0b", bufs=1, align_bytes=64)
        nc.vector.memset(lt0[:], 0.0)
        e0 = second.tile([P, 32], F32, name="e0b", bufs=1, align_bytes=64)
        nc.vector.memset(e0[:], 1.0)
        z0 = second.tile([P, 1], F32, name="z0b", bufs=1)
        nc.vector.memset(z0[:], float(NH))
        state2 = {0: (lt0, e0, z0, None)}
        us2 = {}
        for m in range(1, 5):
            u = second.tile([P, 32], F32, name="ub%d" % m, bufs=1, align_bytes=64)
            nc.vector.memset(u[:], 0.0)
            us2[m] = u
        sqc = second.tile([P, P], F32, name="sqcb", bufs=1)
        nc.vector.memset(sqc[:], 0.0)
        s2 = second.tile([P, NC2, 4, NA], F32, name="s2b", bufs=1)
        fbanks = {}
        nbanks = {}
        y2s = {}
        scol2s = {}
        bc2s = {}
        sb2s = {}

        def softmax_no(rnd, c):
            return 2 * rnd + c // HALF + 1

        def direct(rnd, c):
            return rnd == 1

        def open2(rnd, c):
            if rnd == 0:
                if not direct(rnd, c):
                    qt_ps = psum.tile([P, 4, P], F32, name="qt_ps", tag="f", bufs=3)
                    fbanks[(rnd, c)] = qt_ps
                for k in range(0 if direct(rnd, c) else 4):
                    cs = slice(k * P, (k + 1) * P)
                    mx(fbanks[(rnd, c)][:, k, :], w2c[:, c, cs], w2s[:, c, cs], oc[:], os_[:])
                q_ps = psum.tile([P, NE], F32, name="q_ps", tag="n")
                mx(q_ps[:], oc[:], os_[:], w2c[:, c, :], w2s[:, c, :])
                nbanks[c] = q_ps

        def scale2(rnd, c):
            if direct(rnd, c):
                w = state2[softmax_no(rnd - 1, c)][3][:, c:c + 1]
                wblk = second.tile([P, P], F32, name="wblk", tag="wblk", bufs=6)
                y2s[(rnd, c)] = wblk
                nc.scalar.activation(out=wblk[:], in_=blk_ones[:], func=ACT.Copy, scale=w)
            elif rnd:
                y = second.tile([P, NE], F32, name="y2", tag="y2", bufs=5)
                y2s[(rnd, c)] = y
                w = state2[softmax_no(rnd - 1, c)][3][:, c:c + 1]
                if c % 2 and c >= HALF:
                    nc.gpsimd.tensor_scalar(out=y[:], in0=priors2[:, c, :], scalar1=w, scalar2=0.0, op0=ALU.mult, op1=ALU.add)
                else:
                    nc.scalar.activation(out=y[:], in_=priors2[:, c, :], func=ACT.Copy, scale=w)

        def turn2(rnd, c):
            if rnd == 0:
                nc.scalar.copy(out=priors2[:, c, :], in_=nbanks[c][:])
            elif not direct(rnd, c):
                tr_ps = psum.tile([P, 4, P], F32, name="tr_ps", tag="f", bufs=3)
                fbanks[(rnd, c)] = tr_ps
                for k in range(4):
                    nc.tensor.transpose(tr_ps[:, k, :], y2s[(rnd, c)][:, k * P:(k + 1) * P], ident_f[:])

        def sums2(rnd, c):
            if direct(rnd, c):
                return
            if rnd < 2:
                scol = second.tile([P, 4, NA], F32, name="scol2", tag="scol2", bufs=3)
                scol2s[(rnd, c)] = scol
                dst = scol[:]
            else:
                dst = s2[:, c]
            nc.vector.tensor_reduce(out=dst, in_=fbanks[(rnd, c)][:].rearrange("p k (a h) -> p k a h", a=NA), axis=AX.X, op=ALU.add)

        def repeat2(rnd, c):
            if rnd < 2 and not direct(rnd, c):
                bc = second.tile([P, 4, NA, 32], F32, name="bc2", tag="bc2", bufs=3)
                bc2s[(rnd, c)] = bc
                nc.scalar.copy(out=bc[:], in_=scol2s[(rnd, c)][:].unsqueeze(3).to_broadcast([P, 4, NA, 32]))

        def spread2(rnd, c):
            if rnd < 2:
                sb_ps = psum.tile([P, NE], F32, name="sb_ps2", tag="sb")
                sb2s[(rnd, c)] = sb_ps
                if direct(rnd, c):
                    nc.tensor.matmul(sb_ps[:], lhsT=(y2s[(rnd, c)] if rnd else blk_ones)[:], rhs=priors2[:, c, :], start=True, stop=True)
                for k in range(0 if direct(rnd, c) else 4):
                    nc.tensor.transpose(sb_ps[:, k * P:(k + 1) * P], bc2s[(rnd, c)][:, k].rearrange("p a h -> p (a h)"), ident_f[:])

        def agree2(rnd, c):
            if rnd < 2:
                waste = second.tile([P, NE], BF16, name="waste2", tag="waste2")
                nc.vector.scalar_tensor_tensor(out=waste[:], in0=priors2[:, c, :], scalar=1.0, in1=sb2s[(rnd, c)][:], op0=ALU.mult, op1=ALU.mult,
                                               accum_out=us2[softmax_no(rnd, c)][:, c:c + 1])

        tiny = {}

        def softmax2_step(m, k):
            lt_old, e_old, z_old = state2[m - 1][0], state2[m - 1][1], state2[m - 1][2]
            if k == 0:
                ut = second.tile([P, 32], F32, name="utb", tag="utb", align_bytes=64)
                tiny["ut"] = ut
                nc.vector.transpose(ut[:], us2[m][:])
                n = second.tile([P, 1], F32, name="nb", tag="nb")
                tiny["n"] = n
                eu = second.tile([P, 32], F32, name="eub", tag="eub")
                nc.vector.scalar_tensor_tensor(out=eu[:], in0=ut[:], scalar=1.0, in1=e_old[:], op0=ALU.mult, op1=ALU.mult, accum_out=n[:])
            elif k == 1:
                if m in (1, 2):
                    tiny["f"] = factor(second, tiny["n"], z_old)
                    return
                rt = second.tile([P, 1], F32, name="rt", tag="rt")
                nc.gpsimd.tensor_tensor(out=rt[:], in0=tiny["n"][:], in1=half[:], op=ALU.pow)
                den = second.tile([P, 1], F32, name="den", tag="den")
                nc.vector.tensor_scalar(out=den[:], in0=z_old[:], scalar1=z_old[:, 0:1], scalar2=tiny["n"][:, 0:1], op0=ALU.mult, op1=ALU.add)
                rden = second.tile([P, 1], F32, name="rden", tag="rden")
                nc.vector.reciprocal(out=rden[:], in_=den[:])
                tiny["rt"], tiny["rden"] = rt, rden
            elif k == 3:
                if m not in (1, 2):
                    f = second.tile([P, 1], F32, name="f", tag="f")
                    nc.vector.tensor_tensor(out=f[:], in0=tiny["rt"][:], in1=tiny["rden"][:], op=ALU.mult)
                    tiny["f"] = f
                lt = second.tile([P, 32], F32, name="ltb", tag="ltb")
                tiny["lt"] = lt
                nc.vector.scalar_tensor_tensor(out=lt[:], in0=tiny["ut"][:], scalar=tiny["f"][:, 0:1], in1=lt_old[:], op0=ALU.mult, op1=ALU.add)
            elif k == 4:
                lt = tiny["lt"]
                negmax = second.tile([P, 1], F32, name="negmaxb", tag="negmaxb")
                nc.vector.tensor_reduce(out=negmax[:], in_=lt[:], axis=AX.X, op=ALU.max, negate=True)
                e = second.tile([P, 32], F32, name="eb", tag="eb", align_bytes=64)
                z = second.tile([P, 1], F32, name="zb", tag="zb")
                nc.scalar.activation(out=e[:], in_=lt[:], func=ACT.Exp, bias=negmax[:, 0:1], scale=1.0, accum_out=z[:])
                tiny["new"] = (lt, e, z)
            elif k == 5:
                et = second.tile([P, 32], F32, name="etb", tag="etb", bufs=3, align_bytes=64)
                nc.vector.transpose(et[:], tiny["new"][1][:])
                state2[m] = tiny["new"] + (et,)

        def squares2(half_no, part):
            of_half = slice(half_no * HALF, (half_no + 1) * HALF)
            if part == 0:
                sq = second.tile([P, HALF, 4, NA], F32, name="sqb", tag="sqb")
                tiny["sq"] = sq
                nc.scalar.activation(out=sq[:], in_=s2[:, of_half], func=ACT.Square)
            else:
                nc.vector.tensor_reduce(out=sqc[:].rearrange("p (a c) -> p a c", a=NA)[:, :, of_half],
                                        in_=tiny["sq"][:].rearrange("p c k a -> p a c k"), axis=AX.X, op=ALU.add)

        def finish():
            out_rows = out.rearrange("c a (k f) -> (c a k) f", f=P)
            z = state2[4][2]
            zz = second.tile([P, 1], F32, name="zz2", bufs=1)
            nc.vector.tensor_tensor(out=zz[:], in0=z[:], in1=z[:], op=ALU.mult)
            squares2(1, 0)
            squares2(1, 1)
            n_ps = psum.tile([P, 2], F32, name="n2_ps", tag="t", bufs=1)
            nc.tensor.matmul(n_ps[:], lhsT=sqc[:], rhs=ones_f[:], start=True, stop=True)
            f = late_factor(second, n_ps, zz)
            fb_ps = psum.tile([P, P], F32, name="fb2_ps", tag="t", bufs=1)
            nc.tensor.transpose(fb_ps[:], f[:, 0:1].to_broadcast([P, P]), ident_f[:])
            for half_no in range(2):
                of_half = slice(half_no * HALF, (half_no + 1) * HALF)
                o = second.tile([P, HALF, NA, 4], F32, name="o", tag="o")
                own = fb_ps[:].rearrange("p (a c) -> p c a", a=NA)[:, of_half, :]
                nc.vector.tensor_tensor(out=o[:], in0=s2[:, of_half].rearrange("p c k a -> p c a k"), in1=own.unsqueeze(3).to_broadcast([P, HALF, NA, 4]), op=ALU.mult)
                ot_ps = psum.tile([P, P], F32, name="ot_ps", tag="n")
                nc.tensor.transpose(ot_ps[:], o[:].rearrange("p c a k -> p (c a k)"), ident_f[:])
                res = second.tile([P, P], F32, name="res", tag="res")
                nc.scalar.copy(out=res[:], in_=ot_ps[:])
                nc.sync.dma_start(out=out_rows[half_no * P:(half_no + 1) * P, :], in_=res[:])

        LAGS = {open2: (0,), turn2: (1, 0, 1), sums2: (2, 2, 2), repeat2: (3, 3, 3), spread2: (4, 1, 4), agree2: (5, 2, 5), scale2: (0, 0, 0)}
        with tc.manual_schedule():
            for tick in range(3 * NC2 + 2):
                def run(fn):
                    for rnd, lag in enumerate(LAGS[fn]):
                        c = tick - lag - NC2 * rnd
                        if 0 <= c < NC2:
                            fn(rnd, c)

                def softmax2(k, delay):
                    for m in range(1, 5):
                        if tick - delay == HALF * m + (5 if m < 3 else 2):
                            softmax2_step(m, k)

                softmax2(0, 0)
                softmax2(3, 2)

                run(sums2)
                softmax2(4, 2)
                run(agree2)
                softmax2(5, 3)
                softmax2(1, 0)
                run(repeat2)
                run(spread2)
                run(turn2)
                run(open2)
                run(scale2)
                for part in range(2):
                    if tick == 2 * NC2 + HALF + 2 + part:
                        squares2(0, part)
            finish()
